import numpy as np
import ml_dtypes


def mxq(x, axis, fmt="e4m3"):
    dtype, down = {"e4m3": (ml_dtypes.float8_e4m3fn, 7), "e5m2": (ml_dtypes.float8_e5m2, 14)}[fmt]
    v = np.moveaxis(np.asarray(x, np.float32).astype(ml_dtypes.bfloat16).astype(np.float64), axis, -1)
    blocks = v.reshape(v.shape[:-1] + (-1, 32))
    amax = np.abs(blocks).max(-1, keepdims=True)
    byte = np.maximum(np.where(amax > 0, np.frexp(amax)[1] - 1 + 127, 0) - down, 1)
    scale = np.exp2(byte - 127.0)
    codes = (blocks / scale).astype(np.float32).astype(dtype).astype(np.float64)
    return np.moveaxis((codes * scale).reshape(v.shape), -1, axis)


WIDE = False


def mx_kscale(k):
    if not WIDE:
        return np.ones(k)
    levels = np.array([10, -10, 5, -5, 0])
    a = np.random.permutation(np.resize(levels, k // 512 * 4)).reshape(k // 512, 4)
    idx = np.arange(k)
    return np.exp2(a[idx // 512, idx % 128 // 32])


BF16 = ml_dtypes.bfloat16


def bf(x):
    return np.asarray(x, np.float32).astype(BF16)


def f64(x):
    return np.asarray(x).astype(np.float64)


E2M1 = np.array([0.0, 0.5, 1.0, 1.5, 2.0, 3.0, 4.0, 6.0, -0.0, -0.5, -1.0, -1.5, -2.0, -3.0, -4.0, -6.0])


def pack_weight(w, fmt):
    k, n = w.shape
    w = f64(bf(w)).reshape(k // 32, 32, n)
    amax = np.abs(w).max(1)
    if fmt == "e4m3":
        byte = np.frexp(amax)[1] - 1 + 127 - 7
    else:
        mant, ex = np.frexp(amax / 6.0)
        byte = np.where(mant > 0.5, ex, ex - 1) + 127
    byte = np.clip(np.where(amax > 0, byte, 1), 1, 254)
    scaled = (w * np.exp2(127.0 - byte)[:, None, :]).reshape(k, n).astype(np.float32)
    by_word = np.ascontiguousarray(scaled.reshape(k // 512, 128, 4, n).transpose(0, 1, 3, 2))
    if fmt == "e4m3":
        words = by_word.astype(ml_dtypes.float8_e4m3fn).view(np.uint8)
    else:
        c = by_word.astype(ml_dtypes.float4_e2m1fn).view(np.uint8) & 0xF
        words = c[..., 0::2] | (c[..., 1::2] << 4)
    return np.ascontiguousarray(words), np.ascontiguousarray(byte.astype(np.uint8).reshape(k // 512, 16, n))


def unpack_weight(words, scales, fmt):
    g, p, n, _ = words.shape
    if fmt == "e4m3":
        vals = np.ascontiguousarray(words).view(ml_dtypes.float8_e4m3fn).astype(np.float64)
    else:
        nib = np.empty((g, p, n, 4), np.uint8)
        nib[..., 0::2] = words & 0xF
        nib[..., 1::2] = words >> 4
        vals = E2M1[nib]
    vals = vals * np.repeat(np.exp2(scales.astype(np.float64) - 127.0), 8, axis=1)[..., None]
    return vals.transpose(0, 1, 3, 2).reshape(g * 512, n)

def pack4(w):
    words, scales = pack_weight(w, "e2m1")
    return words.reshape(words.shape[0], 128, -1), scales


def unpack4(words, scales):
    return unpack_weight(words.reshape(words.shape[0], 128, -1, 2), scales, "e2m1")


B, V, H = 512, 128, 1024
G = 4 * H
EPS = 1e-5


def sigmoid(v):
    return 1.0 / (1.0 + np.exp(-v))


def layer_norm(v, w, b):
    mu = v.mean(-1, keepdims=True)
    var = ((v - mu) ** 2).mean(-1, keepdims=True)
    return (v - mu) / np.sqrt(var + EPS) * w + b


def setup_inputs():
    s = mx_kscale(H)
    x = bf(np.random.standard_normal((B, V)))
    h0 = bf(np.random.standard_normal((B, H)) * s)
    c0 = bf(np.random.standard_normal((B, H)))
    w_ih1 = bf(np.random.standard_normal((G, V)) / np.sqrt(V))
    w_hh1 = np.random.standard_normal((G, H)) / np.sqrt(H) / s
    w_hh1_words, w_hh1_scales = pack4(np.ascontiguousarray(w_hh1.T))
    return {"x": x,
            "h0": h0,
            "c0": c0,
            "w_ih1": w_ih1,
            "w_hh1_words": w_hh1_words,
            "w_hh1_scales": w_hh1_scales,
            "lni_w1": bf(1.0 + 0.1 * np.random.standard_normal(G)),
            "lni_b1": bf(0.1 * np.random.standard_normal(G)),
            "lnh_w1": bf(1.0 + 0.1 * np.random.standard_normal(G)),
            "lnh_b1": bf(0.1 * np.random.standard_normal(G)),
            "lnc_w1": bf(1.0 + 0.1 * np.random.standard_normal(H)),
            "lnc_b1": bf(0.1 * np.random.standard_normal(H))}


def reference(x, h0, c0, w_ih1, w_hh1_words, w_hh1_scales, lni_w1, lni_b1, lnh_w1, lnh_b1, lnc_w1, lnc_b1):
    a = f64(x) @ f64(w_ih1).T
    r = mxq(f64(h0), 1, "e4m3") @ unpack4(w_hh1_words, w_hh1_scales)
    gates = layer_norm(a, f64(lni_w1), f64(lni_b1)) + layer_norm(r, f64(lnh_w1), f64(lnh_b1))
    i, f, g, o = np.split(gates, 4, axis=1)
    cy = layer_norm(sigmoid(f) * f64(c0) + sigmoid(i) * np.tanh(g), f64(lnc_w1), f64(lnc_b1))
    hy = sigmoid(o) * np.tanh(cy)
    return hy, cy

@@ -1,0 +1,433 @@
+from contextlib import ExitStack
+
+import concourse.mybir as mybir
+from concourse.masks import make_identity
+
+F32 = mybir.dt.float32
+BF16 = mybir.dt.bfloat16
+I32 = mybir.dt.int32
+U32 = mybir.dt.uint32
+U8 = mybir.dt.uint8
+FP8X4 = mybir.dt.float8_e4m3fn_x4
+FP4X4 = mybir.dt.float4_e2m1fn_x4
+ALU = mybir.AluOpType
+ACT = mybir.ActivationFunctionType
+
+P = 128
+BATCH = 512
+IN = 128
+HID = 1024
+GATES = 4 * HID
+EPS = 1e-5
+ROW_TILES = BATCH // P
+BANK = 512
+BANKS = GATES // BANK
+BLOCKS = GATES // P
+PER_BANK = BANK // P
+K_PASS = 512
+PASSES = HID // K_PASS
+ONES = 2
+W_ROW = IN + 16
+
+FLOPS = 2 * BATCH * GATES * (HID + IN)
+
+
+def tile_multilstm_pa_kernel(
+    tc,
+    x,
+    h0,
+    c0,
+    w_ih1,
+    w_hh1_words,
+    w_hh1_scales,
+    lni_w1,
+    lni_b1,
+    lnh_w1,
+    lnh_b1,
+    lnc_w1,
+    lnc_b1,
+    out_0,
+    out_1,
+):
+    nc = tc.nc
+    with ExitStack() as stack:
+        keep = stack.enter_context(tc.tile_pool(name="keep", bufs=1))
+        stage = stack.enter_context(tc.tile_pool(name="stage", bufs=2))
+        a_pool = stack.enter_context(tc.tile_pool(name="a_pool", bufs=3))
+        gate_pool = stack.enter_context(tc.tile_pool(name="gate_pool", bufs=2))
+        cell_pool = stack.enter_context(tc.tile_pool(name="cell_pool", bufs=2))
+        stats = stack.enter_context(tc.tile_pool(name="stats", bufs=2))
+        psum = stack.enter_context(tc.psum_pool(name="psum", bufs=BANKS))
+
+        w_scales = keep.tile([P, PASSES, GATES], U8, align_bytes=64)
+        nc.vector.memset(w_scales[:].rearrange("p g n -> p (g n)").bitcast(I32), 0)
+
+        ident_bf = keep.tile([P, P], BF16)
+        make_identity(nc, ident_bf[:])
+        ident_f32 = keep.tile([P, P], F32)
+        make_identity(nc, ident_f32[:])
+        neg_half = keep.tile([P, ROW_TILES], F32)
+        nc.gpsimd.memset(neg_half[:], -0.5)
+
+        warm = keep.tile([P, 1], F32)
+        nc.gpsimd.memset(warm[:], 0.0)
+        nc.scalar.activation(out=warm[:], in_=warm[:], func=ACT.Sigmoid)
+
+        x_rows = keep.tile([P, ROW_TILES, IN], BF16)
+        nc.sync.dma_start(out=x_rows[:], in_=x.rearrange("(t p) v -> p t v", p=P))
+
+        w_rows = keep.tile([P, BLOCKS, W_ROW], BF16)
+        nc.vector.memset(w_rows[:, :, IN:W_ROW], 1.0)
+        w_blocks = w_ih1.rearrange("(j p) v -> p j v", p=P)
+        for first in range(0, BLOCKS, BLOCKS // 4):
+            some = slice(first, first + BLOCKS // 4)
+            nc.sync.dma_start(out=w_rows[:, some, 0:IN], in_=w_blocks[:, some, :])
+
+        h_rows = keep.tile([P, ROW_TILES, HID], BF16)
+        nc.sync.dma_start(out=h_rows[:], in_=h0.rearrange("(t p) k -> p t k", p=P))
+
+        for g in range(PASSES):
+            for b in range(2):
+                for r in range(4):
+                    nc.sync.dma_start(
+                        out=w_scales[32 * b + r : P : 64, g, :].bitcast(I32),
+                        in_=w_hh1_scales[g, 4 * b + r : 16 : 8, :].bitcast(I32),
+                    )
+
+        w_words = keep.tile([P, PASSES, 2 * GATES], U8, align_bytes=64)
+        for half in range(2):
+            some = slice(half * GATES, (half + 1) * GATES)
+            for g in range(PASSES):
+                nc.sync.dma_start(
+                    out=w_words[:, g, some].bitcast(I32),
+                    in_=w_hh1_words[g, :, some].bitcast(I32),
+                )
+
+        c_rows = keep.tile([P, ROW_TILES, HID], BF16)
+        nc.sync.dma_start(out=c_rows[:], in_=c0.rearrange("(t p) k -> p t k", p=P))
+
+        gate_vecs = keep.tile([P, P], BF16)
+        for i, vec in enumerate((lni_w1, lnh_w1, lni_b1, lnh_b1)):
+            nc.scalar.dma_start(
+                out=gate_vecs[BLOCKS * i : BLOCKS * (i + 1), :],
+                in_=vec.rearrange("(j p) -> j p", p=P),
+            )
+        cell_blocks = HID // P
+        cell_vecs = keep.tile([P, P], BF16)
+        nc.vector.memset(cell_vecs[:], 0.0)
+        for i, vec in enumerate((lnc_w1, lnc_b1)):
+            nc.scalar.dma_start(
+                out=cell_vecs[cell_blocks * i : cell_blocks * (i + 1), :],
+                in_=vec.rearrange("(j p) -> j p", p=P),
+            )
+
+        vec_ps = psum.tile([P, 2 * P], BF16, tag="bank")
+        nc.tensor.transpose(vec_ps[:, 0:P], gate_vecs[:], ident_bf[:])
+        nc.tensor.transpose(vec_ps[:, P : 2 * P], cell_vecs[:], ident_bf[:])
+        vec_cols = keep.tile([P, 2 * P], BF16)
+        nc.vector.tensor_copy(out=vec_cols[:], in_=vec_ps[:])
+        bias_cols = keep.tile([P, BLOCKS], F32)
+        nc.vector.tensor_tensor(
+            out=bias_cols[:],
+            in0=vec_cols[:, 2 * BLOCKS : 3 * BLOCKS],
+            in1=vec_cols[:, 3 * BLOCKS : 4 * BLOCKS],
+            op=ALU.add,
+        )
+
+        def spread(dst, columns, identity):
+            for first in range(0, columns.shape[1], PER_BANK):
+                spread_ps = psum.tile([P, BANK], columns.dtype, tag="bank")
+                for k in range(PER_BANK):
+                    nc.tensor.transpose(
+                        spread_ps[:, k * P : (k + 1) * P],
+                        columns[:, first + k : first + k + 1].to_broadcast([P, P]),
+                        identity,
+                    )
+                nc.scalar.copy(out=dst[:, first * P : (first + PER_BANK) * P], in_=spread_ps[:])
+
+        gain_a = keep.tile([P, GATES], BF16)
+        spread(gain_a, vec_cols[:, 0:BLOCKS], ident_bf[:])
+        bias = keep.tile([P, GATES], F32)
+        spread(bias, bias_cols[:], ident_f32[:])
+
+        xT_ps = psum.tile([P, BATCH], BF16, tag="bank")
+        for t in range(ROW_TILES):
+            nc.tensor.transpose(xT_ps[:, t * P : (t + 1) * P], x_rows[:, t, :], ident_bf[:])
+        xT = keep.tile([P, BATCH], BF16)
+        nc.vector.tensor_copy(out=xT[:], in_=xT_ps[:])
+        xT_f32 = keep.tile([P, BATCH], F32)
+        nc.vector.tensor_copy(out=xT_f32[:], in_=xT_ps[:])
+
+        wT = keep.tile([P, GATES], BF16)
+        for j in range(BANKS):
+            wT_ps = psum.tile([P, BANK], BF16, tag="bank")
+            for k in range(PER_BANK):
+                nc.tensor.transpose(
+                    wT_ps[:, k * P : (k + 1) * P], w_rows[:, PER_BANK * j + k, 0:IN], ident_bf[:]
+                )
+            nc.vector.tensor_copy(out=wT[:, j * BANK : (j + 1) * BANK], in_=wT_ps[:])
+
+        gram_ps = psum.tile([P, IN + ONES], F32, tag="bank")
+        for j in range(BLOCKS):
+            nc.tensor.matmul(
+                gram_ps[:],
+                lhsT=w_rows[:, j, 0:IN],
+                rhs=w_rows[:, j, 0 : IN + ONES],
+                start=(j == 0),
+                stop=(j == BLOCKS - 1),
+            )
+        gram = keep.tile([P, IN + ONES], F32)
+        nc.vector.tensor_copy(out=gram[:], in_=gram_ps[:])
+
+        a_negmean = keep.tile([P, ROW_TILES], F32)
+        a_sumsq = keep.tile([P, ROW_TILES], F32)
+        for t in range(ROW_TILES):
+            xm_ps = psum.tile([P, IN + ONES], F32, tag="bank")
+            nc.tensor.matmul(
+                xm_ps[:], lhsT=xT_f32[:, t * P : (t + 1) * P], rhs=gram[:], start=True, stop=True
+            )
+            products = stage.tile([P, IN], F32)
+            nc.vector.scalar_tensor_tensor(
+                out=products[:],
+                in0=xm_ps[:, 0:IN],
+                scalar=1.0,
+                in1=x_rows[:, t, :],
+                op0=ALU.mult,
+                op1=ALU.mult,
+                accum_out=a_sumsq[:, t : t + 1],
+            )
+            nc.vector.tensor_scalar(
+                out=a_negmean[:, t : t + 1],
+                in0=xm_ps[:, IN : IN + 1],
+                scalar1=-1.0 / GATES,
+                scalar2=None,
+                op0=ALU.mult,
+            )
+        a_meansq = keep.tile([P, ROW_TILES], F32)
+        nc.vector.tensor_tensor(out=a_meansq[:], in0=a_negmean[:], in1=a_negmean[:], op=ALU.mult)
+        a_var = keep.tile([P, ROW_TILES], F32)
+        nc.vector.scalar_tensor_tensor(
+            out=a_var[:],
+            in0=a_sumsq[:],
+            scalar=1.0 / GATES,
+            in1=a_meansq[:],
+            op0=ALU.mult,
+            op1=ALU.subtract,
+        )
+        nc.vector.tensor_scalar(
+            out=a_var[:], in0=a_var[:], scalar1=EPS, scalar2=None, op0=ALU.add
+        )
+        a_rstd = keep.tile([P, ROW_TILES], F32)
+        nc.gpsimd.tensor_tensor(out=a_rstd[:], in0=a_var[:], in1=neg_half[:], op=ALU.pow)
+
+        h_codes = keep.tile([P, ROW_TILES, PASSES * P], U32, align_bytes=64)
+        h_scales = keep.tile([P, ROW_TILES, PASSES * P], U8, align_bytes=64)
+        pass_words = K_PASS // 2
+
+        def h0_to_mxfp8(t):
+            h_words = h_rows[:, t, :].bitcast(F32)
+            hT_ps = psum.tile([P, PASSES, 2, P], F32, tag="bank")
+            for g in range(PASSES):
+                for u in range(2):
+                    nc.tensor.transpose(
+                        hT_ps[:, g, u, :],
+                        h_words[:, pass_words * g + u : pass_words * (g + 1) : 2],
+                        ident_f32[:],
+                    )
+            grouped = stage.tile([P, PASSES * P * 4], BF16, align_bytes=64)
+            nc.scalar.copy(
+                out=grouped[:].bitcast(F32).rearrange("p (g b u) -> p g b u", g=PASSES, u=2),
+                in_=hT_ps[:].rearrange("p g u b -> p g b u"),
+            )
+            nc.vector.quantize_mx(
+                out=h_codes[:, t, :].bitcast(FP8X4), scales=h_scales[:, t, :], in_=grouped[:]
+            )
+
+        gain_r = keep.tile([P, GATES], BF16)
+        gain_c = keep.tile([P, HID], BF16)
+        bias_c = keep.tile([P, HID], BF16)
+
+        def a_branch(t):
+            a_part = a_pool.tile([P, GATES], F32)
+            for j in range(BANKS):
+                cols = slice(j * BANK, (j + 1) * BANK)
+                a_ps = psum.tile([P, BANK], F32, tag="bank")
+                nc.tensor.matmul(
+                    a_ps[:], lhsT=xT[:, t * P : (t + 1) * P], rhs=wT[:, cols], start=True, stop=True
+                )
+                nc.vector.scalar_tensor_tensor(
+                    out=a_part[:, cols],
+                    in0=a_ps[:],
+                    scalar=a_negmean[:, t : t + 1],
+                    in1=gain_a[:, cols],
+                    op0=ALU.add,
+                    op1=ALU.mult,
+                )
+            for half in range(2):
+                cols = slice(half * GATES // 2, (half + 1) * GATES // 2)
+                nc.vector.scalar_tensor_tensor(
+                    out=a_part[:, cols],
+                    in0=a_part[:, cols],
+                    scalar=a_rstd[:, t : t + 1],
+                    in1=bias[:, cols],
+                    op0=ALU.mult,
+                    op1=ALU.add,
+                )
+            return a_part
+
+        def r_matmuls(t):
+            r_banks = []
+            for j in range(BANKS):
+                r_ps = psum.tile([P, BANK], F32, tag="bank")
+                for g in range(PASSES):
+                    nc.tensor.matmul_mx(
+                        out=r_ps[:],
+                        lhsT=h_codes[:, t, g * P : (g + 1) * P].bitcast(FP8X4),
+                        lhsT_scale=h_scales[:, t, g * P : (g + 1) * P],
+                        rhs=w_words[:, g, 2 * j * BANK : 2 * (j + 1) * BANK].bitcast(FP4X4),
+                        rhs_scale=w_scales[:, g, j * BANK : (j + 1) * BANK],
+                        start=(g == 0),
+                        stop=(g == PASSES - 1),
+                    )
+                r_banks.append(r_ps)
+            return r_banks
+
+        def r_stats(r_banks):
+            r_copy = gate_pool.tile([P, GATES], F32, bufs=1)
+            r_sums = stats.tile([P, BANKS], F32)
+            for j in range(BANKS):
+                nc.scalar.activation(
+                    out=r_copy[:, j * BANK : (j + 1) * BANK],
+                    in_=r_banks[j][:],
+                    func=ACT.Identity,
+                    accum_out=r_sums[:, j : j + 1],
+                )
+            r_scaled = stats.tile([P, BANKS], F32)
+            r_negmean = stats.tile([P, 1], F32)
+            nc.vector.tensor_scalar(
+                out=r_scaled[:],
+                in0=r_sums[:],
+                scalar1=-1.0 / GATES,
+                scalar2=0.0,
+                op0=ALU.mult,
+                op1=ALU.add,
+                accum_out=r_negmean[:],
+            )
+            r_squares = stats.tile([P, 2], F32)
+            for half in range(2):
+                cols = slice(half * GATES // 2, (half + 1) * GATES // 2)
+                nc.scalar.activation(
+                    out=r_copy[:, cols],
+                    in_=r_copy[:, cols],
+                    func=ACT.Square,
+                    bias=r_negmean[:],
+                    accum_out=r_squares[:, half : half + 1],
+                )
+            r_scaled2 = stats.tile([P, 2], F32)
+            r_var = stats.tile([P, 1], F32)
+            nc.vector.tensor_scalar(
+                out=r_scaled2[:],
+                in0=r_squares[:],
+                scalar1=1.0 / GATES,
+                scalar2=EPS,
+                op0=ALU.mult,
+                op1=ALU.add,
+                accum_out=r_var[:],
+            )
+            r_rstd = stats.tile([P, 1], F32)
+            nc.gpsimd.tensor_tensor(out=r_rstd[:], in0=r_var[:], in1=neg_half[:, 0:1], op=ALU.pow)
+            return r_negmean, r_rstd
+
+        def r_branch(r_banks, r_negmean, r_rstd, a_part):
+            gates = gate_pool.tile([P, GATES], F32)
+            for j in range(BANKS):
+                cols = slice(j * BANK, (j + 1) * BANK)
+                nc.vector.scalar_tensor_tensor(
+                    out=gates[:, cols],
+                    in0=r_banks[j][:],
+                    scalar=r_negmean[:],
+                    in1=gain_r[:, cols],
+                    op0=ALU.add,
+                    op1=ALU.mult,
+                )
+            for gate, func in enumerate((ACT.Sigmoid, ACT.Sigmoid, ACT.Tanh, ACT.Sigmoid)):
+                cols = slice(gate * HID, (gate + 1) * HID)
+                nc.vector.scalar_tensor_tensor(
+                    out=gates[:, cols],
+                    in0=gates[:, cols],
+                    scalar=r_rstd[:],
+                    in1=a_part[:, cols],
+                    op0=ALU.mult,
+                    op1=ALU.add,
+                )
+                nc.scalar.activation(out=gates[:, cols], in_=gates[:, cols], func=func)
+            return gates
+
+        def cell(t, gates):
+            rows = slice(t * P, (t + 1) * P)
+            gate_i = gates[:, 0:HID]
+            gate_f = gates[:, HID : 2 * HID]
+            gate_g = gates[:, 2 * HID : 3 * HID]
+            gate_o = gates[:, 3 * HID : 4 * HID]
+            nc.vector.tensor_tensor(out=gate_f, in0=gate_f, in1=c_rows[:, t, :], op=ALU.mult)
+            nc.vector.tensor_tensor(out=gate_i, in0=gate_i, in1=gate_g, op=ALU.mult)
+            cy = cell_pool.tile([P, HID], F32)
+            c_sum = stats.tile([P, 1], F32)
+            nc.vector.scalar_tensor_tensor(
+                out=cy[:],
+                in0=gate_f,
+                scalar=1.0,
+                in1=gate_i,
+                op0=ALU.mult,
+                op1=ALU.add,
+                accum_out=c_sum[:],
+            )
+            c_negmean = stats.tile([P, 1], F32)
+            nc.vector.tensor_scalar(
+                out=c_negmean[:], in0=c_sum[:], scalar1=-1.0 / HID, scalar2=None, op0=ALU.mult
+            )
+            squares = cell_pool.tile([P, HID], BF16)
+            c_sumsq = stats.tile([P, 1], F32)
+            nc.scalar.activation(
+                out=squares[:], in_=cy[:], func=ACT.Square, bias=c_negmean[:], accum_out=c_sumsq[:]
+            )
+            c_var = stats.tile([P, 1], F32)
+            nc.vector.tensor_scalar(
+                out=c_var[:],
+                in0=c_sumsq[:],
+                scalar1=1.0 / HID,
+                scalar2=EPS,
+                op0=ALU.mult,
+                op1=ALU.add,
+            )
+            c_rstd = stats.tile([P, 1], F32)
+            nc.gpsimd.tensor_tensor(out=c_rstd[:], in0=c_var[:], in1=neg_half[:, 0:1], op=ALU.pow)
+            nc.vector.scalar_tensor_tensor(
+                out=cy[:], in0=cy[:], scalar=c_negmean[:], in1=gain_c[:], op0=ALU.add, op1=ALU.mult
+            )
+            nc.vector.scalar_tensor_tensor(
+                out=cy[:], in0=cy[:], scalar=c_rstd[:], in1=bias_c[:], op0=ALU.mult, op1=ALU.add
+            )
+            nc.sync.dma_start(out=out_1[rows, :], in_=cy[:])
+            hy = cell_pool.tile([P, HID], F32)
+            nc.scalar.activation(out=hy[:], in_=cy[:], func=ACT.Tanh)
+            nc.vector.tensor_tensor(out=hy[:], in0=hy[:], in1=gate_o, op=ALU.mult)
+            nc.sync.dma_start(out=out_0[rows, :], in_=hy[:])
+
+        a_parts = [a_branch(0)]
+        for t in range(ROW_TILES):
+            h0_to_mxfp8(t)
+        spread(gain_r, vec_cols[:, BLOCKS : 2 * BLOCKS], ident_bf[:])
+        spread(gain_c, vec_cols[:, P : P + cell_blocks], ident_bf[:])
+        spread(bias_c, vec_cols[:, P + cell_blocks : P + 2 * cell_blocks], ident_bf[:])
+        a_parts.append(a_branch(1))
+        r_banks = r_matmuls(0)
+        r_negmean, r_rstd = r_stats(r_banks)
+        for t in range(ROW_TILES):
+            gates = r_branch(r_banks, r_negmean, r_rstd, a_parts[t])
+            if t + 2 < ROW_TILES:
+                a_parts.append(a_branch(t + 2))
+            if t + 1 < ROW_TILES:
+                r_banks = r_matmuls(t + 1)
+                r_negmean, r_rstd = r_stats(r_banks)
+            cell(t, gates)

@@ -56,8 +56,11 @@ def tile_multilstm_pa_kernel(
         a_pool = stack.enter_context(tc.tile_pool(name="a_pool", bufs=3))
         gate_pool = stack.enter_context(tc.tile_pool(name="gate_pool", bufs=2))
         cell_pool = stack.enter_context(tc.tile_pool(name="cell_pool", bufs=2))
-        stats = stack.enter_context(tc.tile_pool(name="stats", bufs=2))
+        stats = stack.enter_context(tc.tile_pool(name="stats", bufs=4))
         psum = stack.enter_context(tc.psum_pool(name="psum", bufs=BANKS))
+
+        cell_vecs = keep.tile([P, P], BF16)
+        nc.vector.memset(cell_vecs[:], 0.0)
 
         w_scales = keep.tile([P, PASSES, GATES], U8, align_bytes=64)
         nc.vector.memset(w_scales[:].rearrange("p g n -> p (g n)").bitcast(I32), 0)
@@ -113,8 +116,6 @@ def tile_multilstm_pa_kernel(
                 in_=vec.rearrange("(j p) -> j p", p=P),
             )
         cell_blocks = HID // P
-        cell_vecs = keep.tile([P, P], BF16)
-        nc.vector.memset(cell_vecs[:], 0.0)
         for i, vec in enumerate((lnc_w1, lnc_b1)):
             nc.scalar.dma_start(
                 out=cell_vecs[cell_blocks * i : cell_blocks * (i + 1), :],
@@ -147,8 +148,6 @@ def tile_multilstm_pa_kernel(
 
         gain_a = keep.tile([P, GATES], BF16)
         spread(gain_a, vec_cols[:, 0:BLOCKS], ident_bf[:])
-        bias = keep.tile([P, GATES], F32)
-        spread(bias, bias_cols[:], ident_f32[:])
 
         xT_ps = psum.tile([P, BATCH], BF16, tag="bank")
         for t in range(ROW_TILES):
@@ -157,15 +156,6 @@ def tile_multilstm_pa_kernel(
         nc.vector.tensor_copy(out=xT[:], in_=xT_ps[:])
         xT_f32 = keep.tile([P, BATCH], F32)
         nc.vector.tensor_copy(out=xT_f32[:], in_=xT_ps[:])
-
-        wT = keep.tile([P, GATES], BF16)
-        for j in range(BANKS):
-            wT_ps = psum.tile([P, BANK], BF16, tag="bank")
-            for k in range(PER_BANK):
-                nc.tensor.transpose(
-                    wT_ps[:, k * P : (k + 1) * P], w_rows[:, PER_BANK * j + k, 0:IN], ident_bf[:]
-                )
-            nc.vector.tensor_copy(out=wT[:, j * BANK : (j + 1) * BANK], in_=wT_ps[:])
 
         gram_ps = psum.tile([P, IN + ONES], F32, tag="bank")
         for j in range(BLOCKS):
@@ -219,6 +209,18 @@ def tile_multilstm_pa_kernel(
         )
         a_rstd = keep.tile([P, ROW_TILES], F32)
         nc.gpsimd.tensor_tensor(out=a_rstd[:], in0=a_var[:], in1=neg_half[:], op=ALU.pow)
+
+        wT = keep.tile([P, GATES], BF16)
+        for j in range(BANKS):
+            wT_ps = psum.tile([P, BANK], BF16, tag="bank")
+            for k in range(PER_BANK):
+                nc.tensor.transpose(
+                    wT_ps[:, k * P : (k + 1) * P], w_rows[:, PER_BANK * j + k, 0:IN], ident_bf[:]
+                )
+            nc.vector.tensor_copy(out=wT[:, j * BANK : (j + 1) * BANK], in_=wT_ps[:])
+
+        bias = keep.tile([P, GATES], F32)
+        spread(bias, bias_cols[:], ident_f32[:])
 
         h_codes = keep.tile([P, ROW_TILES, PASSES * P], U32, align_bytes=64)
         h_scales = keep.tile([P, ROW_TILES, PASSES * P], U8, align_bytes=64)
@@ -292,6 +294,20 @@ def tile_multilstm_pa_kernel(
                 r_banks.append(r_ps)
             return r_banks
 
+        def rstd_of(sum_of_squares, count):
+            var = stats.tile([P, 1], F32)
+            nc.gpsimd.tensor_scalar(
+                out=var[:],
+                in0=sum_of_squares,
+                scalar1=1.0 / count,
+                scalar2=EPS,
+                op0=ALU.mult,
+                op1=ALU.add,
+            )
+            rstd = stats.tile([P, 1], F32)
+            nc.gpsimd.tensor_tensor(out=rstd[:], in0=var[:], in1=neg_half[:, 0:1], op=ALU.pow)
+            return rstd
+
         def r_stats(r_banks):
             r_copy = gate_pool.tile([P, GATES], F32, bufs=1)
             r_sums = stats.tile([P, BANKS], F32)
@@ -304,39 +320,22 @@ def tile_multilstm_pa_kernel(
                 )
             r_scaled = stats.tile([P, BANKS], F32)
             r_negmean = stats.tile([P, 1], F32)
-            nc.vector.tensor_scalar(
+            nc.scalar.activation(
                 out=r_scaled[:],
-                in0=r_sums[:],
-                scalar1=-1.0 / GATES,
-                scalar2=0.0,
-                op0=ALU.mult,
-                op1=ALU.add,
+                in_=r_sums[:],
+                func=ACT.Identity,
+                scale=-1.0 / GATES,
                 accum_out=r_negmean[:],
             )
-            r_squares = stats.tile([P, 2], F32)
-            for half in range(2):
-                cols = slice(half * GATES // 2, (half + 1) * GATES // 2)
-                nc.scalar.activation(
-                    out=r_copy[:, cols],
-                    in_=r_copy[:, cols],
-                    func=ACT.Square,
-                    bias=r_negmean[:],
-                    accum_out=r_squares[:, half : half + 1],
-                )
-            r_scaled2 = stats.tile([P, 2], F32)
-            r_var = stats.tile([P, 1], F32)
-            nc.vector.tensor_scalar(
-                out=r_scaled2[:],
-                in0=r_squares[:],
-                scalar1=1.0 / GATES,
-                scalar2=EPS,
-                op0=ALU.mult,
-                op1=ALU.add,
-                accum_out=r_var[:],
+            r_sumsq = stats.tile([P, 1], F32)
+            nc.scalar.activation(
+                out=r_copy[:],
+                in_=r_copy[:],
+                func=ACT.Square,
+                bias=r_negmean[:],
+                accum_out=r_sumsq[:],
             )
-            r_rstd = stats.tile([P, 1], F32)
-            nc.gpsimd.tensor_tensor(out=r_rstd[:], in0=r_var[:], in1=neg_half[:, 0:1], op=ALU.pow)
-            return r_negmean, r_rstd
+            return r_negmean, rstd_of(r_sumsq[:], GATES)
 
         def r_branch(r_banks, r_negmean, r_rstd, a_part):
             gates = gate_pool.tile([P, GATES], F32)
@@ -383,25 +382,13 @@ def tile_multilstm_pa_kernel(
                 accum_out=c_sum[:],
             )
             c_negmean = stats.tile([P, 1], F32)
-            nc.vector.tensor_scalar(
-                out=c_negmean[:], in0=c_sum[:], scalar1=-1.0 / HID, scalar2=None, op0=ALU.mult
-            )
+            nc.scalar.mul(out=c_negmean[:], in_=c_sum[:], mul=-1.0 / HID)
             squares = cell_pool.tile([P, HID], BF16)
             c_sumsq = stats.tile([P, 1], F32)
             nc.scalar.activation(
                 out=squares[:], in_=cy[:], func=ACT.Square, bias=c_negmean[:], accum_out=c_sumsq[:]
             )
-            c_var = stats.tile([P, 1], F32)
-            nc.vector.tensor_scalar(
-                out=c_var[:],
-                in0=c_sumsq[:],
-                scalar1=1.0 / HID,
-                scalar2=EPS,
-                op0=ALU.mult,
-                op1=ALU.add,
-            )
-            c_rstd = stats.tile([P, 1], F32)
-            nc.gpsimd.tensor_tensor(out=c_rstd[:], in0=c_var[:], in1=neg_half[:, 0:1], op=ALU.pow)
+            c_rstd = rstd_of(c_sumsq[:], HID)
             nc.vector.scalar_tensor_tensor(
                 out=cy[:], in0=cy[:], scalar=c_negmean[:], in1=gain_c[:], op0=ALU.add, op1=ALU.mult
             )

@@ -59,9 +59,6 @@ def tile_multilstm_pa_kernel(
         stats = stack.enter_context(tc.tile_pool(name="stats", bufs=4))
         psum = stack.enter_context(tc.psum_pool(name="psum", bufs=BANKS))
 
-        cell_vecs = keep.tile([P, P], BF16)
-        nc.vector.memset(cell_vecs[:], 0.0)
-
         w_scales = keep.tile([P, PASSES, GATES], U8, align_bytes=64)
         nc.vector.memset(w_scales[:].rearrange("p g n -> p (g n)").bitcast(I32), 0)
 
@@ -72,8 +69,15 @@ def tile_multilstm_pa_kernel(
         neg_half = keep.tile([P, ROW_TILES], F32)
         nc.gpsimd.memset(neg_half[:], -0.5)
 
+        gate_vecs = keep.tile([P, P], BF16)
+        for i, vec in enumerate((lni_w1, lnh_w1, lni_b1, lnh_b1)):
+            nc.scalar.dma_start(
+                out=gate_vecs[BLOCKS * i : BLOCKS * (i + 1), :],
+                in_=vec.rearrange("(j p) -> j p", p=P),
+            )
+
         warm = keep.tile([P, 1], F32)
-        nc.gpsimd.memset(warm[:], 0.0)
+        nc.vector.memset(warm[:], 0.0)
         nc.scalar.activation(out=warm[:], in_=warm[:], func=ACT.Sigmoid)
 
         x_rows = keep.tile([P, ROW_TILES, IN], BF16)
@@ -109,23 +113,14 @@ def tile_multilstm_pa_kernel(
         c_rows = keep.tile([P, ROW_TILES, HID], BF16)
         nc.sync.dma_start(out=c_rows[:], in_=c0.rearrange("(t p) k -> p t k", p=P))
 
-        gate_vecs = keep.tile([P, P], BF16)
-        for i, vec in enumerate((lni_w1, lnh_w1, lni_b1, lnh_b1)):
-            nc.scalar.dma_start(
-                out=gate_vecs[BLOCKS * i : BLOCKS * (i + 1), :],
-                in_=vec.rearrange("(j p) -> j p", p=P),
-            )
-        cell_blocks = HID // P
-        for i, vec in enumerate((lnc_w1, lnc_b1)):
-            nc.scalar.dma_start(
-                out=cell_vecs[cell_blocks * i : cell_blocks * (i + 1), :],
-                in_=vec.rearrange("(j p) -> j p", p=P),
-            )
+        gain_c = keep.tile([P, HID], BF16)
+        nc.sync.dma_start(out=gain_c[:], in_=lnc_w1.partition_broadcast(P))
+        bias_c = keep.tile([P, HID], BF16)
+        nc.sync.dma_start(out=bias_c[:], in_=lnc_b1.partition_broadcast(P))
 
-        vec_ps = psum.tile([P, 2 * P], BF16, tag="bank")
-        nc.tensor.transpose(vec_ps[:, 0:P], gate_vecs[:], ident_bf[:])
-        nc.tensor.transpose(vec_ps[:, P : 2 * P], cell_vecs[:], ident_bf[:])
-        vec_cols = keep.tile([P, 2 * P], BF16)
+        vec_ps = psum.tile([P, P], BF16, tag="bank")
+        nc.tensor.transpose(vec_ps[:], gate_vecs[:], ident_bf[:])
+        vec_cols = keep.tile([P, P], BF16)
         nc.vector.tensor_copy(out=vec_cols[:], in_=vec_ps[:])
         bias_cols = keep.tile([P, BLOCKS], F32)
         nc.vector.tensor_tensor(
@@ -146,9 +141,6 @@ def tile_multilstm_pa_kernel(
                     )
                 nc.scalar.copy(out=dst[:, first * P : (first + PER_BANK) * P], in_=spread_ps[:])
 
-        gain_a = keep.tile([P, GATES], BF16)
-        spread(gain_a, vec_cols[:, 0:BLOCKS], ident_bf[:])
-
         xT_ps = psum.tile([P, BATCH], BF16, tag="bank")
         for t in range(ROW_TILES):
             nc.tensor.transpose(xT_ps[:, t * P : (t + 1) * P], x_rows[:, t, :], ident_bf[:])
@@ -158,14 +150,23 @@ def tile_multilstm_pa_kernel(
         nc.vector.tensor_copy(out=xT_f32[:], in_=xT_ps[:])
 
         gram_ps = psum.tile([P, IN + ONES], F32, tag="bank")
-        for j in range(BLOCKS):
-            nc.tensor.matmul(
-                gram_ps[:],
-                lhsT=w_rows[:, j, 0:IN],
-                rhs=w_rows[:, j, 0 : IN + ONES],
-                start=(j == 0),
-                stop=(j == BLOCKS - 1),
-            )
+        wT = keep.tile([P, GATES], BF16)
+        for first in range(0, BLOCKS, BLOCKS // 4):
+            for j in range(first, first + BLOCKS // 4):
+                nc.tensor.matmul(
+                    gram_ps[:],
+                    lhsT=w_rows[:, j, 0:IN],
+                    rhs=w_rows[:, j, 0 : IN + ONES],
+                    start=(j == 0),
+                    stop=(j == BLOCKS - 1),
+                )
+            for j in range(first, first + BLOCKS // 4, PER_BANK):
+                wT_ps = psum.tile([P, BANK], BF16, tag="bank")
+                for k in range(PER_BANK):
+                    nc.tensor.transpose(
+                        wT_ps[:, k * P : (k + 1) * P], w_rows[:, j + k, 0:IN], ident_bf[:]
+                    )
+                nc.vector.tensor_copy(out=wT[:, j * P : (j + PER_BANK) * P], in_=wT_ps[:])
         gram = keep.tile([P, IN + ONES], F32)
         nc.vector.tensor_copy(out=gram[:], in_=gram_ps[:])
 
@@ -210,18 +211,6 @@ def tile_multilstm_pa_kernel(
         a_rstd = keep.tile([P, ROW_TILES], F32)
         nc.gpsimd.tensor_tensor(out=a_rstd[:], in0=a_var[:], in1=neg_half[:], op=ALU.pow)
 
-        wT = keep.tile([P, GATES], BF16)
-        for j in range(BANKS):
-            wT_ps = psum.tile([P, BANK], BF16, tag="bank")
-            for k in range(PER_BANK):
-                nc.tensor.transpose(
-                    wT_ps[:, k * P : (k + 1) * P], w_rows[:, PER_BANK * j + k, 0:IN], ident_bf[:]
-                )
-            nc.vector.tensor_copy(out=wT[:, j * BANK : (j + 1) * BANK], in_=wT_ps[:])
-
-        bias = keep.tile([P, GATES], F32)
-        spread(bias, bias_cols[:], ident_f32[:])
-
         h_codes = keep.tile([P, ROW_TILES, PASSES * P], U32, align_bytes=64)
         h_scales = keep.tile([P, ROW_TILES, PASSES * P], U8, align_bytes=64)
         pass_words = K_PASS // 2
@@ -245,11 +234,11 @@ def tile_multilstm_pa_kernel(
                 out=h_codes[:, t, :].bitcast(FP8X4), scales=h_scales[:, t, :], in_=grouped[:]
             )
 
+        gain_a = keep.tile([P, GATES], BF16)
         gain_r = keep.tile([P, GATES], BF16)
-        gain_c = keep.tile([P, HID], BF16)
-        bias_c = keep.tile([P, HID], BF16)
+        bias = keep.tile([P, GATES], F32)
 
-        def a_branch(t):
+        def a_gain(t):
             a_part = a_pool.tile([P, GATES], F32)
             for j in range(BANKS):
                 cols = slice(j * BANK, (j + 1) * BANK)
@@ -265,6 +254,9 @@ def tile_multilstm_pa_kernel(
                     op0=ALU.add,
                     op1=ALU.mult,
                 )
+            return a_part
+
+        def a_bias(t, a_part):
             for half in range(2):
                 cols = slice(half * GATES // 2, (half + 1) * GATES // 2)
                 nc.vector.scalar_tensor_tensor(
@@ -275,7 +267,6 @@ def tile_multilstm_pa_kernel(
                     op0=ALU.mult,
                     op1=ALU.add,
                 )
-            return a_part
 
         def r_matmuls(t):
             r_banks = []
@@ -337,7 +328,7 @@ def tile_multilstm_pa_kernel(
             )
             return r_negmean, rstd_of(r_sumsq[:], GATES)
 
-        def r_branch(r_banks, r_negmean, r_rstd, a_part):
+        def r_gain(r_banks, r_negmean):
             gates = gate_pool.tile([P, GATES], F32)
             for j in range(BANKS):
                 cols = slice(j * BANK, (j + 1) * BANK)
@@ -349,27 +340,28 @@ def tile_multilstm_pa_kernel(
                     op0=ALU.add,
                     op1=ALU.mult,
                 )
-            for gate, func in enumerate((ACT.Sigmoid, ACT.Sigmoid, ACT.Tanh, ACT.Sigmoid)):
-                cols = slice(gate * HID, (gate + 1) * HID)
-                nc.vector.scalar_tensor_tensor(
-                    out=gates[:, cols],
-                    in0=gates[:, cols],
-                    scalar=r_rstd[:],
-                    in1=a_part[:, cols],
-                    op0=ALU.mult,
-                    op1=ALU.add,
-                )
-                nc.scalar.activation(out=gates[:, cols], in_=gates[:, cols], func=func)
             return gates
 
-        def cell(t, gates):
+        def finish_gate(gates, gate, func, r_rstd, a_part):
+            cols = slice(gate * HID, (gate + 1) * HID)
+            nc.vector.scalar_tensor_tensor(
+                out=gates[:, cols],
+                in0=gates[:, cols],
+                scalar=r_rstd[:],
+                in1=a_part[:, cols],
+                op0=ALU.mult,
+                op1=ALU.add,
+            )
+            nc.scalar.activation(out=gates[:, cols], in_=gates[:, cols], func=func)
+
+        def cell(t, gates, r_rstd, a_part):
             rows = slice(t * P, (t + 1) * P)
             gate_i = gates[:, 0:HID]
             gate_f = gates[:, HID : 2 * HID]
             gate_g = gates[:, 2 * HID : 3 * HID]
             gate_o = gates[:, 3 * HID : 4 * HID]
-            nc.vector.tensor_tensor(out=gate_f, in0=gate_f, in1=c_rows[:, t, :], op=ALU.mult)
-            nc.vector.tensor_tensor(out=gate_i, in0=gate_i, in1=gate_g, op=ALU.mult)
+            nc.gpsimd.tensor_tensor(out=gate_f, in0=gate_f, in1=c_rows[:, t, :], op=ALU.mult)
+            nc.gpsimd.tensor_tensor(out=gate_i, in0=gate_i, in1=gate_g, op=ALU.mult)
             cy = cell_pool.tile([P, HID], F32)
             c_sum = stats.tile([P, 1], F32)
             nc.vector.scalar_tensor_tensor(
@@ -381,6 +373,7 @@ def tile_multilstm_pa_kernel(
                 op1=ALU.add,
                 accum_out=c_sum[:],
             )
+            finish_gate(gates, 3, ACT.Sigmoid, r_rstd, a_part)
             c_negmean = stats.tile([P, 1], F32)
             nc.scalar.mul(out=c_negmean[:], in_=c_sum[:], mul=-1.0 / HID)
             squares = cell_pool.tile([P, HID], BF16)
@@ -401,20 +394,27 @@ def tile_multilstm_pa_kernel(
             nc.vector.tensor_tensor(out=hy[:], in0=hy[:], in1=gate_o, op=ALU.mult)
             nc.sync.dma_start(out=out_0[rows, :], in_=hy[:])
 
-        a_parts = [a_branch(0)]
+        spread(gain_a, vec_cols[:, 0:BLOCKS], ident_bf[:])
+        a_parts = [a_gain(0)]
+        spread(bias, bias_cols[:], ident_f32[:])
         for t in range(ROW_TILES):
             h0_to_mxfp8(t)
         spread(gain_r, vec_cols[:, BLOCKS : 2 * BLOCKS], ident_bf[:])
-        spread(gain_c, vec_cols[:, P : P + cell_blocks], ident_bf[:])
-        spread(bias_c, vec_cols[:, P + cell_blocks : P + 2 * cell_blocks], ident_bf[:])
-        a_parts.append(a_branch(1))
+        a_bias(0, a_parts[0])
+        a_parts.append(a_gain(1))
+        a_bias(1, a_parts[1])
+
         r_banks = r_matmuls(0)
         r_negmean, r_rstd = r_stats(r_banks)
         for t in range(ROW_TILES):
-            gates = r_branch(r_banks, r_negmean, r_rstd, a_parts[t])
+            gates = r_gain(r_banks, r_negmean)
+            for gate, func in enumerate((ACT.Sigmoid, ACT.Sigmoid, ACT.Tanh)):
+                finish_gate(gates, gate, func, r_rstd, a_parts[t])
+            this_rstd = r_rstd
             if t + 2 < ROW_TILES:
-                a_parts.append(a_branch(t + 2))
+                a_parts.append(a_gain(t + 2))
+                a_bias(t + 2, a_parts[t + 2])
             if t + 1 < ROW_TILES:
                 r_banks = r_matmuls(t + 1)
                 r_negmean, r_rstd = r_stats(r_banks)
-            cell(t, gates)
+            cell(t, gates, this_rstd, a_parts[t])

@@ -70,8 +70,9 @@ def tile_multilstm_pa_kernel(
         nc.gpsimd.memset(neg_half[:], -0.5)
 
         gate_vecs = keep.tile([P, P], BF16)
-        for i, vec in enumerate((lni_w1, lnh_w1, lni_b1, lnh_b1)):
-            nc.scalar.dma_start(
+        nc.vector.memset(gate_vecs[3 * BLOCKS : P, :], 0.0)
+        for i, vec in enumerate((lni_w1, lni_b1, lnh_b1)):
+            nc.sync.dma_start(
                 out=gate_vecs[BLOCKS * i : BLOCKS * (i + 1), :],
                 in_=vec.rearrange("(j p) -> j p", p=P),
             )
@@ -110,6 +111,9 @@ def tile_multilstm_pa_kernel(
                     in_=w_hh1_words[g, :, some].bitcast(I32),
                 )
 
+        gain_r = keep.tile([P, GATES], BF16)
+        nc.sync.dma_start(out=gain_r[:], in_=lnh_w1.partition_broadcast(P))
+
         c_rows = keep.tile([P, ROW_TILES, HID], BF16)
         nc.sync.dma_start(out=c_rows[:], in_=c0.rearrange("(t p) k -> p t k", p=P))
 
@@ -125,8 +129,8 @@ def tile_multilstm_pa_kernel(
         bias_cols = keep.tile([P, BLOCKS], F32)
         nc.vector.tensor_tensor(
             out=bias_cols[:],
-            in0=vec_cols[:, 2 * BLOCKS : 3 * BLOCKS],
-            in1=vec_cols[:, 3 * BLOCKS : 4 * BLOCKS],
+            in0=vec_cols[:, BLOCKS : 2 * BLOCKS],
+            in1=vec_cols[:, 2 * BLOCKS : 3 * BLOCKS],
             op=ALU.add,
         )
 
@@ -235,7 +239,6 @@ def tile_multilstm_pa_kernel(
             )
 
         gain_a = keep.tile([P, GATES], BF16)
-        gain_r = keep.tile([P, GATES], BF16)
         bias = keep.tile([P, GATES], F32)
 
         def a_gain(t):
@@ -395,13 +398,11 @@ def tile_multilstm_pa_kernel(
             nc.sync.dma_start(out=out_0[rows, :], in_=hy[:])
 
         spread(gain_a, vec_cols[:, 0:BLOCKS], ident_bf[:])
-        a_parts = [a_gain(0)]
+        a_parts = [a_gain(0), a_gain(1)]
         spread(bias, bias_cols[:], ident_f32[:])
         for t in range(ROW_TILES):
             h0_to_mxfp8(t)
-        spread(gain_r, vec_cols[:, BLOCKS : 2 * BLOCKS], ident_bf[:])
         a_bias(0, a_parts[0])
-        a_parts.append(a_gain(1))
         a_bias(1, a_parts[1])
 
         r_banks = r_matmuls(0)

@@ -363,8 +363,8 @@ def tile_multilstm_pa_kernel(
             gate_f = gates[:, HID : 2 * HID]
             gate_g = gates[:, 2 * HID : 3 * HID]
             gate_o = gates[:, 3 * HID : 4 * HID]
-            nc.gpsimd.tensor_tensor(out=gate_f, in0=gate_f, in1=c_rows[:, t, :], op=ALU.mult)
-            nc.gpsimd.tensor_tensor(out=gate_i, in0=gate_i, in1=gate_g, op=ALU.mult)
+            nc.vector.tensor_tensor(out=gate_f, in0=gate_f, in1=c_rows[:, t, :], op=ALU.mult)
+            nc.vector.tensor_tensor(out=gate_i, in0=gate_i, in1=gate_g, op=ALU.mult)
             cy = cell_pool.tile([P, HID], F32)
             c_sum = stats.tile([P, 1], F32)
             nc.vector.scalar_tensor_tensor(

@@ -28,6 +28,10 @@ K_PASS = 512
 PASSES = HID // K_PASS
 ONES = 2
 W_ROW = IN + 16
+QUARTER = BLOCKS // 4
+R_SLOTS = 3
+Q_SLOTS = 5
+POOL_PRODUCTS = False
 
 FLOPS = 2 * BATCH * GATES * (HID + IN)
 
@@ -51,17 +55,25 @@ def tile_multilstm_pa_kernel(
 ):
     nc = tc.nc
     with ExitStack() as stack:
+        stack.enter_context(tc.manual_schedule())
         keep = stack.enter_context(tc.tile_pool(name="keep", bufs=1))
         stage = stack.enter_context(tc.tile_pool(name="stage", bufs=2))
-        a_pool = stack.enter_context(tc.tile_pool(name="a_pool", bufs=3))
+        r_pool = stack.enter_context(tc.tile_pool(name="r_pool", bufs=2))
         gate_pool = stack.enter_context(tc.tile_pool(name="gate_pool", bufs=2))
         cell_pool = stack.enter_context(tc.tile_pool(name="cell_pool", bufs=2))
         stats = stack.enter_context(tc.tile_pool(name="stats", bufs=4))
-        psum = stack.enter_context(tc.psum_pool(name="psum", bufs=BANKS))
+        psum = stack.enter_context(tc.psum_pool(name="psum", bufs=1))
+
+        def r_bank_tile(shape, dtype):
+            r_slot = psum.tile(shape, dtype, tag="r", bufs=R_SLOTS)
+            return r_slot
+
+        def q_bank_tile(shape, dtype):
+            q_slot = psum.tile(shape, dtype, tag="q", bufs=Q_SLOTS)
+            return q_slot
 
         w_scales = keep.tile([P, PASSES, GATES], U8, align_bytes=64)
         nc.vector.memset(w_scales[:].rearrange("p g n -> p (g n)").bitcast(I32), 0)
-
         ident_bf = keep.tile([P, P], BF16)
         make_identity(nc, ident_bf[:])
         ident_f32 = keep.tile([P, P], F32)
@@ -76,24 +88,21 @@ def tile_multilstm_pa_kernel(
                 out=gate_vecs[BLOCKS * i : BLOCKS * (i + 1), :],
                 in_=vec.rearrange("(j p) -> j p", p=P),
             )
-
         warm = keep.tile([P, 1], F32)
         nc.vector.memset(warm[:], 0.0)
         nc.scalar.activation(out=warm[:], in_=warm[:], func=ACT.Sigmoid)
 
         x_rows = keep.tile([P, ROW_TILES, IN], BF16)
         nc.sync.dma_start(out=x_rows[:], in_=x.rearrange("(t p) v -> p t v", p=P))
-
         w_rows = keep.tile([P, BLOCKS, W_ROW], BF16)
         nc.vector.memset(w_rows[:, :, IN:W_ROW], 1.0)
         w_blocks = w_ih1.rearrange("(j p) v -> p j v", p=P)
-        for first in range(0, BLOCKS, BLOCKS // 4):
-            some = slice(first, first + BLOCKS // 4)
+        for first in range(0, BLOCKS, QUARTER):
+            some = slice(first, first + QUARTER)
             nc.sync.dma_start(out=w_rows[:, some, 0:IN], in_=w_blocks[:, some, :])
-
         h_rows = keep.tile([P, ROW_TILES, HID], BF16)
-        nc.sync.dma_start(out=h_rows[:], in_=h0.rearrange("(t p) k -> p t k", p=P))
-
+        h_tiles = h0.rearrange("(t p) k -> p t k", p=P)
+        nc.sync.dma_start(out=h_rows[:, 0:1, :], in_=h_tiles[:, 0:1, :])
         for g in range(PASSES):
             for b in range(2):
                 for r in range(4):
@@ -101,7 +110,6 @@ def tile_multilstm_pa_kernel(
                         out=w_scales[32 * b + r : P : 64, g, :].bitcast(I32),
                         in_=w_hh1_scales[g, 4 * b + r : 16 : 8, :].bitcast(I32),
                     )
-
         w_words = keep.tile([P, PASSES, 2 * GATES], U8, align_bytes=64)
         for half in range(2):
             some = slice(half * GATES, (half + 1) * GATES)
@@ -110,19 +118,18 @@ def tile_multilstm_pa_kernel(
                     out=w_words[:, g, some].bitcast(I32),
                     in_=w_hh1_words[g, :, some].bitcast(I32),
                 )
-
+        nc.sync.dma_start(out=h_rows[:, 1:2, :], in_=h_tiles[:, 1:2, :])
         gain_r = keep.tile([P, GATES], BF16)
         nc.sync.dma_start(out=gain_r[:], in_=lnh_w1.partition_broadcast(P))
-
+        nc.sync.dma_start(out=h_rows[:, 2:ROW_TILES, :], in_=h_tiles[:, 2:ROW_TILES, :])
         c_rows = keep.tile([P, ROW_TILES, HID], BF16)
         nc.sync.dma_start(out=c_rows[:], in_=c0.rearrange("(t p) k -> p t k", p=P))
-
         gain_c = keep.tile([P, HID], BF16)
         nc.sync.dma_start(out=gain_c[:], in_=lnc_w1.partition_broadcast(P))
         bias_c = keep.tile([P, HID], BF16)
         nc.sync.dma_start(out=bias_c[:], in_=lnc_b1.partition_broadcast(P))
 
-        vec_ps = psum.tile([P, P], BF16, tag="bank")
+        vec_ps = r_bank_tile([P, P], BF16)
         nc.tensor.transpose(vec_ps[:], gate_vecs[:], ident_bf[:])
         vec_cols = keep.tile([P, P], BF16)
         nc.vector.tensor_copy(out=vec_cols[:], in_=vec_ps[:])
@@ -133,30 +140,63 @@ def tile_multilstm_pa_kernel(
             in1=vec_cols[:, 2 * BLOCKS : 3 * BLOCKS],
             op=ALU.add,
         )
-
-        def spread(dst, columns, identity):
-            for first in range(0, columns.shape[1], PER_BANK):
-                spread_ps = psum.tile([P, BANK], columns.dtype, tag="bank")
-                for k in range(PER_BANK):
-                    nc.tensor.transpose(
-                        spread_ps[:, k * P : (k + 1) * P],
-                        columns[:, first + k : first + k + 1].to_broadcast([P, P]),
-                        identity,
-                    )
-                nc.scalar.copy(out=dst[:, first * P : (first + PER_BANK) * P], in_=spread_ps[:])
-
-        xT_ps = psum.tile([P, BATCH], BF16, tag="bank")
+        xT_ps = r_bank_tile([P, BATCH], BF16)
         for t in range(ROW_TILES):
             nc.tensor.transpose(xT_ps[:, t * P : (t + 1) * P], x_rows[:, t, :], ident_bf[:])
-        xT = keep.tile([P, BATCH], BF16)
-        nc.vector.tensor_copy(out=xT[:], in_=xT_ps[:])
         xT_f32 = keep.tile([P, BATCH], F32)
         nc.vector.tensor_copy(out=xT_f32[:], in_=xT_ps[:])
 
-        gram_ps = psum.tile([P, IN + ONES], F32, tag="bank")
-        wT = keep.tile([P, GATES], BF16)
-        for first in range(0, BLOCKS, BLOCKS // 4):
-            for j in range(first, first + BLOCKS // 4):
+        h_codes = keep.tile([P, ROW_TILES, PASSES * P], U32, align_bytes=64)
+        h_scales = keep.tile([P, ROW_TILES, PASSES * P], U8, align_bytes=64)
+        pass_words = K_PASS // 2
+
+        def h0_turn(t):
+            h_words = h_rows[:, t, :].bitcast(F32)
+            hT_ps = r_bank_tile([P, PASSES, 2, P], F32)
+            for g in range(PASSES):
+                for u in range(2):
+                    nc.tensor.transpose(
+                        hT_ps[:, g, u, :],
+                        h_words[:, pass_words * g + u : pass_words * (g + 1) : 2],
+                        ident_f32[:],
+                    )
+            return hT_ps
+
+        def h0_group(hT_ps, engine):
+            grouped = stage.tile([P, PASSES * P * 4], BF16, align_bytes=64)
+            if engine == "scalar":
+                nc.scalar.copy(
+                    out=grouped[:].bitcast(F32).rearrange("p (g b u) -> p g b u", g=PASSES, u=2),
+                    in_=hT_ps[:].rearrange("p g u b -> p g b u"),
+                )
+            else:
+                nc.vector.tensor_copy(
+                    out=grouped[:].bitcast(F32).rearrange("p (g b u) -> p g b u", g=PASSES, u=2),
+                    in_=hT_ps[:].rearrange("p g u b -> p g b u"),
+                )
+            return grouped
+
+        def h0_quantize(t, grouped):
+            nc.vector.quantize_mx(
+                out=h_codes[:, t, :].bitcast(FP8X4), scales=h_scales[:, t, :], in_=grouped[:]
+            )
+
+        gain_a = keep.tile([P, GATES], BF16)
+
+        def spread_gain(first):
+            spread_ps = r_bank_tile([P, BANK], BF16)
+            for k in range(PER_BANK):
+                nc.tensor.transpose(
+                    spread_ps[:, k * P : (k + 1) * P],
+                    vec_cols[:, first + k : first + k + 1].to_broadcast([P, P]),
+                    ident_bf[:],
+                )
+            nc.vector.tensor_copy(out=gain_a[:, first * P : (first + PER_BANK) * P], in_=spread_ps[:])
+
+        gram_ps = q_bank_tile([P, IN + ONES], F32)
+
+        def gram_quarter(first):
+            for j in range(first, first + QUARTER):
                 nc.tensor.matmul(
                     gram_ps[:],
                     lhsT=w_rows[:, j, 0:IN],
@@ -164,20 +204,52 @@ def tile_multilstm_pa_kernel(
                     start=(j == 0),
                     stop=(j == BLOCKS - 1),
                 )
-            for j in range(first, first + BLOCKS // 4, PER_BANK):
-                wT_ps = psum.tile([P, BANK], BF16, tag="bank")
-                for k in range(PER_BANK):
-                    nc.tensor.transpose(
-                        wT_ps[:, k * P : (k + 1) * P], w_rows[:, j + k, 0:IN], ident_bf[:]
-                    )
-                nc.vector.tensor_copy(out=wT[:, j * P : (j + PER_BANK) * P], in_=wT_ps[:])
+
+        for q in range(4):
+            if q == 3:
+                grouped_0 = h0_group(h0_turn(0), "scalar")
+            spread_gain(2 * q * PER_BANK)
+            spread_gain((2 * q + 1) * PER_BANK)
+            gram_quarter(q * QUARTER)
+
+        neg_wmean = keep.tile([P, 1], F32)
+        nc.vector.tensor_scalar(
+            out=neg_wmean[:],
+            in0=gram_ps[:, IN : IN + 1],
+            scalar1=-1.0 / GATES,
+            scalar2=None,
+            op0=ALU.mult,
+        )
         gram = keep.tile([P, IN + ONES], F32)
         nc.vector.tensor_copy(out=gram[:], in_=gram_ps[:])
+        h0_quantize(0, grouped_0)
+
+        wcT = keep.tile([P, GATES], F32)
+
+        def w_turn(q):
+            wT_ps = q_bank_tile([P, 2 * BANK], BF16)
+            for k in range(QUARTER):
+                nc.tensor.transpose(
+                    wT_ps[:, k * P : (k + 1) * P], w_rows[:, q * QUARTER + k, 0:IN], ident_bf[:]
+                )
+            return wT_ps
+
+        def w_centre(q, wT_ps):
+            cols = slice(q * 2 * BANK, (q + 1) * 2 * BANK)
+            nc.vector.scalar_tensor_tensor(
+                out=wcT[:, cols],
+                in0=wT_ps[:],
+                scalar=neg_wmean[:],
+                in1=gain_a[:, cols],
+                op0=ALU.add,
+                op1=ALU.mult,
+            )
 
         a_negmean = keep.tile([P, ROW_TILES], F32)
         a_sumsq = keep.tile([P, ROW_TILES], F32)
-        for t in range(ROW_TILES):
-            xm_ps = psum.tile([P, IN + ONES], F32, tag="bank")
+
+        def a_sums(t):
+            xm_ps = r_bank_tile([P, IN + ONES], F32)
             nc.tensor.matmul(
                 xm_ps[:], lhsT=xT_f32[:, t * P : (t + 1) * P], rhs=gram[:], start=True, stop=True
             )
@@ -198,6 +270,10 @@ def tile_multilstm_pa_kernel(
                 scalar2=None,
                 op0=ALU.mult,
             )
+
+        wT_tiles = [w_turn(0), w_turn(1)]
+        for t in range(ROW_TILES):
+            a_sums(t)
         a_meansq = keep.tile([P, ROW_TILES], F32)
         nc.vector.tensor_tensor(out=a_meansq[:], in0=a_negmean[:], in1=a_negmean[:], op=ALU.mult)
         a_var = keep.tile([P, ROW_TILES], F32)
@@ -214,79 +290,26 @@ def tile_multilstm_pa_kernel(
         )
         a_rstd = keep.tile([P, ROW_TILES], F32)
         nc.gpsimd.tensor_tensor(out=a_rstd[:], in0=a_var[:], in1=neg_half[:], op=ALU.pow)
-
-        h_codes = keep.tile([P, ROW_TILES, PASSES * P], U32, align_bytes=64)
-        h_scales = keep.tile([P, ROW_TILES, PASSES * P], U8, align_bytes=64)
-        pass_words = K_PASS // 2
-
-        def h0_to_mxfp8(t):
-            h_words = h_rows[:, t, :].bitcast(F32)
-            hT_ps = psum.tile([P, PASSES, 2, P], F32, tag="bank")
-            for g in range(PASSES):
-                for u in range(2):
-                    nc.tensor.transpose(
-                        hT_ps[:, g, u, :],
-                        h_words[:, pass_words * g + u : pass_words * (g + 1) : 2],
-                        ident_f32[:],
-                    )
-            grouped = stage.tile([P, PASSES * P * 4], BF16, align_bytes=64)
-            nc.scalar.copy(
-                out=grouped[:].bitcast(F32).rearrange("p (g b u) -> p g b u", g=PASSES, u=2),
-                in_=hT_ps[:].rearrange("p g u b -> p g b u"),
+        def a_bank(t, j):
+            a_ps = q_bank_tile([P, BANK], F32)
+            nc.tensor.matmul(
+                a_ps[:],
+                lhsT=xsT[:, t * P : (t + 1) * P],
+                rhs=wcT[:, j * BANK : (j + 1) * BANK],
+                start=True,
+                stop=False,
             )
-            nc.vector.quantize_mx(
-                out=h_codes[:, t, :].bitcast(FP8X4), scales=h_scales[:, t, :], in_=grouped[:]
-            )
-
-        gain_a = keep.tile([P, GATES], BF16)
-        bias = keep.tile([P, GATES], F32)
-
-        def a_gain(t):
-            a_part = a_pool.tile([P, GATES], F32)
-            for j in range(BANKS):
-                cols = slice(j * BANK, (j + 1) * BANK)
-                a_ps = psum.tile([P, BANK], F32, tag="bank")
+            for k in range(PER_BANK):
+                block = j * PER_BANK + k
                 nc.tensor.matmul(
-                    a_ps[:], lhsT=xT[:, t * P : (t + 1) * P], rhs=wT[:, cols], start=True, stop=True
+                    a_ps[:, k * P : (k + 1) * P],
+                    lhsT=bias_cols[:, block : block + 1].to_broadcast([P, P]),
+                    rhs=ident_f32[:],
+                    is_transpose=True,
+                    start=False,
+                    stop=(k == PER_BANK - 1),
                 )
-                nc.vector.scalar_tensor_tensor(
-                    out=a_part[:, cols],
-                    in0=a_ps[:],
-                    scalar=a_negmean[:, t : t + 1],
-                    in1=gain_a[:, cols],
-                    op0=ALU.add,
-                    op1=ALU.mult,
-                )
-            return a_part
-
-        def a_bias(t, a_part):
-            for half in range(2):
-                cols = slice(half * GATES // 2, (half + 1) * GATES // 2)
-                nc.vector.scalar_tensor_tensor(
-                    out=a_part[:, cols],
-                    in0=a_part[:, cols],
-                    scalar=a_rstd[:, t : t + 1],
-                    in1=bias[:, cols],
-                    op0=ALU.mult,
-                    op1=ALU.add,
-                )
-
-        def r_matmuls(t):
-            r_banks = []
-            for j in range(BANKS):
-                r_ps = psum.tile([P, BANK], F32, tag="bank")
-                for g in range(PASSES):
-                    nc.tensor.matmul_mx(
-                        out=r_ps[:],
-                        lhsT=h_codes[:, t, g * P : (g + 1) * P].bitcast(FP8X4),
-                        lhsT_scale=h_scales[:, t, g * P : (g + 1) * P],
-                        rhs=w_words[:, g, 2 * j * BANK : 2 * (j + 1) * BANK].bitcast(FP4X4),
-                        rhs_scale=w_scales[:, g, j * BANK : (j + 1) * BANK],
-                        start=(g == 0),
-                        stop=(g == PASSES - 1),
-                    )
-                r_banks.append(r_ps)
-            return r_banks
+            return a_ps
 
         def rstd_of(sum_of_squares, count):
             var = stats.tile([P, 1], F32)
@@ -302,16 +325,29 @@ def tile_multilstm_pa_kernel(
             nc.gpsimd.tensor_tensor(out=rstd[:], in0=var[:], in1=neg_half[:, 0:1], op=ALU.pow)
             return rstd
 
-        def r_stats(r_banks):
-            r_copy = gate_pool.tile([P, GATES], F32, bufs=1)
-            r_sums = stats.tile([P, BANKS], F32)
-            for j in range(BANKS):
-                nc.scalar.activation(
-                    out=r_copy[:, j * BANK : (j + 1) * BANK],
-                    in_=r_banks[j][:],
-                    func=ACT.Identity,
-                    accum_out=r_sums[:, j : j + 1],
+        def r_mm(t, j):
+            r_ps = r_bank_tile([P, BANK], F32)
+            for g in range(PASSES):
+                nc.tensor.matmul_mx(
+                    out=r_ps[:],
+                    lhsT=h_codes[:, t, g * P : (g + 1) * P].bitcast(FP8X4),
+                    lhsT_scale=h_scales[:, t, g * P : (g + 1) * P],
+                    rhs=w_words[:, g, 2 * j * BANK : 2 * (j + 1) * BANK].bitcast(FP4X4),
+                    rhs_scale=w_scales[:, g, j * BANK : (j + 1) * BANK],
+                    start=(g == 0),
+                    stop=(g == PASSES - 1),
                 )
+            return r_ps
+
+        def r_out(j, r_ps, r_copy, r_sums):
+            nc.scalar.activation(
+                out=r_copy[:, j * BANK : (j + 1) * BANK],
+                in_=r_ps[:],
+                func=ACT.Identity,
+                accum_out=r_sums[:, j : j + 1],
+            )
+
+        def r_mean(r_sums):
             r_scaled = stats.tile([P, BANKS], F32)
             r_negmean = stats.tile([P, 1], F32)
             nc.scalar.activation(
@@ -321,50 +357,124 @@ def tile_multilstm_pa_kernel(
                 scale=-1.0 / GATES,
                 accum_out=r_negmean[:],
             )
+            return r_negmean
+
+        def r_spread(r_copy, r_negmean):
+            r_squares = r_pool.tile([P, GATES], BF16, bufs=1)
             r_sumsq = stats.tile([P, 1], F32)
             nc.scalar.activation(
-                out=r_copy[:],
+                out=r_squares[:],
                 in_=r_copy[:],
                 func=ACT.Square,
                 bias=r_negmean[:],
                 accum_out=r_sumsq[:],
             )
-            return r_negmean, rstd_of(r_sumsq[:], GATES)
+            return rstd_of(r_sumsq[:], GATES)
 
-        def r_gain(r_banks, r_negmean):
-            gates = gate_pool.tile([P, GATES], F32)
-            for j in range(BANKS):
-                cols = slice(j * BANK, (j + 1) * BANK)
-                nc.vector.scalar_tensor_tensor(
-                    out=gates[:, cols],
-                    in0=r_banks[j][:],
-                    scalar=r_negmean[:],
-                    in1=gain_r[:, cols],
-                    op0=ALU.add,
-                    op1=ALU.mult,
-                )
-            return gates
-
-        def finish_gate(gates, gate, func, r_rstd, a_part):
+        def r_gain(gates, gate, r_copy, r_negmean):
             cols = slice(gate * HID, (gate + 1) * HID)
+            nc.vector.scalar_tensor_tensor(
+                out=gates[:, cols],
+                in0=r_copy[:, cols],
+                scalar=r_negmean[:],
+                in1=gain_r[:, cols],
+                op0=ALU.add,
+                op1=ALU.mult,
+            )
+
+        def add_a(gates, j, r_rstd, a_ps):
+            cols = slice(j * BANK, (j + 1) * BANK)
             nc.vector.scalar_tensor_tensor(
                 out=gates[:, cols],
                 in0=gates[:, cols],
                 scalar=r_rstd[:],
-                in1=a_part[:, cols],
+                in1=a_ps[:],
                 op0=ALU.mult,
                 op1=ALU.add,
             )
+
+        def squash(gates, gate, func):
+            cols = slice(gate * HID, (gate + 1) * HID)
             nc.scalar.activation(out=gates[:, cols], in_=gates[:, cols], func=func)
 
-        def cell(t, gates, r_rstd, a_part):
+        def new_r():
+            r_copy = r_pool.tile([P, GATES], F32)
+            r_sums = stats.tile([P, BANKS], F32)
+            return r_copy, r_sums
+
+        r_copy, r_sums = new_r()
+        for j in range(BANKS // 2):
+            r_out(j, r_mm(0, j), r_copy, r_sums)
+        x_scaled = keep.tile([P, ROW_TILES, IN], F32)
+        xsT_ps = r_bank_tile([P, BATCH], F32)
+        for t in range(ROW_TILES):
+            nc.scalar.activation(
+                out=x_scaled[:, t, :], in_=x_rows[:, t, :], func=ACT.Identity, scale=a_rstd[:, t : t + 1]
+            )
+            nc.tensor.transpose(xsT_ps[:, t * P : (t + 1) * P], x_scaled[:, t, :], ident_f32[:])
+        xsT = keep.tile([P, BATCH], F32)
+        nc.scalar.copy(out=xsT[:], in_=xsT_ps[:])
+        w_centre(0, wT_tiles[0])
+        w_centre(1, wT_tiles[1])
+        for j in range(BANKS // 2, BANKS):
+            r_out(j, r_mm(0, j), r_copy, r_sums)
+        r_negmean = r_mean(r_sums)
+        h0_quantize(1, h0_group(h0_turn(1), "vector"))
+        for q in (2, 3):
+            w_centre(q, w_turn(q))
+        a_tiles = {}
+        for j in range(Q_SLOTS):
+            a_tiles[j] = a_bank(0, j)
+        r_tiles = {}
+        for j in range(R_SLOTS):
+            r_tiles[j] = r_mm(1, j)
+        last = None
+
+        def r_step(t, j, next_copy, next_sums):
+            r_out(j, r_tiles[j], next_copy, next_sums)
+            if j + R_SLOTS < BANKS:
+                r_tiles[j + R_SLOTS] = r_mm(t, j + R_SLOTS)
+
+        for t in range(ROW_TILES):
             rows = slice(t * P, (t + 1) * P)
+            more = t + 1 < ROW_TILES
+            r_rstd = r_spread(r_copy, r_negmean)
+            gates = gate_pool.tile([P, GATES], F32)
+            for gate in range(4):
+                r_gain(gates, gate, r_copy, r_negmean)
+            if t > 0 and more:
+                h0_quantize(t + 1, h0_group(hT_next, "vector"))
+                for j in range(R_SLOTS):
+                    r_tiles[j] = r_mm(t + 1, j)
+            if last is not None:
+                lt, lcy, lgates = last
+                hy = cell_pool.tile([P, HID], F32)
+                nc.scalar.activation(out=hy[:], in_=lcy[:], func=ACT.Tanh)
+            if more:
+                next_copy, next_sums = new_r()
+            for gate, func in enumerate((ACT.Sigmoid, ACT.Sigmoid, ACT.Tanh)):
+                for j in (2 * gate, 2 * gate + 1):
+                    add_a(gates, j, r_rstd, a_tiles[j])
+                    if j + Q_SLOTS < BANKS:
+                        a_tiles[j + Q_SLOTS] = a_bank(t, j + Q_SLOTS)
+                squash(gates, gate, func)
+                if more:
+                    r_step(t + 1, gate, next_copy, next_sums)
+                if gate == 0 and last is not None:
+                    nc.vector.tensor_tensor(out=hy[:], in0=hy[:], in1=lgates[:, 3 * HID : 4 * HID], op=ALU.mult)
+                    nc.sync.dma_start(out=out_0[lt * P : (lt + 1) * P, :], in_=hy[:])
             gate_i = gates[:, 0:HID]
             gate_f = gates[:, HID : 2 * HID]
             gate_g = gates[:, 2 * HID : 3 * HID]
-            gate_o = gates[:, 3 * HID : 4 * HID]
-            nc.vector.tensor_tensor(out=gate_f, in0=gate_f, in1=c_rows[:, t, :], op=ALU.mult)
-            nc.vector.tensor_tensor(out=gate_i, in0=gate_i, in1=gate_g, op=ALU.mult)
+            if more:
+                for j in (3, 4, 5):
+                    r_step(t + 1, j, next_copy, next_sums)
+            mul_engine = nc.gpsimd if POOL_PRODUCTS else nc.vector
+            mul_engine.tensor_tensor(out=gate_f, in0=gate_f, in1=c_rows[:, t, :], op=ALU.mult)
+            mul_engine.tensor_tensor(out=gate_i, in0=gate_i, in1=gate_g, op=ALU.mult)
+            if POOL_PRODUCTS:
+                for j in (6, 7):
+                    add_a(gates, j, r_rstd, a_tiles[j])
             cy = cell_pool.tile([P, HID], F32)
             c_sum = stats.tile([P, 1], F32)
             nc.vector.scalar_tensor_tensor(
@@ -376,15 +486,29 @@ def tile_multilstm_pa_kernel(
                 op1=ALU.add,
                 accum_out=c_sum[:],
             )
-            finish_gate(gates, 3, ACT.Sigmoid, r_rstd, a_part)
             c_negmean = stats.tile([P, 1], F32)
-            nc.scalar.mul(out=c_negmean[:], in_=c_sum[:], mul=-1.0 / HID)
+            nc.vector.tensor_scalar(
+                out=c_negmean[:], in0=c_sum[:], scalar1=-1.0 / HID, scalar2=None, op0=ALU.mult
+            )
             squares = cell_pool.tile([P, HID], BF16)
             c_sumsq = stats.tile([P, 1], F32)
             nc.scalar.activation(
                 out=squares[:], in_=cy[:], func=ACT.Square, bias=c_negmean[:], accum_out=c_sumsq[:]
             )
             c_rstd = rstd_of(c_sumsq[:], HID)
+            if not POOL_PRODUCTS:
+                for j in (6, 7):
+                    add_a(gates, j, r_rstd, a_tiles[j])
+            squash(gates, 3, ACT.Sigmoid)
+            if more:
+                for j in range(6, BANKS):
+                    r_step(t + 1, j, next_copy, next_sums)
+                r_negmean = r_mean(next_sums)
+                r_copy = next_copy
+                for j in range(Q_SLOTS):
+                    a_tiles[j] = a_bank(t + 1, j)
+                if t + 2 < ROW_TILES:
+                    hT_next = h0_turn(t + 2)
             nc.vector.scalar_tensor_tensor(
                 out=cy[:], in0=cy[:], scalar=c_negmean[:], in1=gain_c[:], op0=ALU.add, op1=ALU.mult
             )
@@ -392,30 +516,10 @@ def tile_multilstm_pa_kernel(
                 out=cy[:], in0=cy[:], scalar=c_rstd[:], in1=bias_c[:], op0=ALU.mult, op1=ALU.add
             )
             nc.sync.dma_start(out=out_1[rows, :], in_=cy[:])
-            hy = cell_pool.tile([P, HID], F32)
-            nc.scalar.activation(out=hy[:], in_=cy[:], func=ACT.Tanh)
-            nc.vector.tensor_tensor(out=hy[:], in0=hy[:], in1=gate_o, op=ALU.mult)
-            nc.sync.dma_start(out=out_0[rows, :], in_=hy[:])
 
-        spread(gain_a, vec_cols[:, 0:BLOCKS], ident_bf[:])
-        a_parts = [a_gain(0), a_gain(1)]
-        spread(bias, bias_cols[:], ident_f32[:])
-        for t in range(ROW_TILES):
-            h0_to_mxfp8(t)
-        a_bias(0, a_parts[0])
-        a_bias(1, a_parts[1])
-
-        r_banks = r_matmuls(0)
-        r_negmean, r_rstd = r_stats(r_banks)
-        for t in range(ROW_TILES):
-            gates = r_gain(r_banks, r_negmean)
-            for gate, func in enumerate((ACT.Sigmoid, ACT.Sigmoid, ACT.Tanh)):
-                finish_gate(gates, gate, func, r_rstd, a_parts[t])
-            this_rstd = r_rstd
-            if t + 2 < ROW_TILES:
-                a_parts.append(a_gain(t + 2))
-                a_bias(t + 2, a_parts[t + 2])
-            if t + 1 < ROW_TILES:
-                r_banks = r_matmuls(t + 1)
-                r_negmean, r_rstd = r_stats(r_banks)
-            cell(t, gates, this_rstd, a_parts[t])
+            last = (t, cy, gates)
+        lt, lcy, lgates = last
+        hy = cell_pool.tile([P, HID], F32)
+        nc.scalar.activation(out=hy[:], in_=lcy[:], func=ACT.Tanh)
+        nc.vector.tensor_tensor(out=hy[:], in0=hy[:], in1=lgates[:, 3 * HID : 4 * HID], op=ALU.mult)
+        nc.sync.dma_start(out=out_0[lt * P : (lt + 1) * P, :], in_=hy[:])

@@ -31,7 +31,21 @@ W_ROW = IN + 16
 QUARTER = BLOCKS // 4
 R_SLOTS = 3
 Q_SLOTS = 5
-POOL_PRODUCTS = False
+SPREAD_TAG = "q"
+SPREAD_COPY = ["scalar"] * 4 + ["vector"] * 4
+H_COPY = ["scalar", "vector", "vector", "vector"]
+XS_ENGINE = "scalar"
+XC_ENGINE = "scalar"
+M1_POOL = [False] * 4
+HY_POOL = [False] * 4
+SQ_DVE = False
+P1_DVE = []
+ORDER = [0, 1, 2, 3, 4, 5, 6, 7]
+HY_AT = 2
+PA = 2
+PB = 3
+PD = 6
+LAST_PARTS = 2
 
 FLOPS = 2 * BATCH * GATES * (HID + IN)
 
@@ -184,14 +198,20 @@ def tile_multilstm_pa_kernel(
         gain_a = keep.tile([P, GATES], BF16)
 
         def spread_gain(first):
-            spread_ps = r_bank_tile([P, BANK], BF16)
+            spread_ps = (r_bank_tile if SPREAD_TAG == "r" else q_bank_tile)([P, BANK], BF16)
             for k in range(PER_BANK):
                 nc.tensor.transpose(
                     spread_ps[:, k * P : (k + 1) * P],
                     vec_cols[:, first + k : first + k + 1].to_broadcast([P, P]),
                     ident_bf[:],
                 )
-            nc.vector.tensor_copy(out=gain_a[:, first * P : (first + PER_BANK) * P], in_=spread_ps[:])
+            return spread_ps
+
+        def spread_out(first, spread_ps, engine):
+            if engine == "scalar":
+                nc.scalar.copy(out=gain_a[:, first * P : (first + PER_BANK) * P], in_=spread_ps[:])
+            else:
+                nc.vector.tensor_copy(out=gain_a[:, first * P : (first + PER_BANK) * P], in_=spread_ps[:])
 
         gram_ps = q_bank_tile([P, IN + ONES], F32)
 
@@ -205,24 +225,18 @@ def tile_multilstm_pa_kernel(
                     stop=(j == BLOCKS - 1),
                 )
 
-        for q in range(4):
-            if q == 3:
-                grouped_0 = h0_group(h0_turn(0), "scalar")
-            spread_gain(2 * q * PER_BANK)
-            spread_gain((2 * q + 1) * PER_BANK)
-            gram_quarter(q * QUARTER)
-
         neg_wmean = keep.tile([P, 1], F32)
-        nc.vector.tensor_scalar(
-            out=neg_wmean[:],
-            in0=gram_ps[:, IN : IN + 1],
-            scalar1=-1.0 / GATES,
-            scalar2=None,
-            op0=ALU.mult,
-        )
         gram = keep.tile([P, IN + ONES], F32)
-        nc.vector.tensor_copy(out=gram[:], in_=gram_ps[:])
-        h0_quantize(0, grouped_0)
+
+        def gram_out():
+            nc.vector.tensor_scalar(
+                out=neg_wmean[:],
+                in0=gram_ps[:, IN : IN + 1],
+                scalar1=-1.0 / GATES,
+                scalar2=None,
+                op0=ALU.mult,
+            )
+            nc.vector.tensor_copy(out=gram[:], in_=gram_ps[:])
 
         wcT = keep.tile([P, GATES], F32)
 
@@ -248,11 +262,17 @@ def tile_multilstm_pa_kernel(
         a_negmean = keep.tile([P, ROW_TILES], F32)
         a_sumsq = keep.tile([P, ROW_TILES], F32)
 
-        def a_sums(t):
-            xm_ps = r_bank_tile([P, IN + ONES], F32)
-            nc.tensor.matmul(
-                xm_ps[:], lhsT=xT_f32[:, t * P : (t + 1) * P], rhs=gram[:], start=True, stop=True
-            )
+        def a_sums_mm(pair):
+            xm_ps = r_bank_tile([P, 2, IN + ONES], F32)
+            for i in range(2):
+                t = 2 * pair + i
+                nc.tensor.matmul(
+                    xm_ps[:, i, :], lhsT=xT_f32[:, t * P : (t + 1) * P], rhs=gram[:], start=True, stop=True
+                )
+            return xm_ps
+
+        def a_sums(t, xm_pair):
+            xm_ps = xm_pair[:, t % 2, :]
             products = stage.tile([P, IN], F32)
             nc.vector.scalar_tensor_tensor(
                 out=products[:],
@@ -271,25 +291,27 @@ def tile_multilstm_pa_kernel(
                 op0=ALU.mult,
             )
 
-        wT_tiles = [w_turn(0), w_turn(1)]
-        for t in range(ROW_TILES):
-            a_sums(t)
         a_meansq = keep.tile([P, ROW_TILES], F32)
-        nc.vector.tensor_tensor(out=a_meansq[:], in0=a_negmean[:], in1=a_negmean[:], op=ALU.mult)
         a_var = keep.tile([P, ROW_TILES], F32)
-        nc.vector.scalar_tensor_tensor(
-            out=a_var[:],
-            in0=a_sumsq[:],
-            scalar=1.0 / GATES,
-            in1=a_meansq[:],
-            op0=ALU.mult,
-            op1=ALU.subtract,
-        )
-        nc.vector.tensor_scalar(
-            out=a_var[:], in0=a_var[:], scalar1=EPS, scalar2=None, op0=ALU.add
-        )
         a_rstd = keep.tile([P, ROW_TILES], F32)
-        nc.gpsimd.tensor_tensor(out=a_rstd[:], in0=a_var[:], in1=neg_half[:], op=ALU.pow)
+
+        def a_spread():
+            nc.vector.tensor_tensor(out=a_meansq[:], in0=a_negmean[:], in1=a_negmean[:], op=ALU.mult)
+            nc.vector.scalar_tensor_tensor(
+                out=a_var[:],
+                in0=a_sumsq[:],
+                scalar=1.0 / GATES,
+                in1=a_meansq[:],
+                op0=ALU.mult,
+                op1=ALU.subtract,
+            )
+            nc.vector.tensor_scalar(
+                out=a_var[:], in0=a_var[:], scalar1=EPS, scalar2=None, op0=ALU.add
+            )
+            nc.gpsimd.tensor_tensor(out=a_rstd[:], in0=a_var[:], in1=neg_half[:], op=ALU.pow)
+
+        x_scaled = keep.tile([P, ROW_TILES, IN], F32)
+        xsT = keep.tile([P, BATCH], F32)
         def a_bank(t, j):
             a_ps = q_bank_tile([P, BANK], F32)
             nc.tensor.matmul(
@@ -371,8 +393,8 @@ def tile_multilstm_pa_kernel(
             )
             return rstd_of(r_sumsq[:], GATES)
 
-        def r_gain(gates, gate, r_copy, r_negmean):
-            cols = slice(gate * HID, (gate + 1) * HID)
+        def r_gain(gates, half, r_copy, r_negmean):
+            cols = slice(half * GATES // 2, (half + 1) * GATES // 2)
             nc.vector.scalar_tensor_tensor(
                 out=gates[:, cols],
                 in0=r_copy[:, cols],
@@ -397,91 +419,163 @@ def tile_multilstm_pa_kernel(
             cols = slice(gate * HID, (gate + 1) * HID)
             nc.scalar.activation(out=gates[:, cols], in_=gates[:, cols], func=func)
 
+        S = {}
+        ops = {}
+        bank_tag = {}
+        bank_users = {}
+        done = set()
+        banks_taken = {"r": [], "q": []}
+        slots = {"r": R_SLOTS, "q": Q_SLOTS}
+
+        def step(name, deps, what):
+            ops[name] = (what, deps)
+
+        banks_taken["r"] += [("VEC",), ("XT0",)]
+        bank_users["VEC",] = []
+        bank_users["XT0",] = []
+        banks_taken["q"] += [("GRAM",)]
+        bank_users["GRAM",] = [("NW",)]
+
         def new_r():
             r_copy = r_pool.tile([P, GATES], F32)
             r_sums = stats.tile([P, BANKS], F32)
             return r_copy, r_sums
 
-        r_copy, r_sums = new_r()
-        for j in range(BANKS // 2):
-            r_out(j, r_mm(0, j), r_copy, r_sums)
-        x_scaled = keep.tile([P, ROW_TILES, IN], F32)
-        xsT_ps = r_bank_tile([P, BATCH], F32)
-        for t in range(ROW_TILES):
-            nc.scalar.activation(
-                out=x_scaled[:, t, :], in_=x_rows[:, t, :], func=ACT.Identity, scale=a_rstd[:, t : t + 1]
-            )
-            nc.tensor.transpose(xsT_ps[:, t * P : (t + 1) * P], x_scaled[:, t, :], ident_f32[:])
-        xsT = keep.tile([P, BATCH], F32)
-        nc.scalar.copy(out=xsT[:], in_=xsT_ps[:])
-        w_centre(0, wT_tiles[0])
-        w_centre(1, wT_tiles[1])
-        for j in range(BANKS // 2, BANKS):
-            r_out(j, r_mm(0, j), r_copy, r_sums)
-        r_negmean = r_mean(r_sums)
-        h0_quantize(1, h0_group(h0_turn(1), "vector"))
-        for q in (2, 3):
-            w_centre(q, w_turn(q))
-        a_tiles = {}
-        for j in range(Q_SLOTS):
-            a_tiles[j] = a_bank(0, j)
-        r_tiles = {}
-        for j in range(R_SLOTS):
-            r_tiles[j] = r_mm(1, j)
-        last = None
+        def do_SP(g):
+            S["sp", g] = spread_gain(g * PER_BANK)
 
-        def r_step(t, j, next_copy, next_sums):
-            r_out(j, r_tiles[j], next_copy, next_sums)
-            if j + R_SLOTS < BANKS:
-                r_tiles[j + R_SLOTS] = r_mm(t, j + R_SLOTS)
+        def do_XM(pair):
+            S["xm", pair] = a_sums_mm(pair)
 
+        def do_WT(q):
+            S["wT", q] = w_turn(q)
+
+        def do_XS():
+            for t in range(ROW_TILES):
+                if XS_ENGINE == "scalar":
+                    nc.scalar.activation(
+                        out=x_scaled[:, t, :], in_=x_rows[:, t, :], func=ACT.Identity, scale=a_rstd[:, t : t + 1]
+                    )
+                elif XS_ENGINE == "gpsimd":
+                    nc.gpsimd.tensor_scalar(
+                        out=x_scaled[:, t, :],
+                        in0=x_rows[:, t, :],
+                        scalar1=a_rstd[:, t : t + 1],
+                        scalar2=0.0,
+                        op0=ALU.mult,
+                        op1=ALU.add,
+                    )
+                else:
+                    nc.vector.tensor_scalar(
+                        out=x_scaled[:, t, :],
+                        in0=x_rows[:, t, :],
+                        scalar1=a_rstd[:, t : t + 1],
+                        scalar2=None,
+                        op0=ALU.mult,
+                    )
+
+        def do_XC():
+            if XC_ENGINE == "scalar":
+                nc.scalar.copy(out=xsT[:], in_=S["xsT_ps"][:])
+            else:
+                nc.vector.tensor_copy(out=xsT[:], in_=S["xsT_ps"][:])
+
+        def do_XT():
+            xsT_ps = r_bank_tile([P, BATCH], F32)
+            for t in range(ROW_TILES):
+                nc.tensor.transpose(xsT_ps[:, t * P : (t + 1) * P], x_scaled[:, t, :], ident_f32[:])
+            S["xsT_ps"] = xsT_ps
+
+        for g in range(BANKS):
+            step(("SP", g), [], lambda g=g: do_SP(g))
+            bank_tag["SP", g] = SPREAD_TAG
+            bank_users["SP", g] = [("SPC", g)]
+            step(("SPC", g), [("SP", g)], lambda g=g: spread_out(g * PER_BANK, S["sp", g], SPREAD_COPY[g]))
+        for q in range(4):
+            step(("G", q), [], lambda q=q: gram_quarter(q * QUARTER))
+            step(("WT", q), [], lambda q=q: do_WT(q))
+            bank_tag["WT", q] = "q"
+            bank_users["WT", q] = [("WC", q)]
+            step(("WC", q), [("WT", q), ("NW",), ("SPC", 2 * q), ("SPC", 2 * q + 1)], lambda q=q: w_centre(q, S["wT", q]))
+        step(("NW",), [("G", 3)], gram_out)
+        for pair in range(ROW_TILES // 2):
+            step(("XM", pair), [("NW",)], lambda pair=pair: do_XM(pair))
+            bank_tag["XM", pair] = "r"
+            bank_users["XM", pair] = [("AS", 2 * pair), ("AS", 2 * pair + 1)]
         for t in range(ROW_TILES):
-            rows = slice(t * P, (t + 1) * P)
-            more = t + 1 < ROW_TILES
-            r_rstd = r_spread(r_copy, r_negmean)
-            gates = gate_pool.tile([P, GATES], F32)
-            for gate in range(4):
-                r_gain(gates, gate, r_copy, r_negmean)
-            if t > 0 and more:
-                h0_quantize(t + 1, h0_group(hT_next, "vector"))
-                for j in range(R_SLOTS):
-                    r_tiles[j] = r_mm(t + 1, j)
-            if last is not None:
-                lt, lcy, lgates = last
-                hy = cell_pool.tile([P, HID], F32)
-                nc.scalar.activation(out=hy[:], in_=lcy[:], func=ACT.Tanh)
-            if more:
-                next_copy, next_sums = new_r()
-            for gate, func in enumerate((ACT.Sigmoid, ACT.Sigmoid, ACT.Tanh)):
-                for j in (2 * gate, 2 * gate + 1):
-                    add_a(gates, j, r_rstd, a_tiles[j])
-                    if j + Q_SLOTS < BANKS:
-                        a_tiles[j + Q_SLOTS] = a_bank(t, j + Q_SLOTS)
-                squash(gates, gate, func)
-                if more:
-                    r_step(t + 1, gate, next_copy, next_sums)
-                if gate == 0 and last is not None:
-                    nc.vector.tensor_tensor(out=hy[:], in0=hy[:], in1=lgates[:, 3 * HID : 4 * HID], op=ALU.mult)
-                    nc.sync.dma_start(out=out_0[lt * P : (lt + 1) * P, :], in_=hy[:])
-            gate_i = gates[:, 0:HID]
-            gate_f = gates[:, HID : 2 * HID]
-            gate_g = gates[:, 2 * HID : 3 * HID]
-            if more:
-                for j in (3, 4, 5):
-                    r_step(t + 1, j, next_copy, next_sums)
-            mul_engine = nc.gpsimd if POOL_PRODUCTS else nc.vector
-            mul_engine.tensor_tensor(out=gate_f, in0=gate_f, in1=c_rows[:, t, :], op=ALU.mult)
-            mul_engine.tensor_tensor(out=gate_i, in0=gate_i, in1=gate_g, op=ALU.mult)
-            if POOL_PRODUCTS:
-                for j in (6, 7):
-                    add_a(gates, j, r_rstd, a_tiles[j])
+            step(("AS", t), [("XM", t // 2)], lambda t=t: a_sums(t, S["xm", t // 2]))
+        step(("AV",), [("AS", t) for t in range(ROW_TILES)], a_spread)
+        step(("XS",), [("AV",)], do_XS)
+        step(("XT",), [("XS",)], do_XT)
+        bank_tag["XT",] = "r"
+        bank_users["XT",] = [("XC",)]
+        step(("XC",), [("XT",)], do_XC)
+
+        def do_R(t, j):
+            S["r", t, j] = r_mm(t, j)
+
+        def do_P1(t, j):
+            if j == 0:
+                S["copy", t], S["sums", t] = new_r()
+            if j in P1_DVE and t > 0:
+                nc.vector.tensor_scalar(
+                    out=S["copy", t][:, j * BANK : (j + 1) * BANK],
+                    in0=S["r", t, j][:],
+                    scalar1=1.0,
+                    scalar2=None,
+                    op0=ALU.mult,
+                    accum_out=S["sums", t][:, j : j + 1],
+                )
+            else:
+                r_out(j, S["r", t, j], S["copy", t], S["sums", t])
+
+        def do_MEAN(t):
+            S["negmean", t] = r_mean(S["sums", t])
+
+        def do_P2(t):
+            S["rstd", t] = r_spread(S["copy", t], S["negmean", t])
+
+        def do_G1(t, half):
+            if half == 0:
+                gates = gate_pool.tile([P, GATES], F32)
+                S["gates", t] = gates
+            r_gain(S["gates", t], half, S["copy", t], S["negmean", t])
+
+        def do_Q(t, j):
+            S["a", t, j] = a_bank(t, j)
+
+        def do_A2(t, j):
+            add_a(S["gates", t], j, S["rstd", t], S["a", t, j])
+
+        def do_F(t, gate):
+            squash(S["gates", t], gate, ACT.Tanh if gate == 2 else ACT.Sigmoid)
+
+        def do_HT(t):
+            S["hT", t] = h0_turn(t)
+
+        def do_HC(t):
+            S["grouped", t] = h0_group(S["hT", t], H_COPY[t])
+
+        def do_HQ(t):
+            h0_quantize(t, S["grouped", t])
+
+        def do_M1(t):
+            gate_f = S["gates", t][:, HID : 2 * HID]
+            engine = nc.gpsimd if M1_POOL[t] else nc.vector
+            engine.tensor_tensor(out=gate_f, in0=gate_f, in1=c_rows[:, t, :], op=ALU.mult)
+
+        def do_M2(t):
+            gate_i = S["gates", t][:, 0:HID]
+            nc.vector.tensor_tensor(out=gate_i, in0=gate_i, in1=S["gates", t][:, 2 * HID : 3 * HID], op=ALU.mult)
+
+        def do_C(t):
             cy = cell_pool.tile([P, HID], F32)
             c_sum = stats.tile([P, 1], F32)
             nc.vector.scalar_tensor_tensor(
                 out=cy[:],
-                in0=gate_f,
+                in0=S["gates", t][:, HID : 2 * HID],
                 scalar=1.0,
-                in1=gate_i,
+                in1=S["gates", t][:, 0:HID],
                 op0=ALU.mult,
                 op1=ALU.add,
                 accum_out=c_sum[:],
@@ -490,36 +584,173 @@ def tile_multilstm_pa_kernel(
             nc.vector.tensor_scalar(
                 out=c_negmean[:], in0=c_sum[:], scalar1=-1.0 / HID, scalar2=None, op0=ALU.mult
             )
+            S["cy", t] = cy
+            S["c_negmean", t] = c_negmean
+
+        def do_SQ(t):
             squares = cell_pool.tile([P, HID], BF16)
             c_sumsq = stats.tile([P, 1], F32)
-            nc.scalar.activation(
-                out=squares[:], in_=cy[:], func=ACT.Square, bias=c_negmean[:], accum_out=c_sumsq[:]
-            )
-            c_rstd = rstd_of(c_sumsq[:], HID)
-            if not POOL_PRODUCTS:
-                for j in (6, 7):
-                    add_a(gates, j, r_rstd, a_tiles[j])
-            squash(gates, 3, ACT.Sigmoid)
-            if more:
-                for j in range(6, BANKS):
-                    r_step(t + 1, j, next_copy, next_sums)
-                r_negmean = r_mean(next_sums)
-                r_copy = next_copy
-                for j in range(Q_SLOTS):
-                    a_tiles[j] = a_bank(t + 1, j)
-                if t + 2 < ROW_TILES:
-                    hT_next = h0_turn(t + 2)
-            nc.vector.scalar_tensor_tensor(
-                out=cy[:], in0=cy[:], scalar=c_negmean[:], in1=gain_c[:], op0=ALU.add, op1=ALU.mult
-            )
-            nc.vector.scalar_tensor_tensor(
-                out=cy[:], in0=cy[:], scalar=c_rstd[:], in1=bias_c[:], op0=ALU.mult, op1=ALU.add
-            )
-            nc.sync.dma_start(out=out_1[rows, :], in_=cy[:])
+            if SQ_DVE:
+                nc.vector.scalar_tensor_tensor(
+                    out=squares[:],
+                    in0=S["cy", t][:],
+                    scalar=S["c_negmean", t][:],
+                    in1=S["cy", t][:],
+                    op0=ALU.add,
+                    op1=ALU.mult,
+                    accum_out=c_sumsq[:],
+                )
+            else:
+                nc.scalar.activation(
+                    out=squares[:], in_=S["cy", t][:], func=ACT.Square, bias=S["c_negmean", t][:], accum_out=c_sumsq[:]
+                )
+            S["c_rstd", t] = rstd_of(c_sumsq[:], HID)
 
-            last = (t, cy, gates)
-        lt, lcy, lgates = last
-        hy = cell_pool.tile([P, HID], F32)
-        nc.scalar.activation(out=hy[:], in_=lcy[:], func=ACT.Tanh)
-        nc.vector.tensor_tensor(out=hy[:], in0=hy[:], in1=lgates[:, 3 * HID : 4 * HID], op=ALU.mult)
-        nc.sync.dma_start(out=out_0[lt * P : (lt + 1) * P, :], in_=hy[:])
+        def do_V1(t):
+            v1 = cell_pool.tile([P, HID], F32)
+            nc.vector.scalar_tensor_tensor(
+                out=v1[:], in0=S["cy", t][:], scalar=S["c_negmean", t][:], in1=gain_c[:], op0=ALU.add, op1=ALU.mult
+            )
+            S["v1", t] = v1
+
+        def do_CY(t):
+            v1 = S["v1", t]
+            nc.vector.scalar_tensor_tensor(
+                out=v1[:], in0=v1[:], scalar=S["c_rstd", t][:], in1=bias_c[:], op0=ALU.mult, op1=ALU.add
+            )
+            nc.sync.dma_start(out=out_1[t * P : (t + 1) * P, :], in_=v1[:])
+
+        def do_TH(t, part, parts):
+            if part == 0:
+                hy = cell_pool.tile([P, HID], F32)
+                S["hy", t] = hy
+            cols = slice(part * HID // parts, (part + 1) * HID // parts)
+            nc.scalar.activation(out=S["hy", t][:, cols], in_=S["v1", t][:, cols], func=ACT.Tanh)
+
+        def do_HY(t, part, parts):
+            hy = S["hy", t]
+            engine = nc.gpsimd if HY_POOL[t] else nc.vector
+            cols = slice(part * HID // parts, (part + 1) * HID // parts)
+            o_cols = slice(3 * HID + part * HID // parts, 3 * HID + (part + 1) * HID // parts)
+            engine.tensor_tensor(out=hy[:, cols], in0=hy[:, cols], in1=S["gates", t][:, o_cols], op=ALU.mult)
+            nc.sync.dma_start(out=out_0[t * P : (t + 1) * P, cols], in_=hy[:, cols])
+
+        for t in range(ROW_TILES):
+            for j in range(BANKS):
+                step(("R", t, j), [("HQ", t)], lambda t=t, j=j: do_R(t, j))
+                bank_tag["R", t, j] = "r"
+                bank_users["R", t, j] = [("P1", t, j)]
+                step(("P1", t, j), [("R", t, j)] + ([("P1", t, 0)] if j else []), lambda t=t, j=j: do_P1(t, j))
+                step(("Q", t, j), [("XC",), ("WC", j // 2)], lambda t=t, j=j: do_Q(t, j))
+                bank_tag["Q", t, j] = "q"
+                bank_users["Q", t, j] = [("A2", t, j)]
+                step(("A2", t, j), [("Q", t, j), ("G1", t, j // 4), ("P2", t)], lambda t=t, j=j: do_A2(t, j))
+            step(("MEAN", t), [("P1", t, j) for j in range(BANKS)], lambda t=t: do_MEAN(t))
+            step(("P2", t), [("MEAN", t)], lambda t=t: do_P2(t))
+            for gate in range(4):
+                if gate < 2:
+                    step(("G1", t, gate), [("MEAN", t)] + ([("G1", t, 0)] if gate else []), lambda t=t, gate=gate: do_G1(t, gate))
+                step(("F", t, gate), [("A2", t, 2 * gate), ("A2", t, 2 * gate + 1)], lambda t=t, gate=gate: do_F(t, gate))
+            step(("HT", t), [], lambda t=t: do_HT(t))
+            bank_tag["HT", t] = "r"
+            bank_users["HT", t] = [("HC", t)]
+            step(("HC", t), [("HT", t)], lambda t=t: do_HC(t))
+            step(("HQ", t), [("HC", t)], lambda t=t: do_HQ(t))
+            step(("M1", t), [("F", t, 1)], lambda t=t: do_M1(t))
+            step(("M2", t), [("F", t, 0), ("F", t, 2)], lambda t=t: do_M2(t))
+            step(("C", t), [("M1", t), ("M2", t)], lambda t=t: do_C(t))
+            step(("SQ", t), [("C", t)], lambda t=t: do_SQ(t))
+            step(("V1", t), [("C", t)], lambda t=t: do_V1(t))
+            step(("CY", t), [("V1", t), ("SQ", t)], lambda t=t: do_CY(t))
+            parts = LAST_PARTS if t == ROW_TILES - 1 else 1
+            for part in range(parts):
+                step(("TH", t, part), [("CY", t)] + ([("TH", t, 0)] if part else []), lambda t=t, part=part, parts=parts: do_TH(t, part, parts))
+                step(("HY", t, part), [("TH", t, part), ("F", t, 3)], lambda t=t, part=part, parts=parts: do_HY(t, part, parts))
+
+        tensor_q = []
+        scalar_q = []
+        vector_q = []
+        R0 = [("R", 0, j) for j in range(BANKS)]
+        P10 = [("P1", 0, j) for j in range(BANKS)]
+        SP = [("SP", g) for g in range(BANKS)]
+        SPC = [("SPC", g) for g in range(BANKS)]
+        G = [("G", q) for q in range(4)]
+        XM = [("XM", pair) for pair in range(ROW_TILES // 2)]
+        AS = [("AS", t) for t in range(ROW_TILES)]
+        WT = [("WT", q) for q in range(4)]
+        WC = [("WC", q) for q in range(4)]
+        Q0 = [("Q", 0, j) for j in ORDER[0:Q_SLOTS]]
+        R1 = [("R", 1, j) for j in range(R_SLOTS)]
+        tensor_q += SP[0:2] + G + [("HT", 0)] + XM + SP[2:4] + WT[0:2] + R0[0:3] + SP[4:8] + WT[2:4] + [("XT",)] + R0[3:8] + [("HT", 1)] + Q0 + R1
+        scalar_q += SPC[0:2] + [("HC", 0)] + SPC[2:4] + P10[0:1] + [("XS",)] + P10[1:3] + [("XC",)] + P10[3:8] + [("MEAN", 0)]
+        vector_q += [("NW",), ("HQ", 0)] + AS + [("AV",)] + WC[0:2] + SPC[4:8] + WC[2:4] + [("HC", 1), ("HQ", 1)]
+        for f in range(ROW_TILES):
+            prev = f >= 1
+            nxt = f + 1 < ROW_TILES
+            nxt2 = f + 2 < ROW_TILES
+            a2 = [("A2", f, j) for j in ORDER]
+            p1 = [("P1", f + 1, j) for j in range(BANKS)] if nxt else []
+            p1_act = [s for s in p1 if s[2] not in P1_DVE]
+            p1_dve = [s for s in p1 if s[2] in P1_DVE]
+            vector_q += [("G1", f, 0), ("G1", f, 1)]
+            vector_q += a2[0:HY_AT]
+            if prev and not HY_POOL[f - 1]:
+                vector_q += [("HY", f - 1, 0)]
+            vector_q += a2[HY_AT:8]
+            vector_q += p1_dve
+            if not M1_POOL[f]:
+                vector_q += [("M1", f)]
+            vector_q += [("M2", f), ("C", f)]
+            if SQ_DVE:
+                vector_q += [("SQ", f)]
+            vector_q += [("V1", f)]
+            if nxt2:
+                vector_q += [("HC", f + 2), ("HQ", f + 2)]
+            vector_q += [("CY", f)]
+
+            scalar_q += [("P2", f)]
+            if prev:
+                scalar_q += [("TH", f - 1, 0)]
+                if HY_POOL[f - 1]:
+                    scalar_q += [("HY", f - 1, 0)]
+            fs = [("F", f, ORDER[2 * k] // 2) for k in range(4)]
+            scalar_q += p1_act[0:PA] + fs[0:1] + ([("M1", f)] if M1_POOL[f] else []) + p1_act[PA:PB] + fs[1:4]
+            scalar_q += p1_act[PB:PD] + ([] if SQ_DVE else [("SQ", f)]) + p1_act[PD:8]
+            if nxt:
+                scalar_q += [("MEAN", f + 1)]
+
+            tensor_q += [("Q", f, j) for j in ORDER[Q_SLOTS:BANKS]]
+            if nxt:
+                tensor_q += [("R", f + 1, j) for j in range(R_SLOTS, BANKS)]
+                if nxt2:
+                    tensor_q += [("HT", f + 2)]
+                tensor_q += [("Q", f + 1, j) for j in ORDER[0:Q_SLOTS]]
+                if nxt2:
+                    tensor_q += [("R", f + 2, j) for j in range(R_SLOTS)]
+        scalar_q += [("TH", ROW_TILES - 1, part) for part in range(LAST_PARTS)]
+        vector_q += [("HY", ROW_TILES - 1, part) for part in range(LAST_PARTS)]
+
+        queues = [tensor_q, scalar_q, vector_q]
+        place = [0, 0, 0]
+        moved = True
+        while moved:
+            moved = False
+            for e in range(3):
+                while place[e] < len(queues[e]):
+                    name = queues[e][place[e]]
+                    what, deps = ops[name]
+                    if not all(d in done for d in deps):
+                        break
+                    tag = bank_tag.get(name)
+                    if tag is not None:
+                        taken = banks_taken[tag]
+                        if len(taken) >= slots[tag]:
+                            old = taken[len(taken) - slots[tag]]
+                            if not all(u in done for u in bank_users[old]):
+                                break
+                        taken.append(name)
+                    what()
+                    done.add(name)
+                    place[e] += 1
+                    moved = True
+        assert all(place[e] == len(queues[e]) for e in range(3))

@@ -36,11 +36,11 @@ SPREAD_COPY = ["scalar"] * 4 + ["vector"] * 4
 H_COPY = ["scalar", "vector", "vector", "vector"]
 XS_ENGINE = "scalar"
 XC_ENGINE = "scalar"
-M1_POOL = [False] * 4
-HY_POOL = [False] * 4
+M1_POOL = [True] * 4
+HY_POOL = [True, True, True, False]
 SQ_DVE = False
 P1_DVE = []
-ORDER = [0, 1, 2, 3, 4, 5, 6, 7]
+ORDER = [2, 3, 0, 1, 4, 5, 6, 7]
 HY_AT = 2
 PA = 2
 PB = 3

@@ -34,8 +34,8 @@ Q_SLOTS = 5
 SPREAD_TAG = "q"
 SPREAD_COPY = ["scalar"] * 4 + ["vector"] * 4
 H_COPY = ["scalar", "vector", "vector", "vector"]
-XS_ENGINE = "scalar"
-XC_ENGINE = "scalar"
+XS_ENGINE = "gpsimd"
+XC_ENGINE = "vector"
 M1_POOL = [True] * 4
 HY_POOL = [True, True, True, False]
 SQ_DVE = False
@@ -46,6 +46,12 @@ PA = 2
 PB = 3
 PD = 6
 LAST_PARTS = 2
+M2_POOL = [False] * 4
+HC_EARLY = False
+GAIN_AT = [1, 2]
+PA0 = 2
+PB0 = 3
+LAST_IN_R = True
 
 FLOPS = 2 * BATCH * GATES * (HID + IN)
 
@@ -114,6 +120,15 @@ def tile_multilstm_pa_kernel(
         for first in range(0, BLOCKS, QUARTER):
             some = slice(first, first + QUARTER)
             nc.sync.dma_start(out=w_rows[:, some, 0:IN], in_=w_blocks[:, some, :])
+        gain_a = keep.tile([P, GATES], BF16)
+
+        def load_gain(part):
+            cols = slice(part * GATES // 2, (part + 1) * GATES // 2)
+            nc.sync.dma_start(out=gain_a[:, cols], in_=lni_w1[cols].partition_broadcast(P))
+
+        for part in range(2):
+            if GAIN_AT[part] == 0:
+                load_gain(part)
         h_rows = keep.tile([P, ROW_TILES, HID], BF16)
         h_tiles = h0.rearrange("(t p) k -> p t k", p=P)
         nc.sync.dma_start(out=h_rows[:, 0:1, :], in_=h_tiles[:, 0:1, :])
@@ -132,6 +147,9 @@ def tile_multilstm_pa_kernel(
                     out=w_words[:, g, some].bitcast(I32),
                     in_=w_hh1_words[g, :, some].bitcast(I32),
                 )
+            for part in range(2):
+                if GAIN_AT[part] == 1 + half:
+                    load_gain(part)
         nc.sync.dma_start(out=h_rows[:, 1:2, :], in_=h_tiles[:, 1:2, :])
         gain_r = keep.tile([P, GATES], BF16)
         nc.sync.dma_start(out=gain_r[:], in_=lnh_w1.partition_broadcast(P))
@@ -194,8 +212,6 @@ def tile_multilstm_pa_kernel(
             nc.vector.quantize_mx(
                 out=h_codes[:, t, :].bitcast(FP8X4), scales=h_scales[:, t, :], in_=grouped[:]
             )
-
-        gain_a = keep.tile([P, GATES], BF16)
 
         def spread_gain(first):
             spread_ps = (r_bank_tile if SPREAD_TAG == "r" else q_bank_tile)([P, BANK], BF16)
@@ -313,7 +329,8 @@ def tile_multilstm_pa_kernel(
         x_scaled = keep.tile([P, ROW_TILES, IN], F32)
         xsT = keep.tile([P, BATCH], F32)
         def a_bank(t, j):
-            a_ps = q_bank_tile([P, BANK], F32)
+            in_r = LAST_IN_R and t == ROW_TILES - 1 and j in ORDER[Q_SLOTS:BANKS]
+            a_ps = (r_bank_tile if in_r else q_bank_tile)([P, BANK], F32)
             nc.tensor.matmul(
                 a_ps[:],
                 lhsT=xsT[:, t * P : (t + 1) * P],
@@ -496,7 +513,7 @@ def tile_multilstm_pa_kernel(
             step(("WT", q), [], lambda q=q: do_WT(q))
             bank_tag["WT", q] = "q"
             bank_users["WT", q] = [("WC", q)]
-            step(("WC", q), [("WT", q), ("NW",), ("SPC", 2 * q), ("SPC", 2 * q + 1)], lambda q=q: w_centre(q, S["wT", q]))
+            step(("WC", q), [("WT", q), ("NW",)], lambda q=q: w_centre(q, S["wT", q]))
         step(("NW",), [("G", 3)], gram_out)
         for pair in range(ROW_TILES // 2):
             step(("XM", pair), [("NW",)], lambda pair=pair: do_XM(pair))
@@ -566,7 +583,8 @@ def tile_multilstm_pa_kernel(
 
         def do_M2(t):
             gate_i = S["gates", t][:, 0:HID]
-            nc.vector.tensor_tensor(out=gate_i, in0=gate_i, in1=S["gates", t][:, 2 * HID : 3 * HID], op=ALU.mult)
+            engine = nc.gpsimd if M2_POOL[t] else nc.vector
+            engine.tensor_tensor(out=gate_i, in0=gate_i, in1=S["gates", t][:, 2 * HID : 3 * HID], op=ALU.mult)
 
         def do_C(t):
             cy = cell_pool.tile([P, HID], F32)
@@ -642,7 +660,7 @@ def tile_multilstm_pa_kernel(
                 bank_users["R", t, j] = [("P1", t, j)]
                 step(("P1", t, j), [("R", t, j)] + ([("P1", t, 0)] if j else []), lambda t=t, j=j: do_P1(t, j))
                 step(("Q", t, j), [("XC",), ("WC", j // 2)], lambda t=t, j=j: do_Q(t, j))
-                bank_tag["Q", t, j] = "q"
+                bank_tag["Q", t, j] = "r" if (LAST_IN_R and t == ROW_TILES - 1 and j in ORDER[Q_SLOTS:BANKS]) else "q"
                 bank_users["Q", t, j] = [("A2", t, j)]
                 step(("A2", t, j), [("Q", t, j), ("G1", t, j // 4), ("P2", t)], lambda t=t, j=j: do_A2(t, j))
             step(("MEAN", t), [("P1", t, j) for j in range(BANKS)], lambda t=t: do_MEAN(t))
@@ -681,9 +699,9 @@ def tile_multilstm_pa_kernel(
         WC = [("WC", q) for q in range(4)]
         Q0 = [("Q", 0, j) for j in ORDER[0:Q_SLOTS]]
         R1 = [("R", 1, j) for j in range(R_SLOTS)]
-        tensor_q += SP[0:2] + G + [("HT", 0)] + XM + SP[2:4] + WT[0:2] + R0[0:3] + SP[4:8] + WT[2:4] + [("XT",)] + R0[3:8] + [("HT", 1)] + Q0 + R1
-        scalar_q += SPC[0:2] + [("HC", 0)] + SPC[2:4] + P10[0:1] + [("XS",)] + P10[1:3] + [("XC",)] + P10[3:8] + [("MEAN", 0)]
-        vector_q += [("NW",), ("HQ", 0)] + AS + [("AV",)] + WC[0:2] + SPC[4:8] + WC[2:4] + [("HC", 1), ("HQ", 1)]
+        tensor_q += G + [("HT", 0)] + XM + WT[0:2] + R0[0:3] + WT[2:4] + [("XT",)] + R0[3:8] + [("HT", 1)] + Q0 + R1
+        scalar_q += [("HC", 0)] + P10 + [("MEAN", 0)]
+        vector_q += [("NW",), ("HQ", 0)] + AS + [("AV",), ("XS",)] + WC[0:2] + [("XC",)] + WC[2:4] + [("HC", 1), ("HQ", 1)]
         for f in range(ROW_TILES):
             prev = f >= 1
             nxt = f + 1 < ROW_TILES
@@ -698,14 +716,18 @@ def tile_multilstm_pa_kernel(
                 vector_q += [("HY", f - 1, 0)]
             vector_q += a2[HY_AT:8]
             vector_q += p1_dve
+            if nxt2 and HC_EARLY:
+                vector_q += [("HC", f + 2)]
             if not M1_POOL[f]:
                 vector_q += [("M1", f)]
-            vector_q += [("M2", f), ("C", f)]
+            if not M2_POOL[f]:
+                vector_q += [("M2", f)]
+            vector_q += [("C", f)]
             if SQ_DVE:
                 vector_q += [("SQ", f)]
             vector_q += [("V1", f)]
             if nxt2:
-                vector_q += [("HC", f + 2), ("HQ", f + 2)]
+                vector_q += ([] if HC_EARLY else [("HC", f + 2)]) + [("HQ", f + 2)]
             vector_q += [("CY", f)]
 
             scalar_q += [("P2", f)]
@@ -714,17 +736,23 @@ def tile_multilstm_pa_kernel(
                 if HY_POOL[f - 1]:
                     scalar_q += [("HY", f - 1, 0)]
             fs = [("F", f, ORDER[2 * k] // 2) for k in range(4)]
-            scalar_q += p1_act[0:PA] + fs[0:1] + ([("M1", f)] if M1_POOL[f] else []) + p1_act[PA:PB] + fs[1:4]
-            scalar_q += p1_act[PB:PD] + ([] if SQ_DVE else [("SQ", f)]) + p1_act[PD:8]
+            pa = PA if prev else PA0
+            pb = PB if prev else PB0
+            scalar_q += p1_act[0:pa] + fs[0:1] + ([("M1", f)] if M1_POOL[f] else []) + p1_act[pa:pb] + fs[1:3]
+            scalar_q += ([("M2", f)] if M2_POOL[f] else []) + fs[3:4]
+            scalar_q += p1_act[pb:PD] + ([] if SQ_DVE else [("SQ", f)]) + p1_act[PD:8]
             if nxt:
                 scalar_q += [("MEAN", f + 1)]
 
-            tensor_q += [("Q", f, j) for j in ORDER[Q_SLOTS:BANKS]]
+            if nxt or not LAST_IN_R:
+                tensor_q += [("Q", f, j) for j in ORDER[Q_SLOTS:BANKS]]
             if nxt:
                 tensor_q += [("R", f + 1, j) for j in range(R_SLOTS, BANKS)]
                 if nxt2:
                     tensor_q += [("HT", f + 2)]
                 tensor_q += [("Q", f + 1, j) for j in ORDER[0:Q_SLOTS]]
+                if LAST_IN_R and not nxt2:
+                    tensor_q += [("Q", f + 1, j) for j in ORDER[Q_SLOTS:BANKS]]
                 if nxt2:
                     tensor_q += [("R", f + 2, j) for j in range(R_SLOTS)]
         scalar_q += [("TH", ROW_TILES - 1, part) for part in range(LAST_PARTS)]

@@ -37,7 +37,7 @@ H_COPY = ["scalar", "vector", "vector", "vector"]
 XS_ENGINE = "gpsimd"
 XC_ENGINE = "vector"
 M1_POOL = [True] * 4
-HY_POOL = [True, True, True, False]
+HY_POOL = [True, True, False, False]
 SQ_DVE = False
 P1_DVE = []
 ORDER = [2, 3, 0, 1, 4, 5, 6, 7]
@@ -52,7 +52,11 @@ GAIN_AT = [1, 2]
 PA0 = 2
 PB0 = 3
 LAST_IN_R = True
+TAIL = 0
 
+DEFER = True
+HEAD = 0
+VT = 0
 FLOPS = 2 * BATCH * GATES * (HID + IN)
 
 
@@ -541,6 +545,7 @@ def tile_multilstm_pa_kernel(
                     scalar1=1.0,
                     scalar2=None,
                     op0=ALU.mult,
+                    op1=ALU.add,
                     accum_out=S["sums", t][:, j : j + 1],
                 )
             else:
@@ -598,11 +603,14 @@ def tile_multilstm_pa_kernel(
                 op1=ALU.add,
                 accum_out=c_sum[:],
             )
+            S["cy", t] = cy
+            S["c_sum", t] = c_sum
+
+        def do_NM(t):
             c_negmean = stats.tile([P, 1], F32)
             nc.vector.tensor_scalar(
-                out=c_negmean[:], in0=c_sum[:], scalar1=-1.0 / HID, scalar2=None, op0=ALU.mult
+                out=c_negmean[:], in0=S["c_sum", t][:], scalar1=-1.0 / HID, scalar2=None, op0=ALU.mult
             )
-            S["cy", t] = cy
             S["c_negmean", t] = c_negmean
 
         def do_SQ(t):
@@ -677,8 +685,9 @@ def tile_multilstm_pa_kernel(
             step(("M1", t), [("F", t, 1)], lambda t=t: do_M1(t))
             step(("M2", t), [("F", t, 0), ("F", t, 2)], lambda t=t: do_M2(t))
             step(("C", t), [("M1", t), ("M2", t)], lambda t=t: do_C(t))
-            step(("SQ", t), [("C", t)], lambda t=t: do_SQ(t))
-            step(("V1", t), [("C", t)], lambda t=t: do_V1(t))
+            step(("NM", t), [("C", t)], lambda t=t: do_NM(t))
+            step(("SQ", t), [("NM", t)], lambda t=t: do_SQ(t))
+            step(("V1", t), [("NM", t)], lambda t=t: do_V1(t))
             step(("CY", t), [("V1", t), ("SQ", t)], lambda t=t: do_CY(t))
             parts = LAST_PARTS if t == ROW_TILES - 1 else 1
             for part in range(parts):
@@ -690,8 +699,6 @@ def tile_multilstm_pa_kernel(
         vector_q = []
         R0 = [("R", 0, j) for j in range(BANKS)]
         P10 = [("P1", 0, j) for j in range(BANKS)]
-        SP = [("SP", g) for g in range(BANKS)]
-        SPC = [("SPC", g) for g in range(BANKS)]
         G = [("G", q) for q in range(4)]
         XM = [("XM", pair) for pair in range(ROW_TILES // 2)]
         AS = [("AS", t) for t in range(ROW_TILES)]
@@ -699,48 +706,57 @@ def tile_multilstm_pa_kernel(
         WC = [("WC", q) for q in range(4)]
         Q0 = [("Q", 0, j) for j in ORDER[0:Q_SLOTS]]
         R1 = [("R", 1, j) for j in range(R_SLOTS)]
-        tensor_q += G + [("HT", 0)] + XM + WT[0:2] + R0[0:3] + WT[2:4] + [("XT",)] + R0[3:8] + [("HT", 1)] + Q0 + R1
+        if HEAD == 0:
+            tensor_q += G + [("HT", 0)] + XM + WT[0:2] + R0[0:3] + WT[2:4] + [("XT",)] + R0[3:8] + [("HT", 1)] + Q0 + R1
+        else:
+            tensor_q += G + [("HT", 0)] + XM + WT[0:2] + R0[0:3] + WT[2:4] + [("XT",)] + R0[3:8] + [("HT", 1)] + R1 + Q0
         scalar_q += [("HC", 0)] + P10 + [("MEAN", 0)]
         vector_q += [("NW",), ("HQ", 0)] + AS + [("AV",), ("XS",)] + WC[0:2] + [("XC",)] + WC[2:4] + [("HC", 1), ("HQ", 1)]
+        LAST = ROW_TILES - 1
         for f in range(ROW_TILES):
             prev = f >= 1
             nxt = f + 1 < ROW_TILES
             nxt2 = f + 2 < ROW_TILES
+            late = DEFER and f == LAST - 1
+            after_late = DEFER and f == LAST
             a2 = [("A2", f, j) for j in ORDER]
             p1 = [("P1", f + 1, j) for j in range(BANKS)] if nxt else []
             p1_act = [s for s in p1 if s[2] not in P1_DVE]
             p1_dve = [s for s in p1 if s[2] in P1_DVE]
             vector_q += [("G1", f, 0), ("G1", f, 1)]
-            vector_q += a2[0:HY_AT]
-            if prev and not HY_POOL[f - 1]:
-                vector_q += [("HY", f - 1, 0)]
-            vector_q += a2[HY_AT:8]
-            vector_q += p1_dve
-            if nxt2 and HC_EARLY:
-                vector_q += [("HC", f + 2)]
-            if not M1_POOL[f]:
-                vector_q += [("M1", f)]
-            if not M2_POOL[f]:
-                vector_q += [("M2", f)]
-            vector_q += [("C", f)]
-            if SQ_DVE:
-                vector_q += [("SQ", f)]
-            vector_q += [("V1", f)]
-            if nxt2:
-                vector_q += ([] if HC_EARLY else [("HC", f + 2)]) + [("HQ", f + 2)]
-            vector_q += [("CY", f)]
+            vector_q += a2
+            hc = [("HC", f + 2)] if nxt2 else []
+            hq = [("HQ", f + 2)] if nxt2 else []
+            m2 = [] if M2_POOL[f] else [("M2", f)]
+            if after_late:
+                vector_q += m2 + [("C", f), ("NM", f), ("CY", f - 1), ("V1", f), ("CY", f), ("HY", f - 1, 0)]
+            elif late:
+                vector_q += p1_dve + m2 + [("C", f), ("NM", f), ("V1", f)]
+            elif VT == 0:
+                vector_q += p1_dve + m2 + [("C", f), ("NM", f), ("V1", f)] + hc + hq + [("CY", f)]
+            elif VT == 1:
+                vector_q += p1_dve + hc + m2 + [("C", f), ("NM", f), ("V1", f)] + hq + [("CY", f)]
+            elif VT == 2:
+                vector_q += p1_dve + hc + m2 + [("C", f)] + hq + [("NM", f), ("V1", f)] + [("CY", f)]
 
             scalar_q += [("P2", f)]
-            if prev:
+            if after_late:
+                scalar_q += [("SQ", f - 1), ("F", f - 1, 3)]
+            elif prev:
                 scalar_q += [("TH", f - 1, 0)]
                 if HY_POOL[f - 1]:
                     scalar_q += [("HY", f - 1, 0)]
             fs = [("F", f, ORDER[2 * k] // 2) for k in range(4)]
             pa = PA if prev else PA0
             pb = PB if prev else PB0
-            scalar_q += p1_act[0:pa] + fs[0:1] + ([("M1", f)] if M1_POOL[f] else []) + p1_act[pa:pb] + fs[1:3]
-            scalar_q += ([("M2", f)] if M2_POOL[f] else []) + fs[3:4]
-            scalar_q += p1_act[pb:PD] + ([] if SQ_DVE else [("SQ", f)]) + p1_act[PD:8]
+            scalar_q += p1_act[0:pa] + fs[0:1] + [("M1", f)] + p1_act[pa:pb] + fs[1:3] + ([("M2", f)] if M2_POOL[f] else [])
+            if late:
+                scalar_q += p1_act[pb:8]
+            else:
+                scalar_q += fs[3:4]
+                scalar_q += p1_act[pb:PD] + [("SQ", f)] + p1_act[PD:8]
+            if after_late:
+                scalar_q += [("TH", f - 1, 0)]
             if nxt:
                 scalar_q += [("MEAN", f + 1)]
 

@@ -19,7 +19,7 @@ IN = 128
 HID = 1024
 GATES = 4 * HID
 EPS = 1e-5
-ROW_TILES = BATCH // P
+TILES = BATCH // P
 BANK = 512
 BANKS = GATES // BANK
 BLOCKS = GATES // P
@@ -27,37 +27,65 @@ PER_BANK = BANK // P
 K_PASS = 512
 PASSES = HID // K_PASS
 ONES = 2
-W_ROW = IN + 16
-QUARTER = BLOCKS // 4
 R_SLOTS = 3
 Q_SLOTS = 5
-SPREAD_TAG = "q"
-SPREAD_COPY = ["scalar"] * 4 + ["vector"] * 4
-H_COPY = ["scalar", "vector", "vector", "vector"]
-XS_ENGINE = "gpsimd"
-XC_ENGINE = "vector"
-M1_POOL = [True] * 4
-HY_POOL = [True, True, False, False]
-SQ_DVE = False
-P1_DVE = []
 ORDER = [2, 3, 0, 1, 4, 5, 6, 7]
-HY_AT = 2
-PA = 2
-PB = 3
-PD = 6
+FIG = ORDER[0:6]
+GROUPS = [[0], [1, 2, 3]]
+WPARTS = 4
 LAST_PARTS = 2
-M2_POOL = [False] * 4
-HC_EARLY = False
-GAIN_AT = [1, 2]
-PA0 = 2
-PB0 = 3
-LAST_IN_R = True
-TAIL = 0
-
-DEFER = True
-HEAD = 0
-VT = 0
+HY_POOL = [True, True, False, False]
+HC_ON = ["scalar", "vector", "vector", "vector"]
 FLOPS = 2 * BATCH * GATES * (HID + IN)
+
+LOADS = [("h", 0), ("x",), ("w", 0), ("w", 1), ("w", 2), ("w", 3), ("scales",), ("words", 0), ("bias",), ("gain_a", 0), ("words", 1), ("words", 2), ("gain_a", 1), ("words", 3), ("h", 1), ("gain_r", 0), ("gain_r", 1), ("h23",), ("c",), ("gain_c",), ("bias_c",)]
+
+
+def R(t, a, b):
+    return [("R", t, j) for j in range(a, b)]
+
+
+def P1(t, a, b):
+    return [("P1", t, j) for j in range(a, b)]
+
+
+def Q(t, *js):
+    return [("Q", t, j) for j in js]
+
+
+def A2(t, *js):
+    return [("A2", t, j) for j in js]
+
+
+def F(t, *gs):
+    return [("F", t, g) for g in gs]
+
+
+G4 = [("G", 0), ("G", 1), ("G", 2), ("G", 3)]
+T_LIST = (
+    [("HT", 0), ("XT0",)] + G4 + [("WT", 1), ("XM", 0)] + R(0, 0, 4) + [("XM", 1)] + R(0, 4, 8)
+    + [("HT", 1), ("XT", 0), ("VEC",), ("WT", 0), ("WT", 2), ("WT", 3)]
+    + R(1, 0, 1) + Q(0, 2) + R(1, 1, 3) + Q(0, 3) + R(1, 3, 5) + Q(0, 0) + R(1, 5, 8) + Q(0, 1) + [("HT", 2), ("HT", 3)] + Q(0, 4) + [("XT", 1)] + Q(0, 5)
+    + R(2, 0, 3) + Q(1, 2) + R(2, 3, 6) + Q(1, 3, 0) + R(2, 6, 8) + Q(1, 1) + R(3, 0, 1) + Q(1, 4, 5) + R(3, 1, 2) + Q(0, 6, 7)
+    + R(3, 2, 4) + Q(2, 2, 3) + R(3, 4, 6) + Q(2, 0) + R(3, 6, 8) + Q(2, 1, 4, 5)
+    + Q(3, *FIG) + Q(1, 6, 7) + Q(2, 6, 7) + Q(3, 6, 7)
+)
+S_LIST = (
+    [("HC", 0)] + P1(0, 0, 8) + [("MEAN", 0), ("P2", 0)] + P1(1, 0, 5) + F(0, 1) + P1(1, 5, 8) + [("MEAN", 1), ("P2", 1)]
+    + P1(2, 0, 3) + F(0, 0) + P1(2, 3, 5) + F(0, 2) + P1(2, 5, 8) + [("MEAN", 2), ("P2", 2), ("SQ", 0)]
+    + F(1, 1) + P1(3, 0, 1) + F(1, 0) + P1(3, 1, 2) + F(1, 2) + P1(3, 2, 4) + F(0, 3) + P1(3, 4, 8) + [("MEAN", 3), ("SQ", 1), ("TH", 0, 0), ("P2", 3)]
+    + F(2, 1, 0, 2) + F(3, 1, 0, 2) + [("SQ", 2)] + F(1, 3) + [("TH", 1, 0), ("SQ", 3), ("TH", 2, 0)] + F(2, 3) + F(3, 3) + [("TH", 3, 0), ("TH", 3, 1)]
+)
+V_LIST = (
+    [("HQ", 0), ("XC0",), ("NW",), ("AS", 0), ("AV", 0), ("WC", 1), ("XS", 0), ("AS", 1), ("AV", 1), ("HC", 1), ("HQ", 1), ("XC", 0), ("VECC",), ("WC", 0)]
+    + [("G1", 0, 0), ("WC", 2)] + A2(0, 2, 3) + [("WC", 3), ("G1", 0, 1)] + A2(0, 0) + [("HC", 2), ("HC", 3), ("XS", 1)] + A2(0, 1) + [("HQ", 2), ("HQ", 3), ("XC", 1)] + A2(0, 4)
+    + [("G1", 1, 0)] + A2(0, 5) + [("G1", 1, 1)]
+    + A2(1, 2) + [("M2", 0)] + A2(1, 3) + [("C", 0)] + A2(1, 0) + [("NM", 0), ("G1", 2, 0), ("V1", 0)] + A2(1, 1, 4, 5) + [("G1", 2, 1)] + A2(0, 6, 7) + [("CY", 0)]
+    + [("M2", 1)] + A2(2, 2) + [("C", 1)] + A2(2, 3) + [("NM", 1)] + A2(2, 0) + [("V1", 1), ("G1", 3, 0)] + A2(2, 1, 4, 5) + [("G1", 3, 1), ("CY", 1)]
+    + A2(3, 2, 3) + [("M2", 2)] + A2(3, 0, 1) + [("C", 2)] + A2(3, 4, 5) + [("NM", 2)] + A2(1, 6, 7) + [("M2", 3)] + A2(2, 6) + [("V1", 2), ("C", 3)] + A2(2, 7) + [("NM", 3), ("CY", 2), ("V1", 3)] + A2(3, 6, 7)
+    + [("CY", 3), ("HY", 2, 0), ("HY", 3, 0), ("HY", 3, 1)]
+)
+G_LIST = [("PW", 0), ("PW", 1), ("RS", 0), ("RS", 1), ("M1", 0), ("RS", 2), ("RC", 0), ("M1", 1), ("HY", 0, 0), ("RC", 1), ("RS", 3), ("M1", 2), ("M1", 3), ("RC", 2), ("HY", 1, 0), ("RC", 3)]
 
 
 def tile_multilstm_pa_kernel(
@@ -83,112 +111,135 @@ def tile_multilstm_pa_kernel(
         keep = stack.enter_context(tc.tile_pool(name="keep", bufs=1))
         stage = stack.enter_context(tc.tile_pool(name="stage", bufs=2))
         r_pool = stack.enter_context(tc.tile_pool(name="r_pool", bufs=2))
-        gate_pool = stack.enter_context(tc.tile_pool(name="gate_pool", bufs=2))
-        cell_pool = stack.enter_context(tc.tile_pool(name="cell_pool", bufs=2))
-        stats = stack.enter_context(tc.tile_pool(name="stats", bufs=4))
+        gate_pool = stack.enter_context(tc.tile_pool(name="gate_pool", bufs=TILES))
+        stats = stack.enter_context(tc.tile_pool(name="stats", bufs=2 * TILES))
         psum = stack.enter_context(tc.psum_pool(name="psum", bufs=1))
 
-        def r_bank_tile(shape, dtype):
+        def r_bank(shape, dtype):
             r_slot = psum.tile(shape, dtype, tag="r", bufs=R_SLOTS)
             return r_slot
 
-        def q_bank_tile(shape, dtype):
+        def q_bank(shape, dtype):
             q_slot = psum.tile(shape, dtype, tag="q", bufs=Q_SLOTS)
             return q_slot
 
         w_scales = keep.tile([P, PASSES, GATES], U8, align_bytes=64)
         nc.vector.memset(w_scales[:].rearrange("p g n -> p (g n)").bitcast(I32), 0)
-        ident_bf = keep.tile([P, P], BF16)
-        make_identity(nc, ident_bf[:])
         ident_f32 = keep.tile([P, P], F32)
         make_identity(nc, ident_f32[:])
-        neg_half = keep.tile([P, ROW_TILES], F32)
+        ident_bf = keep.tile([P, P], BF16)
+        make_identity(nc, ident_bf[:])
+        neg_half = keep.tile([P, TILES], F32)
         nc.gpsimd.memset(neg_half[:], -0.5)
-
         gate_vecs = keep.tile([P, P], BF16)
-        nc.vector.memset(gate_vecs[3 * BLOCKS : P, :], 0.0)
-        for i, vec in enumerate((lni_w1, lni_b1, lnh_b1)):
-            nc.sync.dma_start(
-                out=gate_vecs[BLOCKS * i : BLOCKS * (i + 1), :],
-                in_=vec.rearrange("(j p) -> j p", p=P),
-            )
+        nc.vector.memset(gate_vecs[2 * BLOCKS : P, :], 0.0)
         warm = keep.tile([P, 1], F32)
         nc.vector.memset(warm[:], 0.0)
         nc.scalar.activation(out=warm[:], in_=warm[:], func=ACT.Sigmoid)
+        ones = keep.tile([P, ONES], BF16)
+        nc.vector.memset(ones[:], 1.0)
 
-        x_rows = keep.tile([P, ROW_TILES, IN], BF16)
-        nc.sync.dma_start(out=x_rows[:], in_=x.rearrange("(t p) v -> p t v", p=P))
-        w_rows = keep.tile([P, BLOCKS, W_ROW], BF16)
-        nc.vector.memset(w_rows[:, :, IN:W_ROW], 1.0)
-        w_blocks = w_ih1.rearrange("(j p) v -> p j v", p=P)
-        for first in range(0, BLOCKS, QUARTER):
-            some = slice(first, first + QUARTER)
-            nc.sync.dma_start(out=w_rows[:, some, 0:IN], in_=w_blocks[:, some, :])
+        x_rows = keep.tile([P, TILES, IN], BF16)
+        w_rows = keep.tile([P, BANKS, PER_BANK, IN], BF16)
+        w_banks = w_ih1.rearrange("(b p t) v -> p b t v", p=P, t=PER_BANK)
         gain_a = keep.tile([P, GATES], BF16)
-
-        def load_gain(part):
-            cols = slice(part * GATES // 2, (part + 1) * GATES // 2)
-            nc.sync.dma_start(out=gain_a[:, cols], in_=lni_w1[cols].partition_broadcast(P))
-
-        for part in range(2):
-            if GAIN_AT[part] == 0:
-                load_gain(part)
-        h_rows = keep.tile([P, ROW_TILES, HID], BF16)
-        h_tiles = h0.rearrange("(t p) k -> p t k", p=P)
-        nc.sync.dma_start(out=h_rows[:, 0:1, :], in_=h_tiles[:, 0:1, :])
-        for g in range(PASSES):
-            for b in range(2):
-                for r in range(4):
-                    nc.sync.dma_start(
-                        out=w_scales[32 * b + r : P : 64, g, :].bitcast(I32),
-                        in_=w_hh1_scales[g, 4 * b + r : 16 : 8, :].bitcast(I32),
-                    )
+        h_rows = keep.tile([P, TILES, HID], BF16)
+        h_tiles = h0.rearrange("(p t) k -> p t k", t=TILES)
         w_words = keep.tile([P, PASSES, 2 * GATES], U8, align_bytes=64)
-        for half in range(2):
-            some = slice(half * GATES, (half + 1) * GATES)
-            for g in range(PASSES):
-                nc.sync.dma_start(
-                    out=w_words[:, g, some].bitcast(I32),
-                    in_=w_hh1_words[g, :, some].bitcast(I32),
-                )
-            for part in range(2):
-                if GAIN_AT[part] == 1 + half:
-                    load_gain(part)
-        nc.sync.dma_start(out=h_rows[:, 1:2, :], in_=h_tiles[:, 1:2, :])
         gain_r = keep.tile([P, GATES], BF16)
-        nc.sync.dma_start(out=gain_r[:], in_=lnh_w1.partition_broadcast(P))
-        nc.sync.dma_start(out=h_rows[:, 2:ROW_TILES, :], in_=h_tiles[:, 2:ROW_TILES, :])
-        c_rows = keep.tile([P, ROW_TILES, HID], BF16)
-        nc.sync.dma_start(out=c_rows[:], in_=c0.rearrange("(t p) k -> p t k", p=P))
+        c_rows = keep.tile([P, TILES, HID], BF16)
         gain_c = keep.tile([P, HID], BF16)
-        nc.sync.dma_start(out=gain_c[:], in_=lnc_w1.partition_broadcast(P))
         bias_c = keep.tile([P, HID], BF16)
-        nc.sync.dma_start(out=bias_c[:], in_=lnc_b1.partition_broadcast(P))
+        hy_tiles = out_0.rearrange("(p t) k -> p t k", t=TILES)
+        cy_tiles = out_1.rearrange("(p t) k -> p t k", t=TILES)
 
-        vec_ps = r_bank_tile([P, P], BF16)
-        nc.tensor.transpose(vec_ps[:], gate_vecs[:], ident_bf[:])
+        def load(what, i=0):
+            dma = nc.sync.dma_start
+            if what == "bias":
+                for n, vec in enumerate((lni_b1, lnh_b1)):
+                    dma(out=gate_vecs[BLOCKS * n : BLOCKS * (n + 1), :], in_=vec.rearrange("(j p) -> j p", p=P))
+            elif what == "x":
+                dma(out=x_rows[:], in_=x.rearrange("(p t) v -> p t v", t=TILES))
+            elif what == "w":
+                dma(out=w_rows[:, 2 * i : 2 * i + 2, :, :], in_=w_banks[:, 2 * i : 2 * i + 2, :, :])
+            elif what == "h":
+                dma(out=h_rows[:, i : i + 1, :], in_=h_tiles[:, i : i + 1, :])
+            elif what == "h23":
+                dma(out=h_rows[:, 2:4, :], in_=h_tiles[:, 2:4, :])
+            elif what == "scales":
+                for r in range(4):
+                    dma(
+                        out=w_scales[r:P:32, :, :].bitcast(I32),
+                        in_=w_hh1_scales[:, r:16:4, :].rearrange("g q n -> q g n").bitcast(I32),
+                    )
+            elif what == "words":
+                n = 2 * GATES // WPARTS
+                some = slice(i * n, (i + 1) * n)
+                for g in range(PASSES):
+                    dma(out=w_words[:, g, some].bitcast(I32), in_=w_hh1_words[g, :, some].bitcast(I32))
+            elif what == "gain_a":
+                cols = slice(i * GATES // 2, (i + 1) * GATES // 2)
+                dma(out=gain_a[:, cols], in_=lni_w1[cols].partition_broadcast(P))
+            elif what == "gain_r":
+                cols = slice(i * GATES // 2, (i + 1) * GATES // 2)
+                dma(out=gain_r[:, cols], in_=lnh_w1[cols].partition_broadcast(P))
+            elif what == "c":
+                dma(out=c_rows[:], in_=c0.rearrange("(p t) k -> p t k", t=TILES))
+            elif what == "gain_c":
+                dma(out=gain_c[:], in_=lnc_w1.partition_broadcast(P))
+            elif what == "bias_c":
+                dma(out=bias_c[:], in_=lnc_b1.partition_broadcast(P))
+
+        for name in LOADS:
+            load(*name)
+
+        S = {}
+        ops = {}
+        bank_tag = {}
+        bank_users = {}
+
+        def step(name, deps, what, bank=None, users=()):
+            ops[name] = (what, deps)
+            if bank is not None:
+                bank_tag[name] = bank
+                bank_users[name] = list(users)
+
         vec_cols = keep.tile([P, P], BF16)
-        nc.vector.tensor_copy(out=vec_cols[:], in_=vec_ps[:])
         bias_cols = keep.tile([P, BLOCKS], F32)
-        nc.vector.tensor_tensor(
-            out=bias_cols[:],
-            in0=vec_cols[:, BLOCKS : 2 * BLOCKS],
-            in1=vec_cols[:, 2 * BLOCKS : 3 * BLOCKS],
-            op=ALU.add,
-        )
-        xT_ps = r_bank_tile([P, BATCH], BF16)
-        for t in range(ROW_TILES):
-            nc.tensor.transpose(xT_ps[:, t * P : (t + 1) * P], x_rows[:, t, :], ident_bf[:])
         xT_f32 = keep.tile([P, BATCH], F32)
-        nc.vector.tensor_copy(out=xT_f32[:], in_=xT_ps[:])
 
-        h_codes = keep.tile([P, ROW_TILES, PASSES * P], U32, align_bytes=64)
-        h_scales = keep.tile([P, ROW_TILES, PASSES * P], U8, align_bytes=64)
+        def do_VEC():
+            vec_ps = r_bank([P, P], BF16)
+            nc.tensor.transpose(vec_ps[:], gate_vecs[:], ident_bf[:])
+            S["vec"] = vec_ps
+
+        def do_VECC():
+            nc.vector.tensor_copy(out=vec_cols[:], in_=S["vec"][:])
+            nc.vector.tensor_tensor(
+                out=bias_cols[:], in0=vec_cols[:, 0:BLOCKS], in1=vec_cols[:, BLOCKS : 2 * BLOCKS], op=ALU.add
+            )
+
+        def do_XT0():
+            xT_ps = r_bank([P, BATCH], BF16)
+            for t in range(TILES):
+                nc.tensor.transpose(xT_ps[:, t * P : (t + 1) * P], x_rows[:, t, :], ident_bf[:])
+            S["xT"] = xT_ps
+
+        def do_XC0():
+            nc.vector.tensor_copy(out=xT_f32[:], in_=S["xT"][:])
+
+        step(("VEC",), [], do_VEC, "r", [("VECC",)])
+        step(("VECC",), [("VEC",)], do_VECC)
+        step(("XT0",), [], do_XT0, "r", [("XC0",)])
+        step(("XC0",), [("XT0",)], do_XC0)
+
+        h_codes = keep.tile([P, TILES, PASSES * P], U32, align_bytes=64)
+        h_scales = keep.tile([P, TILES, PASSES * P], U8, align_bytes=64)
         pass_words = K_PASS // 2
 
-        def h0_turn(t):
+        def do_HT(t):
             h_words = h_rows[:, t, :].bitcast(F32)
-            hT_ps = r_bank_tile([P, PASSES, 2, P], F32)
+            hT_ps = r_bank([P, PASSES, 2, P], F32)
             for g in range(PASSES):
                 for u in range(2):
                     nc.tensor.transpose(
@@ -196,145 +247,236 @@ def tile_multilstm_pa_kernel(
                         h_words[:, pass_words * g + u : pass_words * (g + 1) : 2],
                         ident_f32[:],
                     )
-            return hT_ps
+            S["hT", t] = hT_ps
 
-        def h0_group(hT_ps, engine):
+        def do_HC(t):
             grouped = stage.tile([P, PASSES * P * 4], BF16, align_bytes=64)
-            if engine == "scalar":
-                nc.scalar.copy(
-                    out=grouped[:].bitcast(F32).rearrange("p (g b u) -> p g b u", g=PASSES, u=2),
-                    in_=hT_ps[:].rearrange("p g u b -> p g b u"),
-                )
+            out = grouped[:].bitcast(F32).rearrange("p (g b u) -> p g b u", g=PASSES, u=2)
+            hT = S["hT", t][:].rearrange("p g u b -> p g b u")
+            if HC_ON[t] == "scalar":
+                nc.scalar.copy(out=out, in_=hT)
             else:
-                nc.vector.tensor_copy(
-                    out=grouped[:].bitcast(F32).rearrange("p (g b u) -> p g b u", g=PASSES, u=2),
-                    in_=hT_ps[:].rearrange("p g u b -> p g b u"),
-                )
-            return grouped
+                nc.vector.tensor_copy(out=out, in_=hT)
+            S["grouped", t] = grouped
 
-        def h0_quantize(t, grouped):
+        def do_HQ(t):
             nc.vector.quantize_mx(
-                out=h_codes[:, t, :].bitcast(FP8X4), scales=h_scales[:, t, :], in_=grouped[:]
+                out=h_codes[:, t, :].bitcast(FP8X4), scales=h_scales[:, t, :], in_=S["grouped", t][:]
             )
 
-        def spread_gain(first):
-            spread_ps = (r_bank_tile if SPREAD_TAG == "r" else q_bank_tile)([P, BANK], BF16)
-            for k in range(PER_BANK):
-                nc.tensor.transpose(
-                    spread_ps[:, k * P : (k + 1) * P],
-                    vec_cols[:, first + k : first + k + 1].to_broadcast([P, P]),
-                    ident_bf[:],
-                )
-            return spread_ps
-
-        def spread_out(first, spread_ps, engine):
-            if engine == "scalar":
-                nc.scalar.copy(out=gain_a[:, first * P : (first + PER_BANK) * P], in_=spread_ps[:])
-            else:
-                nc.vector.tensor_copy(out=gain_a[:, first * P : (first + PER_BANK) * P], in_=spread_ps[:])
-
-        gram_ps = q_bank_tile([P, IN + ONES], F32)
-
-        def gram_quarter(first):
-            for j in range(first, first + QUARTER):
-                nc.tensor.matmul(
-                    gram_ps[:],
-                    lhsT=w_rows[:, j, 0:IN],
-                    rhs=w_rows[:, j, 0 : IN + ONES],
-                    start=(j == 0),
-                    stop=(j == BLOCKS - 1),
-                )
+        for t in range(TILES):
+            step(("HT", t), [], lambda t=t: do_HT(t), "r", [("HC", t)])
+            step(("HC", t), [("HT", t)], lambda t=t: do_HC(t))
+            step(("HQ", t), [("HC", t)], lambda t=t: do_HQ(t))
 
         neg_wmean = keep.tile([P, 1], F32)
         gram = keep.tile([P, IN + ONES], F32)
 
-        def gram_out():
+        def do_G(q):
+            if q == 0:
+                gram_ps = q_bank([P, IN], F32)
+                wsum_ps = q_bank([P, ONES], F32)
+                S["gram"] = gram_ps
+                S["wsum"] = wsum_ps
+            for b in range(2 * q, 2 * q + 2):
+                for k in range(PER_BANK):
+                    block = w_rows[:, b, k, :]
+                    first = b == 0 and k == 0
+                    last = b == BANKS - 1 and k == PER_BANK - 1
+                    nc.tensor.matmul(S["gram"][:], lhsT=block, rhs=block, start=first, stop=last)
+                    nc.tensor.matmul(S["wsum"][:], lhsT=block, rhs=ones[:], start=first, stop=last)
+
+        def do_NW():
             nc.vector.tensor_scalar(
-                out=neg_wmean[:],
-                in0=gram_ps[:, IN : IN + 1],
-                scalar1=-1.0 / GATES,
-                scalar2=None,
-                op0=ALU.mult,
+                out=neg_wmean[:], in0=S["wsum"][:, 0:1], scalar1=-1.0 / GATES, scalar2=None, op0=ALU.mult
             )
-            nc.vector.tensor_copy(out=gram[:], in_=gram_ps[:])
+            nc.vector.tensor_copy(out=gram[:, 0:IN], in_=S["gram"][:])
+            nc.vector.tensor_copy(out=gram[:, IN : IN + ONES], in_=S["wsum"][:])
+
+        for q in range(4):
+            step(("G", q), [("G", q - 1)] if q else [], lambda q=q: do_G(q))
+        bank_tag["G", 0] = "q"
+        bank_users["G", 0] = [("NW",)]
+        step(("NW",), [("G", 3)], do_NW)
 
         wcT = keep.tile([P, GATES], F32)
 
-        def w_turn(q):
-            wT_ps = q_bank_tile([P, 2 * BANK], BF16)
-            for k in range(QUARTER):
+        def do_WT(q):
+            wT_ps = q_bank([P, 2 * BANK], BF16)
+            for k in range(2 * PER_BANK):
                 nc.tensor.transpose(
-                    wT_ps[:, k * P : (k + 1) * P], w_rows[:, q * QUARTER + k, 0:IN], ident_bf[:]
+                    wT_ps[:, k * P : (k + 1) * P], w_rows[:, 2 * q + k // PER_BANK, k % PER_BANK, :], ident_bf[:]
                 )
-            return wT_ps
+            S["wT", q] = wT_ps
 
-        def w_centre(q, wT_ps):
-            cols = slice(q * 2 * BANK, (q + 1) * 2 * BANK)
-            nc.vector.scalar_tensor_tensor(
-                out=wcT[:, cols],
-                in0=wT_ps[:],
-                scalar=neg_wmean[:],
-                in1=gain_a[:, cols],
-                op0=ALU.add,
-                op1=ALU.mult,
-            )
+        def do_WC(q):
+            for b in range(2):
+                cols = slice((2 * q + b) * BANK, (2 * q + b + 1) * BANK)
+                nc.vector.scalar_tensor_tensor(
+                    out=wcT[:, cols].rearrange("v (p t) -> v p t", t=PER_BANK),
+                    in0=S["wT", q][:, b * BANK : (b + 1) * BANK].rearrange("v (t p) -> v p t", t=PER_BANK),
+                    scalar=neg_wmean[:],
+                    in1=gain_a[:, cols].rearrange("v (p t) -> v p t", t=PER_BANK),
+                    op0=ALU.add,
+                    op1=ALU.mult,
+                )
 
-        a_negmean = keep.tile([P, ROW_TILES], F32)
-        a_sumsq = keep.tile([P, ROW_TILES], F32)
+        for q in range(4):
+            step(("WT", q), [], lambda q=q: do_WT(q), "q", [("WC", q)])
+            step(("WC", q), [("WT", q), ("NW",)], lambda q=q: do_WC(q))
 
-        def a_sums_mm(pair):
-            xm_ps = r_bank_tile([P, 2, IN + ONES], F32)
-            for i in range(2):
-                t = 2 * pair + i
+        a_negmean = keep.tile([P, TILES], F32)
+        a_sumsq = keep.tile([P, TILES], F32)
+        a_meansq = keep.tile([P, TILES], F32)
+        a_var = keep.tile([P, TILES], F32)
+        a_rstd = keep.tile([P, TILES], F32)
+        x_scaled = keep.tile([P, TILES, IN], F32)
+        xsT = keep.tile([P, BATCH], F32)
+
+        def do_XM(i):
+            xm_ps = r_bank([P, len(GROUPS[i]), IN + ONES], F32)
+            for n, t in enumerate(GROUPS[i]):
                 nc.tensor.matmul(
-                    xm_ps[:, i, :], lhsT=xT_f32[:, t * P : (t + 1) * P], rhs=gram[:], start=True, stop=True
+                    xm_ps[:, n, :], lhsT=xT_f32[:, t * P : (t + 1) * P], rhs=gram[:], start=True, stop=True
                 )
-            return xm_ps
+            S["xm", i] = xm_ps
 
-        def a_sums(t, xm_pair):
-            xm_ps = xm_pair[:, t % 2, :]
-            products = stage.tile([P, IN], F32)
-            nc.vector.scalar_tensor_tensor(
-                out=products[:],
-                in0=xm_ps[:, 0:IN],
-                scalar=1.0,
-                in1=x_rows[:, t, :],
-                op0=ALU.mult,
-                op1=ALU.mult,
-                accum_out=a_sumsq[:, t : t + 1],
-            )
+        def some(i):
+            return slice(GROUPS[i][0], GROUPS[i][-1] + 1)
+
+        def do_AS(i):
+            for n, t in enumerate(GROUPS[i]):
+                products = stage.tile([P, IN], F32)
+                nc.vector.scalar_tensor_tensor(
+                    out=products[:],
+                    in0=S["xm", i][:, n, 0:IN],
+                    scalar=1.0,
+                    in1=x_rows[:, t, :],
+                    op0=ALU.mult,
+                    op1=ALU.mult,
+                    accum_out=a_sumsq[:, t : t + 1],
+                )
             nc.vector.tensor_scalar(
-                out=a_negmean[:, t : t + 1],
-                in0=xm_ps[:, IN : IN + 1],
-                scalar1=-1.0 / GATES,
-                scalar2=None,
-                op0=ALU.mult,
+                out=a_negmean[:, some(i)], in0=S["xm", i][:, :, IN], scalar1=-1.0 / GATES, scalar2=None, op0=ALU.mult
             )
 
-        a_meansq = keep.tile([P, ROW_TILES], F32)
-        a_var = keep.tile([P, ROW_TILES], F32)
-        a_rstd = keep.tile([P, ROW_TILES], F32)
-
-        def a_spread():
-            nc.vector.tensor_tensor(out=a_meansq[:], in0=a_negmean[:], in1=a_negmean[:], op=ALU.mult)
+        def do_AV(i):
+            nc.vector.tensor_tensor(
+                out=a_meansq[:, some(i)], in0=a_negmean[:, some(i)], in1=a_negmean[:, some(i)], op=ALU.mult
+            )
             nc.vector.scalar_tensor_tensor(
-                out=a_var[:],
-                in0=a_sumsq[:],
+                out=a_var[:, some(i)],
+                in0=a_sumsq[:, some(i)],
                 scalar=1.0 / GATES,
-                in1=a_meansq[:],
+                in1=a_meansq[:, some(i)],
                 op0=ALU.mult,
                 op1=ALU.subtract,
             )
             nc.vector.tensor_scalar(
-                out=a_var[:], in0=a_var[:], scalar1=EPS, scalar2=None, op0=ALU.add
+                out=a_var[:, some(i)], in0=a_var[:, some(i)], scalar1=EPS, scalar2=None, op0=ALU.add
             )
-            nc.gpsimd.tensor_tensor(out=a_rstd[:], in0=a_var[:], in1=neg_half[:], op=ALU.pow)
 
-        x_scaled = keep.tile([P, ROW_TILES, IN], F32)
-        xsT = keep.tile([P, BATCH], F32)
-        def a_bank(t, j):
-            in_r = LAST_IN_R and t == ROW_TILES - 1 and j in ORDER[Q_SLOTS:BANKS]
-            a_ps = (r_bank_tile if in_r else q_bank_tile)([P, BANK], F32)
+        def do_PW(i):
+            nc.gpsimd.tensor_tensor(
+                out=a_rstd[:, some(i)], in0=a_var[:, some(i)], in1=neg_half[:, some(i)], op=ALU.pow
+            )
+
+        def do_XS(i):
+            for t in GROUPS[i]:
+                nc.vector.tensor_scalar(
+                    out=x_scaled[:, t, :], in0=x_rows[:, t, :], scalar1=a_rstd[:, t : t + 1], scalar2=None, op0=ALU.mult
+                )
+
+        def do_XT(i):
+            xsT_ps = r_bank([P, len(GROUPS[i]), P], F32)
+            for n, t in enumerate(GROUPS[i]):
+                nc.tensor.transpose(xsT_ps[:, n, :], x_scaled[:, t, :], ident_f32[:])
+            S["xsT", i] = xsT_ps
+
+        def do_XC(i):
+            out = xsT[:, GROUPS[i][0] * P : (GROUPS[i][-1] + 1) * P]
+            nc.vector.tensor_copy(out=out, in_=S["xsT", i][:].rearrange("p t b -> p (t b)"))
+
+        for i in range(2):
+            step(("XM", i), [("NW",), ("XC0",)], lambda i=i: do_XM(i), "r", [("AS", i)])
+            step(("AS", i), [("XM", i)], lambda i=i: do_AS(i))
+            step(("AV", i), [("AS", i)], lambda i=i: do_AV(i))
+            step(("PW", i), [("AV", i)], lambda i=i: do_PW(i))
+            step(("XS", i), [("PW", i)], lambda i=i: do_XS(i))
+            step(("XT", i), [("XS", i)], lambda i=i: do_XT(i), "r", [("XC", i)])
+            step(("XC", i), [("XT", i)], lambda i=i: do_XC(i))
+
+        def do_R(t, j):
+            r_ps = r_bank([P, BANK], F32)
+            for g in range(PASSES):
+                nc.tensor.matmul_mx(
+                    out=r_ps[:],
+                    lhsT=h_codes[:, t, g * P : (g + 1) * P].bitcast(FP8X4),
+                    lhsT_scale=h_scales[:, t, g * P : (g + 1) * P],
+                    rhs=w_words[:, g, 2 * j * BANK : 2 * (j + 1) * BANK].bitcast(FP4X4),
+                    rhs_scale=w_scales[:, g, j * BANK : (j + 1) * BANK],
+                    start=(g == 0),
+                    stop=(g == PASSES - 1),
+                )
+            S["r", t, j] = r_ps
+
+        def do_P1(t, j):
+            if j == 0:
+                r_copy = r_pool.tile([P, GATES], F32)
+                r_sums = stats.tile([P, BANKS], F32)
+                S["copy", t] = r_copy
+                S["sums", t] = r_sums
+            nc.scalar.activation(
+                out=S["copy", t][:, j * BANK : (j + 1) * BANK],
+                in_=S["r", t, j][:],
+                func=ACT.Identity,
+                accum_out=S["sums", t][:, j : j + 1],
+            )
+
+        def do_MEAN(t):
+            r_scaled = stats.tile([P, BANKS], F32)
+            r_negmean = stats.tile([P, 1], F32)
+            nc.scalar.activation(
+                out=r_scaled[:], in_=S["sums", t][:], func=ACT.Identity, scale=-1.0 / GATES, accum_out=r_negmean[:]
+            )
+            S["negmean", t] = r_negmean
+
+        def do_P2(t):
+            r_squares = r_pool.tile([P, GATES], BF16, bufs=1)
+            r_sumsq = stats.tile([P, 1], F32)
+            nc.scalar.activation(
+                out=r_squares[:], in_=S["copy", t][:], func=ACT.Square, bias=S["negmean", t][:], accum_out=r_sumsq[:]
+            )
+            S["sumsq", t] = r_sumsq
+
+        def rstd_of(sum_of_squares, count):
+            var = stats.tile([P, 1], F32)
+            nc.gpsimd.tensor_scalar(
+                out=var[:], in0=sum_of_squares, scalar1=1.0 / count, scalar2=EPS, op0=ALU.mult, op1=ALU.add
+            )
+            rstd = stats.tile([P, 1], F32)
+            nc.gpsimd.tensor_tensor(out=rstd[:], in0=var[:], in1=neg_half[:, 0:1], op=ALU.pow)
+            return rstd
+
+        def do_RS(t):
+            S["rstd", t] = rstd_of(S["sumsq", t][:], GATES)
+
+        def do_G1(t, half):
+            if half == 0:
+                gates = gate_pool.tile([P, GATES], F32)
+                S["gates", t] = gates
+            cols = slice(half * GATES // 2, (half + 1) * GATES // 2)
+            nc.vector.scalar_tensor_tensor(
+                out=S["gates", t][:, cols],
+                in0=S["copy", t][:, cols],
+                scalar=S["negmean", t][:],
+                in1=gain_r[:, cols],
+                op0=ALU.add,
+                op1=ALU.mult,
+            )
+
+        def do_Q(t, j):
+            a_ps = q_bank([P, BANK], F32)
             nc.tensor.matmul(
                 a_ps[:],
                 lhsT=xsT[:, t * P : (t + 1) * P],
@@ -352,258 +494,42 @@ def tile_multilstm_pa_kernel(
                     start=False,
                     stop=(k == PER_BANK - 1),
                 )
-            return a_ps
-
-        def rstd_of(sum_of_squares, count):
-            var = stats.tile([P, 1], F32)
-            nc.gpsimd.tensor_scalar(
-                out=var[:],
-                in0=sum_of_squares,
-                scalar1=1.0 / count,
-                scalar2=EPS,
-                op0=ALU.mult,
-                op1=ALU.add,
-            )
-            rstd = stats.tile([P, 1], F32)
-            nc.gpsimd.tensor_tensor(out=rstd[:], in0=var[:], in1=neg_half[:, 0:1], op=ALU.pow)
-            return rstd
-
-        def r_mm(t, j):
-            r_ps = r_bank_tile([P, BANK], F32)
-            for g in range(PASSES):
-                nc.tensor.matmul_mx(
-                    out=r_ps[:],
-                    lhsT=h_codes[:, t, g * P : (g + 1) * P].bitcast(FP8X4),
-                    lhsT_scale=h_scales[:, t, g * P : (g + 1) * P],
-                    rhs=w_words[:, g, 2 * j * BANK : 2 * (j + 1) * BANK].bitcast(FP4X4),
-                    rhs_scale=w_scales[:, g, j * BANK : (j + 1) * BANK],
-                    start=(g == 0),
-                    stop=(g == PASSES - 1),
-                )
-            return r_ps
-
-        def r_out(j, r_ps, r_copy, r_sums):
-            nc.scalar.activation(
-                out=r_copy[:, j * BANK : (j + 1) * BANK],
-                in_=r_ps[:],
-                func=ACT.Identity,
-                accum_out=r_sums[:, j : j + 1],
-            )
-
-        def r_mean(r_sums):
-            r_scaled = stats.tile([P, BANKS], F32)
-            r_negmean = stats.tile([P, 1], F32)
-            nc.scalar.activation(
-                out=r_scaled[:],
-                in_=r_sums[:],
-                func=ACT.Identity,
-                scale=-1.0 / GATES,
-                accum_out=r_negmean[:],
-            )
-            return r_negmean
-
-        def r_spread(r_copy, r_negmean):
-            r_squares = r_pool.tile([P, GATES], BF16, bufs=1)
-            r_sumsq = stats.tile([P, 1], F32)
-            nc.scalar.activation(
-                out=r_squares[:],
-                in_=r_copy[:],
-                func=ACT.Square,
-                bias=r_negmean[:],
-                accum_out=r_sumsq[:],
-            )
-            return rstd_of(r_sumsq[:], GATES)
-
-        def r_gain(gates, half, r_copy, r_negmean):
-            cols = slice(half * GATES // 2, (half + 1) * GATES // 2)
-            nc.vector.scalar_tensor_tensor(
-                out=gates[:, cols],
-                in0=r_copy[:, cols],
-                scalar=r_negmean[:],
-                in1=gain_r[:, cols],
-                op0=ALU.add,
-                op1=ALU.mult,
-            )
-
-        def add_a(gates, j, r_rstd, a_ps):
-            cols = slice(j * BANK, (j + 1) * BANK)
-            nc.vector.scalar_tensor_tensor(
-                out=gates[:, cols],
-                in0=gates[:, cols],
-                scalar=r_rstd[:],
-                in1=a_ps[:],
-                op0=ALU.mult,
-                op1=ALU.add,
-            )
-
-        def squash(gates, gate, func):
-            cols = slice(gate * HID, (gate + 1) * HID)
-            nc.scalar.activation(out=gates[:, cols], in_=gates[:, cols], func=func)
-
-        S = {}
-        ops = {}
-        bank_tag = {}
-        bank_users = {}
-        done = set()
-        banks_taken = {"r": [], "q": []}
-        slots = {"r": R_SLOTS, "q": Q_SLOTS}
-
-        def step(name, deps, what):
-            ops[name] = (what, deps)
-
-        banks_taken["r"] += [("VEC",), ("XT0",)]
-        bank_users["VEC",] = []
-        bank_users["XT0",] = []
-        banks_taken["q"] += [("GRAM",)]
-        bank_users["GRAM",] = [("NW",)]
-
-        def new_r():
-            r_copy = r_pool.tile([P, GATES], F32)
-            r_sums = stats.tile([P, BANKS], F32)
-            return r_copy, r_sums
-
-        def do_SP(g):
-            S["sp", g] = spread_gain(g * PER_BANK)
-
-        def do_XM(pair):
-            S["xm", pair] = a_sums_mm(pair)
-
-        def do_WT(q):
-            S["wT", q] = w_turn(q)
-
-        def do_XS():
-            for t in range(ROW_TILES):
-                if XS_ENGINE == "scalar":
-                    nc.scalar.activation(
-                        out=x_scaled[:, t, :], in_=x_rows[:, t, :], func=ACT.Identity, scale=a_rstd[:, t : t + 1]
-                    )
-                elif XS_ENGINE == "gpsimd":
-                    nc.gpsimd.tensor_scalar(
-                        out=x_scaled[:, t, :],
-                        in0=x_rows[:, t, :],
-                        scalar1=a_rstd[:, t : t + 1],
-                        scalar2=0.0,
-                        op0=ALU.mult,
-                        op1=ALU.add,
-                    )
-                else:
-                    nc.vector.tensor_scalar(
-                        out=x_scaled[:, t, :],
-                        in0=x_rows[:, t, :],
-                        scalar1=a_rstd[:, t : t + 1],
-                        scalar2=None,
-                        op0=ALU.mult,
-                    )
-
-        def do_XC():
-            if XC_ENGINE == "scalar":
-                nc.scalar.copy(out=xsT[:], in_=S["xsT_ps"][:])
-            else:
-                nc.vector.tensor_copy(out=xsT[:], in_=S["xsT_ps"][:])
-
-        def do_XT():
-            xsT_ps = r_bank_tile([P, BATCH], F32)
-            for t in range(ROW_TILES):
-                nc.tensor.transpose(xsT_ps[:, t * P : (t + 1) * P], x_scaled[:, t, :], ident_f32[:])
-            S["xsT_ps"] = xsT_ps
-
-        for g in range(BANKS):
-            step(("SP", g), [], lambda g=g: do_SP(g))
-            bank_tag["SP", g] = SPREAD_TAG
-            bank_users["SP", g] = [("SPC", g)]
-            step(("SPC", g), [("SP", g)], lambda g=g: spread_out(g * PER_BANK, S["sp", g], SPREAD_COPY[g]))
-        for q in range(4):
-            step(("G", q), [], lambda q=q: gram_quarter(q * QUARTER))
-            step(("WT", q), [], lambda q=q: do_WT(q))
-            bank_tag["WT", q] = "q"
-            bank_users["WT", q] = [("WC", q)]
-            step(("WC", q), [("WT", q), ("NW",)], lambda q=q: w_centre(q, S["wT", q]))
-        step(("NW",), [("G", 3)], gram_out)
-        for pair in range(ROW_TILES // 2):
-            step(("XM", pair), [("NW",)], lambda pair=pair: do_XM(pair))
-            bank_tag["XM", pair] = "r"
-            bank_users["XM", pair] = [("AS", 2 * pair), ("AS", 2 * pair + 1)]
-        for t in range(ROW_TILES):
-            step(("AS", t), [("XM", t // 2)], lambda t=t: a_sums(t, S["xm", t // 2]))
-        step(("AV",), [("AS", t) for t in range(ROW_TILES)], a_spread)
-        step(("XS",), [("AV",)], do_XS)
-        step(("XT",), [("XS",)], do_XT)
-        bank_tag["XT",] = "r"
-        bank_users["XT",] = [("XC",)]
-        step(("XC",), [("XT",)], do_XC)
-
-        def do_R(t, j):
-            S["r", t, j] = r_mm(t, j)
-
-        def do_P1(t, j):
-            if j == 0:
-                S["copy", t], S["sums", t] = new_r()
-            if j in P1_DVE and t > 0:
-                nc.vector.tensor_scalar(
-                    out=S["copy", t][:, j * BANK : (j + 1) * BANK],
-                    in0=S["r", t, j][:],
-                    scalar1=1.0,
-                    scalar2=None,
-                    op0=ALU.mult,
-                    op1=ALU.add,
-                    accum_out=S["sums", t][:, j : j + 1],
-                )
-            else:
-                r_out(j, S["r", t, j], S["copy", t], S["sums", t])
-
-        def do_MEAN(t):
-            S["negmean", t] = r_mean(S["sums", t])
-
-        def do_P2(t):
-            S["rstd", t] = r_spread(S["copy", t], S["negmean", t])
-
-        def do_G1(t, half):
-            if half == 0:
-                gates = gate_pool.tile([P, GATES], F32)
-                S["gates", t] = gates
-            r_gain(S["gates", t], half, S["copy", t], S["negmean", t])
-
-        def do_Q(t, j):
-            S["a", t, j] = a_bank(t, j)
+            S["a", t, j] = a_ps
 
         def do_A2(t, j):
-            add_a(S["gates", t], j, S["rstd", t], S["a", t, j])
+            cols = slice(j * BANK, (j + 1) * BANK)
+            nc.vector.scalar_tensor_tensor(
+                out=S["gates", t][:, cols],
+                in0=S["gates", t][:, cols],
+                scalar=S["rstd", t][:],
+                in1=S["a", t, j][:],
+                op0=ALU.mult,
+                op1=ALU.add,
+            )
 
-        def do_F(t, gate):
-            squash(S["gates", t], gate, ACT.Tanh if gate == 2 else ACT.Sigmoid)
+        def gate(t, g):
+            return S["gates", t][:, g * HID : (g + 1) * HID]
 
-        def do_HT(t):
-            S["hT", t] = h0_turn(t)
-
-        def do_HC(t):
-            S["grouped", t] = h0_group(S["hT", t], H_COPY[t])
-
-        def do_HQ(t):
-            h0_quantize(t, S["grouped", t])
+        def do_F(t, g):
+            nc.scalar.activation(out=gate(t, g), in_=gate(t, g), func=ACT.Tanh if g == 2 else ACT.Sigmoid)
 
         def do_M1(t):
-            gate_f = S["gates", t][:, HID : 2 * HID]
-            engine = nc.gpsimd if M1_POOL[t] else nc.vector
-            engine.tensor_tensor(out=gate_f, in0=gate_f, in1=c_rows[:, t, :], op=ALU.mult)
+            nc.gpsimd.tensor_tensor(out=gate(t, 1), in0=gate(t, 1), in1=c_rows[:, t, :], op=ALU.mult)
 
         def do_M2(t):
-            gate_i = S["gates", t][:, 0:HID]
-            engine = nc.gpsimd if M2_POOL[t] else nc.vector
-            engine.tensor_tensor(out=gate_i, in0=gate_i, in1=S["gates", t][:, 2 * HID : 3 * HID], op=ALU.mult)
+            nc.vector.tensor_tensor(out=gate(t, 0), in0=gate(t, 0), in1=gate(t, 2), op=ALU.mult)
 
         def do_C(t):
-            cy = cell_pool.tile([P, HID], F32)
             c_sum = stats.tile([P, 1], F32)
             nc.vector.scalar_tensor_tensor(
-                out=cy[:],
-                in0=S["gates", t][:, HID : 2 * HID],
+                out=gate(t, 0),
+                in0=gate(t, 1),
                 scalar=1.0,
-                in1=S["gates", t][:, 0:HID],
+                in1=gate(t, 0),
                 op0=ALU.mult,
                 op1=ALU.add,
                 accum_out=c_sum[:],
             )
-            S["cy", t] = cy
             S["c_sum", t] = c_sum
 
         def do_NM(t):
@@ -614,172 +540,84 @@ def tile_multilstm_pa_kernel(
             S["c_negmean", t] = c_negmean
 
         def do_SQ(t):
-            squares = cell_pool.tile([P, HID], BF16)
+            squares = stage.tile([P, HID], BF16)
             c_sumsq = stats.tile([P, 1], F32)
-            if SQ_DVE:
-                nc.vector.scalar_tensor_tensor(
-                    out=squares[:],
-                    in0=S["cy", t][:],
-                    scalar=S["c_negmean", t][:],
-                    in1=S["cy", t][:],
-                    op0=ALU.add,
-                    op1=ALU.mult,
-                    accum_out=c_sumsq[:],
-                )
-            else:
-                nc.scalar.activation(
-                    out=squares[:], in_=S["cy", t][:], func=ACT.Square, bias=S["c_negmean", t][:], accum_out=c_sumsq[:]
-                )
-            S["c_rstd", t] = rstd_of(c_sumsq[:], HID)
+            nc.scalar.activation(
+                out=squares[:], in_=gate(t, 0), func=ACT.Square, bias=S["c_negmean", t][:], accum_out=c_sumsq[:]
+            )
+            S["c_sumsq", t] = c_sumsq
+
+        def do_RC(t):
+            S["c_rstd", t] = rstd_of(S["c_sumsq", t][:], HID)
 
         def do_V1(t):
-            v1 = cell_pool.tile([P, HID], F32)
             nc.vector.scalar_tensor_tensor(
-                out=v1[:], in0=S["cy", t][:], scalar=S["c_negmean", t][:], in1=gain_c[:], op0=ALU.add, op1=ALU.mult
+                out=gate(t, 2), in0=gate(t, 0), scalar=S["c_negmean", t][:], in1=gain_c[:], op0=ALU.add, op1=ALU.mult
             )
-            S["v1", t] = v1
 
         def do_CY(t):
-            v1 = S["v1", t]
             nc.vector.scalar_tensor_tensor(
-                out=v1[:], in0=v1[:], scalar=S["c_rstd", t][:], in1=bias_c[:], op0=ALU.mult, op1=ALU.add
+                out=gate(t, 2), in0=gate(t, 2), scalar=S["c_rstd", t][:], in1=bias_c[:], op0=ALU.mult, op1=ALU.add
             )
-            nc.sync.dma_start(out=out_1[t * P : (t + 1) * P, :], in_=v1[:])
+            nc.sync.dma_start(out=cy_tiles[:, t, :], in_=gate(t, 2))
+
+        def part_cols(g, part, parts):
+            return slice(g * HID + part * HID // parts, g * HID + (part + 1) * HID // parts)
 
         def do_TH(t, part, parts):
-            if part == 0:
-                hy = cell_pool.tile([P, HID], F32)
-                S["hy", t] = hy
-            cols = slice(part * HID // parts, (part + 1) * HID // parts)
-            nc.scalar.activation(out=S["hy", t][:, cols], in_=S["v1", t][:, cols], func=ACT.Tanh)
+            gates = S["gates", t]
+            nc.scalar.activation(
+                out=gates[:, part_cols(1, part, parts)], in_=gates[:, part_cols(2, part, parts)], func=ACT.Tanh
+            )
 
         def do_HY(t, part, parts):
-            hy = S["hy", t]
+            gates = S["gates", t]
             engine = nc.gpsimd if HY_POOL[t] else nc.vector
-            cols = slice(part * HID // parts, (part + 1) * HID // parts)
-            o_cols = slice(3 * HID + part * HID // parts, 3 * HID + (part + 1) * HID // parts)
-            engine.tensor_tensor(out=hy[:, cols], in0=hy[:, cols], in1=S["gates", t][:, o_cols], op=ALU.mult)
-            nc.sync.dma_start(out=out_0[t * P : (t + 1) * P, cols], in_=hy[:, cols])
+            tanh_cy = gates[:, part_cols(1, part, parts)]
+            engine.tensor_tensor(out=tanh_cy, in0=tanh_cy, in1=gates[:, part_cols(3, part, parts)], op=ALU.mult)
+            nc.sync.dma_start(out=hy_tiles[:, t, part_cols(0, part, parts)], in_=tanh_cy)
 
-        for t in range(ROW_TILES):
+        for t in range(TILES):
             for j in range(BANKS):
-                step(("R", t, j), [("HQ", t)], lambda t=t, j=j: do_R(t, j))
-                bank_tag["R", t, j] = "r"
-                bank_users["R", t, j] = [("P1", t, j)]
+                step(("R", t, j), [("HQ", t)], lambda t=t, j=j: do_R(t, j), "r", [("P1", t, j)])
                 step(("P1", t, j), [("R", t, j)] + ([("P1", t, 0)] if j else []), lambda t=t, j=j: do_P1(t, j))
-                step(("Q", t, j), [("XC",), ("WC", j // 2)], lambda t=t, j=j: do_Q(t, j))
-                bank_tag["Q", t, j] = "r" if (LAST_IN_R and t == ROW_TILES - 1 and j in ORDER[Q_SLOTS:BANKS]) else "q"
-                bank_users["Q", t, j] = [("A2", t, j)]
-                step(("A2", t, j), [("Q", t, j), ("G1", t, j // 4), ("P2", t)], lambda t=t, j=j: do_A2(t, j))
+                step(
+                    ("Q", t, j),
+                    [("XC", 0 if t in GROUPS[0] else 1), ("WC", j // 2), ("VECC",)],
+                    lambda t=t, j=j: do_Q(t, j),
+                    "q",
+                    [("A2", t, j)],
+                )
+                step(("A2", t, j), [("Q", t, j), ("G1", t, j // 4), ("RS", t)], lambda t=t, j=j: do_A2(t, j))
             step(("MEAN", t), [("P1", t, j) for j in range(BANKS)], lambda t=t: do_MEAN(t))
             step(("P2", t), [("MEAN", t)], lambda t=t: do_P2(t))
-            for gate in range(4):
-                if gate < 2:
-                    step(("G1", t, gate), [("MEAN", t)] + ([("G1", t, 0)] if gate else []), lambda t=t, gate=gate: do_G1(t, gate))
-                step(("F", t, gate), [("A2", t, 2 * gate), ("A2", t, 2 * gate + 1)], lambda t=t, gate=gate: do_F(t, gate))
-            step(("HT", t), [], lambda t=t: do_HT(t))
-            bank_tag["HT", t] = "r"
-            bank_users["HT", t] = [("HC", t)]
-            step(("HC", t), [("HT", t)], lambda t=t: do_HC(t))
-            step(("HQ", t), [("HC", t)], lambda t=t: do_HQ(t))
+            step(("RS", t), [("P2", t)], lambda t=t: do_RS(t))
+            for half in range(2):
+                step(("G1", t, half), [("MEAN", t)] + ([("G1", t, 0)] if half else []), lambda t=t, half=half: do_G1(t, half))
+            for g in range(4):
+                step(("F", t, g), [("A2", t, 2 * g), ("A2", t, 2 * g + 1)], lambda t=t, g=g: do_F(t, g))
             step(("M1", t), [("F", t, 1)], lambda t=t: do_M1(t))
             step(("M2", t), [("F", t, 0), ("F", t, 2)], lambda t=t: do_M2(t))
             step(("C", t), [("M1", t), ("M2", t)], lambda t=t: do_C(t))
             step(("NM", t), [("C", t)], lambda t=t: do_NM(t))
             step(("SQ", t), [("NM", t)], lambda t=t: do_SQ(t))
+            step(("RC", t), [("SQ", t)], lambda t=t: do_RC(t))
             step(("V1", t), [("NM", t)], lambda t=t: do_V1(t))
-            step(("CY", t), [("V1", t), ("SQ", t)], lambda t=t: do_CY(t))
-            parts = LAST_PARTS if t == ROW_TILES - 1 else 1
+            step(("CY", t), [("V1", t), ("RC", t)], lambda t=t: do_CY(t))
+            parts = LAST_PARTS if t == TILES - 1 else 1
             for part in range(parts):
-                step(("TH", t, part), [("CY", t)] + ([("TH", t, 0)] if part else []), lambda t=t, part=part, parts=parts: do_TH(t, part, parts))
+                step(("TH", t, part), [("CY", t)], lambda t=t, part=part, parts=parts: do_TH(t, part, parts))
                 step(("HY", t, part), [("TH", t, part), ("F", t, 3)], lambda t=t, part=part, parts=parts: do_HY(t, part, parts))
 
-        tensor_q = []
-        scalar_q = []
-        vector_q = []
-        R0 = [("R", 0, j) for j in range(BANKS)]
-        P10 = [("P1", 0, j) for j in range(BANKS)]
-        G = [("G", q) for q in range(4)]
-        XM = [("XM", pair) for pair in range(ROW_TILES // 2)]
-        AS = [("AS", t) for t in range(ROW_TILES)]
-        WT = [("WT", q) for q in range(4)]
-        WC = [("WC", q) for q in range(4)]
-        Q0 = [("Q", 0, j) for j in ORDER[0:Q_SLOTS]]
-        R1 = [("R", 1, j) for j in range(R_SLOTS)]
-        if HEAD == 0:
-            tensor_q += G + [("HT", 0)] + XM + WT[0:2] + R0[0:3] + WT[2:4] + [("XT",)] + R0[3:8] + [("HT", 1)] + Q0 + R1
-        else:
-            tensor_q += G + [("HT", 0)] + XM + WT[0:2] + R0[0:3] + WT[2:4] + [("XT",)] + R0[3:8] + [("HT", 1)] + R1 + Q0
-        scalar_q += [("HC", 0)] + P10 + [("MEAN", 0)]
-        vector_q += [("NW",), ("HQ", 0)] + AS + [("AV",), ("XS",)] + WC[0:2] + [("XC",)] + WC[2:4] + [("HC", 1), ("HQ", 1)]
-        LAST = ROW_TILES - 1
-        for f in range(ROW_TILES):
-            prev = f >= 1
-            nxt = f + 1 < ROW_TILES
-            nxt2 = f + 2 < ROW_TILES
-            late = DEFER and f == LAST - 1
-            after_late = DEFER and f == LAST
-            a2 = [("A2", f, j) for j in ORDER]
-            p1 = [("P1", f + 1, j) for j in range(BANKS)] if nxt else []
-            p1_act = [s for s in p1 if s[2] not in P1_DVE]
-            p1_dve = [s for s in p1 if s[2] in P1_DVE]
-            vector_q += [("G1", f, 0), ("G1", f, 1)]
-            vector_q += a2
-            hc = [("HC", f + 2)] if nxt2 else []
-            hq = [("HQ", f + 2)] if nxt2 else []
-            m2 = [] if M2_POOL[f] else [("M2", f)]
-            if after_late:
-                vector_q += m2 + [("C", f), ("NM", f), ("CY", f - 1), ("V1", f), ("CY", f), ("HY", f - 1, 0)]
-            elif late:
-                vector_q += p1_dve + m2 + [("C", f), ("NM", f), ("V1", f)]
-            elif VT == 0:
-                vector_q += p1_dve + m2 + [("C", f), ("NM", f), ("V1", f)] + hc + hq + [("CY", f)]
-            elif VT == 1:
-                vector_q += p1_dve + hc + m2 + [("C", f), ("NM", f), ("V1", f)] + hq + [("CY", f)]
-            elif VT == 2:
-                vector_q += p1_dve + hc + m2 + [("C", f)] + hq + [("NM", f), ("V1", f)] + [("CY", f)]
-
-            scalar_q += [("P2", f)]
-            if after_late:
-                scalar_q += [("SQ", f - 1), ("F", f - 1, 3)]
-            elif prev:
-                scalar_q += [("TH", f - 1, 0)]
-                if HY_POOL[f - 1]:
-                    scalar_q += [("HY", f - 1, 0)]
-            fs = [("F", f, ORDER[2 * k] // 2) for k in range(4)]
-            pa = PA if prev else PA0
-            pb = PB if prev else PB0
-            scalar_q += p1_act[0:pa] + fs[0:1] + [("M1", f)] + p1_act[pa:pb] + fs[1:3] + ([("M2", f)] if M2_POOL[f] else [])
-            if late:
-                scalar_q += p1_act[pb:8]
-            else:
-                scalar_q += fs[3:4]
-                scalar_q += p1_act[pb:PD] + [("SQ", f)] + p1_act[PD:8]
-            if after_late:
-                scalar_q += [("TH", f - 1, 0)]
-            if nxt:
-                scalar_q += [("MEAN", f + 1)]
-
-            if nxt or not LAST_IN_R:
-                tensor_q += [("Q", f, j) for j in ORDER[Q_SLOTS:BANKS]]
-            if nxt:
-                tensor_q += [("R", f + 1, j) for j in range(R_SLOTS, BANKS)]
-                if nxt2:
-                    tensor_q += [("HT", f + 2)]
-                tensor_q += [("Q", f + 1, j) for j in ORDER[0:Q_SLOTS]]
-                if LAST_IN_R and not nxt2:
-                    tensor_q += [("Q", f + 1, j) for j in ORDER[Q_SLOTS:BANKS]]
-                if nxt2:
-                    tensor_q += [("R", f + 2, j) for j in range(R_SLOTS)]
-        scalar_q += [("TH", ROW_TILES - 1, part) for part in range(LAST_PARTS)]
-        vector_q += [("HY", ROW_TILES - 1, part) for part in range(LAST_PARTS)]
-
-        queues = [tensor_q, scalar_q, vector_q]
-        place = [0, 0, 0]
+        queues = [T_LIST, S_LIST, V_LIST, G_LIST]
+        slots = {"r": R_SLOTS, "q": Q_SLOTS}
+        banks_taken = {"r": [], "q": []}
+        done = set()
+        place = [0, 0, 0, 0]
         moved = True
         while moved:
             moved = False
-            for e in range(3):
+            for e in range(4):
                 while place[e] < len(queues[e]):
                     name = queues[e][place[e]]
                     what, deps = ops[name]
@@ -793,8 +631,10 @@ def tile_multilstm_pa_kernel(
                             if not all(u in done for u in bank_users[old]):
                                 break
                         taken.append(name)
+                        if name == ("G", 0):
+                            taken.append(name)
                     what()
                     done.add(name)
                     place[e] += 1
                     moved = True
-        assert all(place[e] == len(queues[e]) for e in range(3))
+        assert all(place[e] == len(queues[e]) for e in range(4))

@@ -34,7 +34,6 @@ FIG = ORDER[0:6]
 GROUPS = [[0], [1, 2, 3]]
 WPARTS = 4
 LAST_PARTS = 2
-HY_POOL = [True, True, False, False]
 HC_ON = ["scalar", "vector", "vector", "vector"]
 FLOPS = 2 * BATCH * GATES * (HID + IN)
 
@@ -80,12 +79,12 @@ V_LIST = (
     [("HQ", 0), ("XC0",), ("NW",), ("AS", 0), ("AV", 0), ("WC", 1), ("XS", 0), ("AS", 1), ("AV", 1), ("HC", 1), ("HQ", 1), ("XC", 0), ("VECC",), ("WC", 0)]
     + [("G1", 0, 0), ("WC", 2)] + A2(0, 2, 3) + [("WC", 3), ("G1", 0, 1)] + A2(0, 0) + [("HC", 2), ("HC", 3), ("XS", 1)] + A2(0, 1) + [("HQ", 2), ("HQ", 3), ("XC", 1)] + A2(0, 4)
     + [("G1", 1, 0)] + A2(0, 5) + [("G1", 1, 1)]
-    + A2(1, 2) + [("M2", 0)] + A2(1, 3) + [("C", 0)] + A2(1, 0) + [("NM", 0), ("G1", 2, 0), ("V1", 0)] + A2(1, 1, 4, 5) + [("G1", 2, 1)] + A2(0, 6, 7) + [("CY", 0)]
-    + [("M2", 1)] + A2(2, 2) + [("C", 1)] + A2(2, 3) + [("NM", 1)] + A2(2, 0) + [("V1", 1), ("G1", 3, 0)] + A2(2, 1, 4, 5) + [("G1", 3, 1), ("CY", 1)]
-    + A2(3, 2, 3) + [("M2", 2)] + A2(3, 0, 1) + [("C", 2)] + A2(3, 4, 5) + [("NM", 2)] + A2(1, 6, 7) + [("M2", 3)] + A2(2, 6) + [("V1", 2), ("C", 3)] + A2(2, 7) + [("NM", 3), ("CY", 2), ("V1", 3)] + A2(3, 6, 7)
-    + [("CY", 3), ("HY", 2, 0), ("HY", 3, 0), ("HY", 3, 1)]
+    + A2(1, 2) + [("M1",0),("M2", 0)] + A2(1, 3) + [("C", 0)] + A2(1, 0) + [("NM", 0), ("G1", 2, 0), ("V1", 0)] + A2(1, 1, 4, 5) + [("G1", 2, 1)] + A2(0, 6, 7) + [("CY", 0)]
+    + [("M1",1),("M2", 1)] + A2(2, 2) + [("C", 1)] + A2(2, 3) + [("NM", 1)] + A2(2, 0) + [("V1", 1), ("G1", 3, 0)] + A2(2, 1, 4, 5) + [("G1", 3, 1), ("CY", 1),("HY",0,0)]
+    + A2(3, 2, 3) + [("M1",2),("M2", 2)] + A2(3, 0, 1) + [("C", 2)] + A2(3, 4, 5) + [("NM", 2)] + A2(1, 6, 7) + [("M1",3),("M2", 3)] + A2(2, 6) + [("V1", 2), ("C", 3)] + A2(2, 7) + [("NM", 3), ("CY", 2), ("V1", 3)] + A2(3, 6, 7)
+    + [("HY",1,0),("CY", 3), ("HY", 2, 0), ("HY", 3, 0), ("HY", 3, 1)]
 )
-G_LIST = [("PW", 0), ("PW", 1), ("RS", 0), ("RS", 1), ("M1", 0), ("RS", 2), ("RC", 0), ("M1", 1), ("HY", 0, 0), ("RC", 1), ("RS", 3), ("M1", 2), ("M1", 3), ("RC", 2), ("HY", 1, 0), ("RC", 3)]
+G_LIST = [("PW", 0), ("PW", 1), ("RS", 0), ("RS", 1), ("RS", 2), ("RC", 0), ("RC", 1), ("RS", 3), ("RC", 2), ("RC", 3)]
 
 
 def tile_multilstm_pa_kernel(
@@ -514,7 +513,7 @@ def tile_multilstm_pa_kernel(
             nc.scalar.activation(out=gate(t, g), in_=gate(t, g), func=ACT.Tanh if g == 2 else ACT.Sigmoid)
 
         def do_M1(t):
-            nc.gpsimd.tensor_tensor(out=gate(t, 1), in0=gate(t, 1), in1=c_rows[:, t, :], op=ALU.mult)
+            nc.vector.tensor_tensor(out=gate(t, 1), in0=gate(t, 1), in1=c_rows[:, t, :], op=ALU.mult)
 
         def do_M2(t):
             nc.vector.tensor_tensor(out=gate(t, 0), in0=gate(t, 0), in1=gate(t, 2), op=ALU.mult)
@@ -572,9 +571,8 @@ def tile_multilstm_pa_kernel(
 
         def do_HY(t, part, parts):
             gates = S["gates", t]
-            engine = nc.gpsimd if HY_POOL[t] else nc.vector
             tanh_cy = gates[:, part_cols(1, part, parts)]
-            engine.tensor_tensor(out=tanh_cy, in0=tanh_cy, in1=gates[:, part_cols(3, part, parts)], op=ALU.mult)
+            nc.vector.tensor_tensor(out=tanh_cy, in0=tanh_cy, in1=gates[:, part_cols(3, part, parts)], op=ALU.mult)
             nc.sync.dma_start(out=hy_tiles[:, t, part_cols(0, part, parts)], in_=tanh_cy)
 
         for t in range(TILES):

@@ -34,10 +34,14 @@ FIG = ORDER[0:6]
 GROUPS = [[0], [1, 2, 3]]
 WPARTS = 4
 LAST_PARTS = 2
+DUMMIES = 6
+M1_POOL = [False] * 4
+HY_POOL = [False] * 4
 HC_ON = ["scalar", "vector", "vector", "vector"]
 FLOPS = 2 * BATCH * GATES * (HID + IN)
 
-LOADS = [("h", 0), ("x",), ("w", 0), ("w", 1), ("w", 2), ("w", 3), ("scales",), ("words", 0), ("bias",), ("gain_a", 0), ("words", 1), ("words", 2), ("gain_a", 1), ("words", 3), ("h", 1), ("gain_r", 0), ("gain_r", 1), ("h23",), ("c",), ("gain_c",), ("bias_c",)]
+SPC_ON = ["scalar"] * 4 + ["vector"] * 4
+LOADS = [("vecs",), ("h", 0), ("x",), ("w", 0), ("w", 1), ("w", 2), ("w", 3), ("scales",), ("words", 0), ("words", 1), ("words", 2), ("words", 3), ("h", 1), ("gain_r", 0), ("gain_r", 1), ("h23",), ("c",), ("gain_c",), ("bias_c",)]
 
 
 def R(t, a, b):
@@ -52,6 +56,10 @@ def Q(t, *js):
     return [("Q", t, j) for j in js]
 
 
+def SP(a, b):
+    return [("SP", i) for i in range(a, b)]
+
+
 def A2(t, *js):
     return [("A2", t, j) for j in js]
 
@@ -60,23 +68,25 @@ def F(t, *gs):
     return [("F", t, g) for g in gs]
 
 
-G4 = [("G", 0), ("G", 1), ("G", 2), ("G", 3)]
+G4 = [("GB",), ("G", 0), ("G", 1), ("G", 2), ("G", 3)]
+DUMMIES = 4
 T_LIST = (
-    [("HT", 0), ("XT0",)] + G4 + [("WT", 1), ("XM", 0)] + R(0, 0, 4) + [("XM", 1)] + R(0, 4, 8)
-    + [("HT", 1), ("XT", 0), ("VEC",), ("WT", 0), ("WT", 2), ("WT", 3)]
+[("DUM",),("VEC",),("HT",0)]+[("SP",2),("SP",3)]+[("XT0",)]+[("SP",0),("SP",1)]+[("GB",),("G",0),("G",1)]+[("SP",4)]+[("G",2)]+[("SP",5)]+[("G",3),("WT",1),("XM",0)]+[("SP",6),("SP",7)]+R(0,0,4)+[("XM",1)]+R(0,4,8)+[("HT", 1), ("XT", 0), ("WT", 0), ("WT", 2), ("WT", 3)]
     + R(1, 0, 1) + Q(0, 2) + R(1, 1, 3) + Q(0, 3) + R(1, 3, 5) + Q(0, 0) + R(1, 5, 8) + Q(0, 1) + [("HT", 2), ("HT", 3)] + Q(0, 4) + [("XT", 1)] + Q(0, 5)
     + R(2, 0, 3) + Q(1, 2) + R(2, 3, 6) + Q(1, 3, 0) + R(2, 6, 8) + Q(1, 1) + R(3, 0, 1) + Q(1, 4, 5) + R(3, 1, 2) + Q(0, 6, 7)
     + R(3, 2, 4) + Q(2, 2, 3) + R(3, 4, 6) + Q(2, 0) + R(3, 6, 8) + Q(2, 1, 4, 5)
     + Q(3, *FIG) + Q(1, 6, 7) + Q(2, 6, 7) + Q(3, 6, 7)
 )
+
 S_LIST = (
-    [("HC", 0)] + P1(0, 0, 8) + [("MEAN", 0), ("P2", 0)] + P1(1, 0, 5) + F(0, 1) + P1(1, 5, 8) + [("MEAN", 1), ("P2", 1)]
+    [("SPC",2),("HC",0),("SPC",3),("SPC",0),("SPC",1)]+P1(0,0,8) + [("MEAN", 0), ("P2", 0)] + P1(1, 0, 5) + F(0, 1) + P1(1, 5, 8) + [("MEAN", 1), ("P2", 1)]
     + P1(2, 0, 3) + F(0, 0) + P1(2, 3, 5) + F(0, 2) + P1(2, 5, 8) + [("MEAN", 2), ("P2", 2), ("SQ", 0)]
     + F(1, 1) + P1(3, 0, 1) + F(1, 0) + P1(3, 1, 2) + F(1, 2) + P1(3, 2, 4) + F(0, 3) + P1(3, 4, 8) + [("MEAN", 3), ("SQ", 1), ("TH", 0, 0), ("P2", 3)]
     + F(2, 1, 0, 2) + F(3, 1, 0, 2) + [("SQ", 2)] + F(1, 3) + [("TH", 1, 0), ("SQ", 3), ("TH", 2, 0)] + F(2, 3) + F(3, 3) + [("TH", 3, 0), ("TH", 3, 1)]
 )
+
 V_LIST = (
-    [("HQ", 0), ("XC0",), ("NW",), ("AS", 0), ("AV", 0), ("WC", 1), ("XS", 0), ("AS", 1), ("AV", 1), ("HC", 1), ("HQ", 1), ("XC", 0), ("VECC",), ("WC", 0)]
+    [("VECC",),("XC0",),("HQ",0),("SPC",4),("SPC",5), ("NW",), ("AS", 0),("SPC",6), ("AV", 0), ("SPC",7),("WC", 1), ("XS", 0), ("AS", 1), ("AV", 1), ("HC", 1), ("HQ", 1), ("XC", 0), ("WC", 0)]
     + [("G1", 0, 0), ("WC", 2)] + A2(0, 2, 3) + [("WC", 3), ("G1", 0, 1)] + A2(0, 0) + [("HC", 2), ("HC", 3), ("XS", 1)] + A2(0, 1) + [("HQ", 2), ("HQ", 3), ("XC", 1)] + A2(0, 4)
     + [("G1", 1, 0)] + A2(0, 5) + [("G1", 1, 1)]
     + A2(1, 2) + [("M1",0),("M2", 0)] + A2(1, 3) + [("C", 0)] + A2(1, 0) + [("NM", 0), ("G1", 2, 0), ("V1", 0)] + A2(1, 1, 4, 5) + [("G1", 2, 1)] + A2(0, 6, 7) + [("CY", 0)]
@@ -84,6 +94,7 @@ V_LIST = (
     + A2(3, 2, 3) + [("M1",2),("M2", 2)] + A2(3, 0, 1) + [("C", 2)] + A2(3, 4, 5) + [("NM", 2)] + A2(1, 6, 7) + [("M1",3),("M2", 3)] + A2(2, 6) + [("V1", 2), ("C", 3)] + A2(2, 7) + [("NM", 3), ("CY", 2), ("V1", 3)] + A2(3, 6, 7)
     + [("HY",1,0),("CY", 3), ("HY", 2, 0), ("HY", 3, 0), ("HY", 3, 1)]
 )
+
 G_LIST = [("PW", 0), ("PW", 1), ("RS", 0), ("RS", 1), ("RS", 2), ("RC", 0), ("RC", 1), ("RS", 3), ("RC", 2), ("RC", 3)]
 
 
@@ -122,6 +133,8 @@ def tile_multilstm_pa_kernel(
             q_slot = psum.tile(shape, dtype, tag="q", bufs=Q_SLOTS)
             return q_slot
 
+        zeros = keep.tile([P, P], F32)
+        nc.vector.memset(zeros[:], 0.0)
         w_scales = keep.tile([P, PASSES, GATES], U8, align_bytes=64)
         nc.vector.memset(w_scales[:].rearrange("p g n -> p (g n)").bitcast(I32), 0)
         ident_f32 = keep.tile([P, P], F32)
@@ -131,7 +144,7 @@ def tile_multilstm_pa_kernel(
         neg_half = keep.tile([P, TILES], F32)
         nc.gpsimd.memset(neg_half[:], -0.5)
         gate_vecs = keep.tile([P, P], BF16)
-        nc.vector.memset(gate_vecs[2 * BLOCKS : P, :], 0.0)
+        nc.vector.memset(gate_vecs[3 * BLOCKS : P, :], 0.0)
         warm = keep.tile([P, 1], F32)
         nc.vector.memset(warm[:], 0.0)
         nc.scalar.activation(out=warm[:], in_=warm[:], func=ACT.Sigmoid)
@@ -154,8 +167,8 @@ def tile_multilstm_pa_kernel(
 
         def load(what, i=0):
             dma = nc.sync.dma_start
-            if what == "bias":
-                for n, vec in enumerate((lni_b1, lnh_b1)):
+            if what == "vecs":
+                for n, vec in enumerate((lni_w1, lni_b1, lnh_b1)):
                     dma(out=gate_vecs[BLOCKS * n : BLOCKS * (n + 1), :], in_=vec.rearrange("(j p) -> j p", p=P))
             elif what == "x":
                 dma(out=x_rows[:], in_=x.rearrange("(p t) v -> p t v", t=TILES))
@@ -176,9 +189,6 @@ def tile_multilstm_pa_kernel(
                 some = slice(i * n, (i + 1) * n)
                 for g in range(PASSES):
                     dma(out=w_words[:, g, some].bitcast(I32), in_=w_hh1_words[g, :, some].bitcast(I32))
-            elif what == "gain_a":
-                cols = slice(i * GATES // 2, (i + 1) * GATES // 2)
-                dma(out=gain_a[:, cols], in_=lni_w1[cols].partition_broadcast(P))
             elif what == "gain_r":
                 cols = slice(i * GATES // 2, (i + 1) * GATES // 2)
                 dma(out=gain_r[:, cols], in_=lnh_w1[cols].partition_broadcast(P))
@@ -203,6 +213,13 @@ def tile_multilstm_pa_kernel(
                 bank_tag[name] = bank
                 bank_users[name] = list(users)
 
+        def do_DUM():
+            dummy_ps = r_bank([P, P], F32)
+            for n in range(DUMMIES):
+                nc.tensor.matmul(dummy_ps[:], lhsT=zeros[:], rhs=zeros[:], start=True, stop=True)
+
+        step(("DUM",), [], do_DUM, "r", [])
+
         vec_cols = keep.tile([P, P], BF16)
         bias_cols = keep.tile([P, BLOCKS], F32)
         xT_f32 = keep.tile([P, BATCH], F32)
@@ -215,7 +232,10 @@ def tile_multilstm_pa_kernel(
         def do_VECC():
             nc.vector.tensor_copy(out=vec_cols[:], in_=S["vec"][:])
             nc.vector.tensor_tensor(
-                out=bias_cols[:], in0=vec_cols[:, 0:BLOCKS], in1=vec_cols[:, BLOCKS : 2 * BLOCKS], op=ALU.add
+                out=bias_cols[:],
+                in0=vec_cols[:, BLOCKS : 2 * BLOCKS],
+                in1=vec_cols[:, 2 * BLOCKS : 3 * BLOCKS],
+                op=ALU.add,
             )
 
         def do_XT0():
@@ -227,6 +247,25 @@ def tile_multilstm_pa_kernel(
         def do_XC0():
             nc.vector.tensor_copy(out=xT_f32[:], in_=S["xT"][:])
 
+        def do_SP(b):
+            spread_ps = q_bank([P, BANK], BF16)
+            for k in range(PER_BANK):
+                block = b * PER_BANK + k
+                nc.tensor.transpose(
+                    spread_ps[:, k * P : (k + 1) * P], vec_cols[:, block : block + 1].to_broadcast([P, P]), ident_bf[:]
+                )
+            S["spread", b] = spread_ps
+
+        def do_SPC(b):
+            out = gain_a[:, b * BANK : (b + 1) * BANK]
+            if SPC_ON[b] == "scalar":
+                nc.scalar.copy(out=out, in_=S["spread", b][:])
+            else:
+                nc.vector.tensor_copy(out=out, in_=S["spread", b][:])
+
+        for b in range(BANKS):
+            step(("SP", b), [("VECC",)], lambda b=b: do_SP(b), "q", [("SPC", b)])
+            step(("SPC", b), [("SP", b)], lambda b=b: do_SPC(b))
         step(("VEC",), [], do_VEC, "r", [("VECC",)])
         step(("VECC",), [("VEC",)], do_VECC)
         step(("XT0",), [], do_XT0, "r", [("XC0",)])
@@ -271,11 +310,13 @@ def tile_multilstm_pa_kernel(
         neg_wmean = keep.tile([P, 1], F32)
         gram = keep.tile([P, IN + ONES], F32)
 
+        def do_GB():
+            gram_ps = q_bank([P, IN], F32)
+            S["gram"] = gram_ps
+
         def do_G(q):
             if q == 0:
-                gram_ps = q_bank([P, IN], F32)
                 wsum_ps = q_bank([P, ONES], F32)
-                S["gram"] = gram_ps
                 S["wsum"] = wsum_ps
             for b in range(2 * q, 2 * q + 2):
                 for k in range(PER_BANK):
@@ -292,8 +333,9 @@ def tile_multilstm_pa_kernel(
             nc.vector.tensor_copy(out=gram[:, 0:IN], in_=S["gram"][:])
             nc.vector.tensor_copy(out=gram[:, IN : IN + ONES], in_=S["wsum"][:])
 
+        step(("GB",), [], do_GB, "q", [("NW",)])
         for q in range(4):
-            step(("G", q), [("G", q - 1)] if q else [], lambda q=q: do_G(q))
+            step(("G", q), [("G", q - 1)] if q else [("GB",)], lambda q=q: do_G(q))
         bank_tag["G", 0] = "q"
         bank_users["G", 0] = [("NW",)]
         step(("NW",), [("G", 3)], do_NW)
@@ -322,7 +364,7 @@ def tile_multilstm_pa_kernel(
 
         for q in range(4):
             step(("WT", q), [], lambda q=q: do_WT(q), "q", [("WC", q)])
-            step(("WC", q), [("WT", q), ("NW",)], lambda q=q: do_WC(q))
+            step(("WC", q), [("WT", q), ("NW",), ("SPC", 2 * q), ("SPC", 2 * q + 1)], lambda q=q: do_WC(q))
 
         a_negmean = keep.tile([P, TILES], F32)
         a_sumsq = keep.tile([P, TILES], F32)
@@ -513,7 +555,8 @@ def tile_multilstm_pa_kernel(
             nc.scalar.activation(out=gate(t, g), in_=gate(t, g), func=ACT.Tanh if g == 2 else ACT.Sigmoid)
 
         def do_M1(t):
-            nc.vector.tensor_tensor(out=gate(t, 1), in0=gate(t, 1), in1=c_rows[:, t, :], op=ALU.mult)
+            engine = nc.gpsimd if M1_POOL[t] else nc.vector
+            engine.tensor_tensor(out=gate(t, 1), in0=gate(t, 1), in1=c_rows[:, t, :], op=ALU.mult)
 
         def do_M2(t):
             nc.vector.tensor_tensor(out=gate(t, 0), in0=gate(t, 0), in1=gate(t, 2), op=ALU.mult)
@@ -571,8 +614,9 @@ def tile_multilstm_pa_kernel(
 
         def do_HY(t, part, parts):
             gates = S["gates", t]
+            engine = nc.gpsimd if HY_POOL[t] else nc.vector
             tanh_cy = gates[:, part_cols(1, part, parts)]
-            nc.vector.tensor_tensor(out=tanh_cy, in0=tanh_cy, in1=gates[:, part_cols(3, part, parts)], op=ALU.mult)
+            engine.tensor_tensor(out=tanh_cy, in0=tanh_cy, in1=gates[:, part_cols(3, part, parts)], op=ALU.mult)
             nc.sync.dma_start(out=hy_tiles[:, t, part_cols(0, part, parts)], in_=tanh_cy)
 
         for t in range(TILES):
@@ -629,8 +673,6 @@ def tile_multilstm_pa_kernel(
                             if not all(u in done for u in bank_users[old]):
                                 break
                         taken.append(name)
-                        if name == ("G", 0):
-                            taken.append(name)
                     what()
                     done.add(name)
                     place[e] += 1

@@ -34,9 +34,8 @@ FIG = ORDER[0:6]
 GROUPS = [[0], [1, 2, 3]]
 WPARTS = 4
 LAST_PARTS = 2
-DUMMIES = 6
-M1_POOL = [False] * 4
-HY_POOL = [False] * 4
+M1_POOL = [False,False,True,False]
+HY_POOL = [False]*4
 HC_ON = ["scalar", "vector", "vector", "vector"]
 FLOPS = 2 * BATCH * GATES * (HID + IN)
 
@@ -69,33 +68,29 @@ def F(t, *gs):
 
 
 G4 = [("GB",), ("G", 0), ("G", 1), ("G", 2), ("G", 3)]
-DUMMIES = 4
+DUMMIES = [6,1,1]
 T_LIST = (
-[("DUM",),("VEC",),("HT",0)]+[("SP",2),("SP",3)]+[("XT0",)]+[("SP",0),("SP",1)]+[("GB",),("G",0),("G",1)]+[("SP",4)]+[("G",2)]+[("SP",5)]+[("G",3),("WT",1),("XM",0)]+[("SP",6),("SP",7)]+R(0,0,4)+[("XM",1)]+R(0,4,8)+[("HT", 1), ("XT", 0), ("WT", 0), ("WT", 2), ("WT", 3)]
-    + R(1, 0, 1) + Q(0, 2) + R(1, 1, 3) + Q(0, 3) + R(1, 3, 5) + Q(0, 0) + R(1, 5, 8) + Q(0, 1) + [("HT", 2), ("HT", 3)] + Q(0, 4) + [("XT", 1)] + Q(0, 5)
-    + R(2, 0, 3) + Q(1, 2) + R(2, 3, 6) + Q(1, 3, 0) + R(2, 6, 8) + Q(1, 1) + R(3, 0, 1) + Q(1, 4, 5) + R(3, 1, 2) + Q(0, 6, 7)
-    + R(3, 2, 4) + Q(2, 2, 3) + R(3, 4, 6) + Q(2, 0) + R(3, 6, 8) + Q(2, 1, 4, 5)
+    [("DUM",0), ("VEC",), ("HT",0), ("SP",2), ("DUM",1), ("SP",3), ("XT0",), ("SP",0), ("DUM",2), ("SP",1), ("GB",), ("G",0), ("G",1), ("SP",4), ("G",2), ("SP",5), ("G",3), ("WT",1), ("XM",0), ("SP",6), ("SP",7)] + R(0,0,4) + [("XM",1)] + R(0,4,8) + [("HT", 1), ("XT", 0), ("WT", 0), ("WT", 2), ("WT", 3)]
+    + Q(0,2,3,0) + R(1,0,8) + Q(0,1) + [("HT",2), ("HT",3)] + Q(0,4) + [("XT",1)] + Q(0,5)
+    + R(2,0,3) + Q(1,2) + R(2,3,6) + Q(1,3,0) + R(2,6,8) + R(3,0,1) + Q(1,1,4,5) + Q(0,6,7)
+    + R(3,1,4) + Q(2,2,3,0) + R(3,4,8) + Q(2,1,4,5)
     + Q(3, *FIG) + Q(1, 6, 7) + Q(2, 6, 7) + Q(3, 6, 7)
 )
-
 S_LIST = (
-    [("SPC",2),("HC",0),("SPC",3),("SPC",0),("SPC",1)]+P1(0,0,8) + [("MEAN", 0), ("P2", 0)] + P1(1, 0, 5) + F(0, 1) + P1(1, 5, 8) + [("MEAN", 1), ("P2", 1)]
+    [("SPC",2), ("HC",0), ("SPC",3), ("SPC",0), ("SPC",1)] + P1(0,0,8) + [("MEAN", 0), ("P2", 0)] + P1(1, 0, 5) + F(0, 1) + P1(1, 5, 8) + [("MEAN", 1), ("P2", 1)]
     + P1(2, 0, 3) + F(0, 0) + P1(2, 3, 5) + F(0, 2) + P1(2, 5, 8) + [("MEAN", 2), ("P2", 2), ("SQ", 0)]
     + F(1, 1) + P1(3, 0, 1) + F(1, 0) + P1(3, 1, 2) + F(1, 2) + P1(3, 2, 4) + F(0, 3) + P1(3, 4, 8) + [("MEAN", 3), ("SQ", 1), ("TH", 0, 0), ("P2", 3)]
-    + F(2, 1, 0, 2) + F(3, 1, 0, 2) + [("SQ", 2)] + F(1, 3) + [("TH", 1, 0), ("SQ", 3), ("TH", 2, 0)] + F(2, 3) + F(3, 3) + [("TH", 3, 0), ("TH", 3, 1)]
+    + F(2,1,0,2) + F(3,1,0) + [("SQ",2)] + F(3,2) + F(1,3) + [("TH",1,0), ("SQ",3), ("TH",2,0)] + F(2,3) + F(3,3) + [("TH",3,0), ("TH",3,1)]
 )
-
 V_LIST = (
-    [("VECC",),("XC0",),("HQ",0),("SPC",4),("SPC",5), ("NW",), ("AS", 0),("SPC",6), ("AV", 0), ("SPC",7),("WC", 1), ("XS", 0), ("AS", 1), ("AV", 1), ("HC", 1), ("HQ", 1), ("XC", 0), ("WC", 0)]
-    + [("G1", 0, 0), ("WC", 2)] + A2(0, 2, 3) + [("WC", 3), ("G1", 0, 1)] + A2(0, 0) + [("HC", 2), ("HC", 3), ("XS", 1)] + A2(0, 1) + [("HQ", 2), ("HQ", 3), ("XC", 1)] + A2(0, 4)
-    + [("G1", 1, 0)] + A2(0, 5) + [("G1", 1, 1)]
-    + A2(1, 2) + [("M1",0),("M2", 0)] + A2(1, 3) + [("C", 0)] + A2(1, 0) + [("NM", 0), ("G1", 2, 0), ("V1", 0)] + A2(1, 1, 4, 5) + [("G1", 2, 1)] + A2(0, 6, 7) + [("CY", 0)]
-    + [("M1",1),("M2", 1)] + A2(2, 2) + [("C", 1)] + A2(2, 3) + [("NM", 1)] + A2(2, 0) + [("V1", 1), ("G1", 3, 0)] + A2(2, 1, 4, 5) + [("G1", 3, 1), ("CY", 1),("HY",0,0)]
-    + A2(3, 2, 3) + [("M1",2),("M2", 2)] + A2(3, 0, 1) + [("C", 2)] + A2(3, 4, 5) + [("NM", 2)] + A2(1, 6, 7) + [("M1",3),("M2", 3)] + A2(2, 6) + [("V1", 2), ("C", 3)] + A2(2, 7) + [("NM", 3), ("CY", 2), ("V1", 3)] + A2(3, 6, 7)
-    + [("HY",1,0),("CY", 3), ("HY", 2, 0), ("HY", 3, 0), ("HY", 3, 1)]
+    [("VECC",), ("XC0",), ("HQ",0), ("SPC",4), ("SPC",5), ("NW",), ("AS", 0), ("SPC",6), ("AV", 0), ("SPC",7), ("WC", 1), ("XS", 0), ("AS", 1), ("AV", 1), ("HC", 1), ("HQ", 1), ("XC", 0), ("WC", 0)]
+    + [("G1", 0, 0), ("WC", 2)] + A2(0, 2, 3) + [("WC", 3), ("G1", 0, 1)] + A2(0, 0) + [("HC", 2), ("HC", 3), ("XS", 1)] + A2(0, 1) + [("HQ", 2), ("HQ", 3), ("XC", 1)] + A2(0, 4) + [("G1", 1, 0)] + A2(0, 5) + [("G1", 1, 1)]
+    + A2(1, 2) + [("M1",0), ("M2", 0)] + A2(1, 3) + [("C", 0)] + A2(1, 0) + [("NM", 0), ("G1", 2, 0), ("V1", 0)] + A2(1, 1, 4, 5) + [("G1", 2, 1)] + A2(0, 6, 7) + [("CY", 0)]
+    + [("M1",1), ("M2",1)] + A2(2,2) + [("C",1)] + A2(2,3) + [("NM",1)] + A2(2,0) + [("V1",1), ("G1",3,0)] + A2(2,1) + [("G1",3,1), ("CY",1), ("HY",0,0)] + A2(2,4,5)
+    + A2(3,2,3,0,1) + [("M2",2), ("M1",3), ("C",2)] + A2(3,4) + [("NM",2)] + A2(3,5) + [("V1",2)] + A2(1,6,7) + [("M2",3)] + A2(2,6) + [("C",3)] + A2(2,7) + [("NM",3), ("CY",2), ("V1",3)] + A2(3,6,7)
+    + [("HY",1,0), ("CY", 3), ("HY", 2, 0), ("HY", 3, 0), ("HY", 3, 1)]
 )
-
-G_LIST = [("PW", 0), ("PW", 1), ("RS", 0), ("RS", 1), ("RS", 2), ("RC", 0), ("RC", 1), ("RS", 3), ("RC", 2), ("RC", 3)]
+G_LIST = [("PW",0),("PW",1),("RS",0),("RS",1),("RS",2),("RC",0),("RC",1),("RS",3),("M1",2),("RC",2),("RC",3)]
 
 
 def tile_multilstm_pa_kernel(
@@ -213,12 +208,13 @@ def tile_multilstm_pa_kernel(
                 bank_tag[name] = bank
                 bank_users[name] = list(users)
 
-        def do_DUM():
+        def do_DUM(count):
             dummy_ps = r_bank([P, P], F32)
-            for n in range(DUMMIES):
+            for n in range(count):
                 nc.tensor.matmul(dummy_ps[:], lhsT=zeros[:], rhs=zeros[:], start=True, stop=True)
 
-        step(("DUM",), [], do_DUM, "r", [])
+        for i, count in enumerate(DUMMIES):
+            step(("DUM", i), [], lambda count=count: do_DUM(count), "r", [])
 
         vec_cols = keep.tile([P, P], BF16)
         bias_cols = keep.tile([P, BLOCKS], F32)

@@ -34,7 +34,7 @@ FIG = ORDER[0:6]
 GROUPS = [[0], [1, 2, 3]]
 WPARTS = 4
 LAST_PARTS = 2
-M1_POOL = [False,False,True,False]
+M1_POOL = [True,False,True,False]
 HY_POOL = [False]*4
 HC_ON = ["scalar", "vector", "vector", "vector"]
 FLOPS = 2 * BATCH * GATES * (HID + IN)
@@ -68,12 +68,12 @@ def F(t, *gs):
 
 
 G4 = [("GB",), ("G", 0), ("G", 1), ("G", 2), ("G", 3)]
-DUMMIES = [6,1,1]
+DUMMIES = [2]
 T_LIST = (
-    [("DUM",0), ("VEC",), ("HT",0), ("SP",2), ("DUM",1), ("SP",3), ("XT0",), ("SP",0), ("DUM",2), ("SP",1), ("GB",), ("G",0), ("G",1), ("SP",4), ("G",2), ("SP",5), ("G",3), ("WT",1), ("XM",0), ("SP",6), ("SP",7)] + R(0,0,4) + [("XM",1)] + R(0,4,8) + [("HT", 1), ("XT", 0), ("WT", 0), ("WT", 2), ("WT", 3)]
+    [("DUM",0), ("VEC",), ("HT",0), ("SP",2), ("SP",3), ("XT0",), ("SP",0), ("SP",1), ("GB",), ("G",0), ("G",1), ("SP",4), ("G",2), ("SP",5), ("G",3), ("WT",1), ("XM",0), ("SP",6), ("SP",7)] + R(0,0,4) + [("XM",1)] + R(0,4,8) + [("HT", 1), ("XT", 0), ("WT", 0), ("WT", 2), ("WT", 3)]
     + Q(0,2,3,0) + R(1,0,8) + Q(0,1) + [("HT",2), ("HT",3)] + Q(0,4) + [("XT",1)] + Q(0,5)
-    + R(2,0,3) + Q(1,2) + R(2,3,6) + Q(1,3,0) + R(2,6,8) + R(3,0,1) + Q(1,1,4,5) + Q(0,6,7)
-    + R(3,1,4) + Q(2,2,3,0) + R(3,4,8) + Q(2,1,4,5)
+    + R(2,0,3) + Q(1,2) + R(2,3,6) + Q(1,3) + R(2,6,8) + R(3,0,1) + Q(1,0,1,4,5) + Q(0,6,7)
+    + R(3,1,5) + Q(2,2,3,0) + R(3,5,8) + Q(2,1,4,5)
     + Q(3, *FIG) + Q(1, 6, 7) + Q(2, 6, 7) + Q(3, 6, 7)
 )
 S_LIST = (
@@ -83,14 +83,14 @@ S_LIST = (
     + F(2,1,0,2) + F(3,1,0) + [("SQ",2)] + F(3,2) + F(1,3) + [("TH",1,0), ("SQ",3), ("TH",2,0)] + F(2,3) + F(3,3) + [("TH",3,0), ("TH",3,1)]
 )
 V_LIST = (
-    [("VECC",), ("XC0",), ("HQ",0), ("SPC",4), ("SPC",5), ("NW",), ("AS", 0), ("SPC",6), ("AV", 0), ("SPC",7), ("WC", 1), ("XS", 0), ("AS", 1), ("AV", 1), ("HC", 1), ("HQ", 1), ("XC", 0), ("WC", 0)]
-    + [("G1", 0, 0), ("WC", 2)] + A2(0, 2, 3) + [("WC", 3), ("G1", 0, 1)] + A2(0, 0) + [("HC", 2), ("HC", 3), ("XS", 1)] + A2(0, 1) + [("HQ", 2), ("HQ", 3), ("XC", 1)] + A2(0, 4) + [("G1", 1, 0)] + A2(0, 5) + [("G1", 1, 1)]
-    + A2(1, 2) + [("M1",0), ("M2", 0)] + A2(1, 3) + [("C", 0)] + A2(1, 0) + [("NM", 0), ("G1", 2, 0), ("V1", 0)] + A2(1, 1, 4, 5) + [("G1", 2, 1)] + A2(0, 6, 7) + [("CY", 0)]
-    + [("M1",1), ("M2",1)] + A2(2,2) + [("C",1)] + A2(2,3) + [("NM",1)] + A2(2,0) + [("V1",1), ("G1",3,0)] + A2(2,1) + [("G1",3,1), ("CY",1), ("HY",0,0)] + A2(2,4,5)
-    + A2(3,2,3,0,1) + [("M2",2), ("M1",3), ("C",2)] + A2(3,4) + [("NM",2)] + A2(3,5) + [("V1",2)] + A2(1,6,7) + [("M2",3)] + A2(2,6) + [("C",3)] + A2(2,7) + [("NM",3), ("CY",2), ("V1",3)] + A2(3,6,7)
+    [("VECC",), ("XC0",), ("HQ",0), ("SPC",4), ("SPC",5), ("NW",), ("AS", 0), ("SPC",6), ("AV", 0), ("SPC",7), ("WC", 1), ("XS", 0), ("AS", 1), ("AV", 1), ("HC", 1), ("XC", 0), ("HQ", 1), ("WC", 0)]
+    + [("G1", 0, 0), ("WC", 2)] + A2(0, 2, 3) + [("WC", 3), ("G1", 0, 1)] + A2(0, 0) + [("HC", 2), ("XS", 1), ("HC", 3)] + A2(0, 1) + [("HQ", 2), ("HQ", 3), ("XC", 1)] + A2(0, 4) + [("G1", 1, 0)] + A2(0, 5) + [("G1", 1, 1)]
+    + A2(1, 2) + [("M2", 0)] + A2(1, 3) + [("C", 0)] + A2(1, 0) + [("NM", 0), ("G1", 2, 0), ("V1", 0)] + A2(1, 1, 4, 5) + [("G1", 2, 1)] + A2(0, 6, 7) + [("CY", 0)]
+    + [("M1",1), ("M2",1)] + A2(2,2) + [("C",1)] + A2(2,3) + [("NM",1)] + A2(2,0) + [("V1",1), ("G1",3,0)] + A2(2,1) + [("G1",3,1), ("CY",1)] + A2(2,4,5)
+    + A2(3,2,3,0,1) + [("M2",2), ("M1",3), ("C",2)] + A2(3,4) + [("NM",2)] + A2(3,5) + [("V1",2)] + [("HY",0,0)] + A2(1,6,7) + [("M2",3)] + A2(2,6) + [("C",3)] + A2(2,7) + [("NM",3), ("CY",2), ("V1",3)] + A2(3,6,7)
     + [("HY",1,0), ("CY", 3), ("HY", 2, 0), ("HY", 3, 0), ("HY", 3, 1)]
 )
-G_LIST = [("PW",0),("PW",1),("RS",0),("RS",1),("RS",2),("RC",0),("RC",1),("RS",3),("M1",2),("RC",2),("RC",3)]
+G_LIST = [("PW",0),("PW",1),("RS",0),("M1",0),("RS",1),("RS",2),("RC",0),("RC",1),("RS",3),("M1",2),("RC",2),("RC",3)]
 
 
 def tile_multilstm_pa_kernel(

@@ -71,7 +71,7 @@ G4 = [("GB",), ("G", 0), ("G", 1), ("G", 2), ("G", 3)]
 DUMMIES = [2]
 T_LIST = (
     [("DUM",0), ("VEC",), ("HT",0), ("SP",2), ("SP",3), ("XT0",), ("SP",0), ("SP",1), ("GB",), ("G",0), ("G",1), ("SP",4), ("G",2), ("SP",5), ("G",3), ("WT",1), ("XM",0), ("SP",6), ("SP",7)] + R(0,0,4) + [("XM",1)] + R(0,4,8) + [("HT", 1), ("XT", 0), ("WT", 0), ("WT", 2), ("WT", 3)]
-    + Q(0,2,3,0) + R(1,0,8) + Q(0,1) + [("HT",2), ("HT",3)] + Q(0,4) + [("XT",1)] + Q(0,5)
+    + Q(0,2) + R(1,0,3) + Q(0,3) + R(1,3,8) + Q(0,0,1) + [("HT",2), ("HT",3)] + Q(0,4) + [("XT",1)] + Q(0,5)
     + R(2,0,3) + Q(1,2) + R(2,3,6) + Q(1,3) + R(2,6,8) + R(3,0,1) + Q(1,0,1,4,5) + Q(0,6,7)
     + R(3,1,5) + Q(2,2,3,0) + R(3,5,8) + Q(2,1,4,5)
     + Q(3, *FIG) + Q(1, 6, 7) + Q(2, 6, 7) + Q(3, 6, 7)
@@ -79,7 +79,7 @@ T_LIST = (
 S_LIST = (
     [("SPC",2), ("HC",0), ("SPC",3), ("SPC",0), ("SPC",1)] + P1(0,0,8) + [("MEAN", 0), ("P2", 0)] + P1(1, 0, 5) + F(0, 1) + P1(1, 5, 8) + [("MEAN", 1), ("P2", 1)]
     + P1(2, 0, 3) + F(0, 0) + P1(2, 3, 5) + F(0, 2) + P1(2, 5, 8) + [("MEAN", 2), ("P2", 2), ("SQ", 0)]
-    + F(1, 1) + P1(3, 0, 1) + F(1, 0) + P1(3, 1, 2) + F(1, 2) + P1(3, 2, 4) + F(0, 3) + P1(3, 4, 8) + [("MEAN", 3), ("SQ", 1), ("TH", 0, 0), ("P2", 3)]
+    + F(1, 1) + P1(3, 0, 1) + F(1, 0) + P1(3, 1, 2) + F(1, 2) + P1(3, 2, 4) + F(0, 3) + P1(3,4,5) + [("TH",0,0)] + P1(3,5,8) + [("MEAN",3), ("SQ",1), ("P2",3)]
     + F(2,1,0,2) + F(3,1,0) + [("SQ",2)] + F(3,2) + F(1,3) + [("TH",1,0), ("SQ",3), ("TH",2,0)] + F(2,3) + F(3,3) + [("TH",3,0), ("TH",3,1)]
 )
 V_LIST = (
@@ -87,8 +87,8 @@ V_LIST = (
     + [("G1", 0, 0), ("WC", 2)] + A2(0, 2, 3) + [("WC", 3), ("G1", 0, 1)] + A2(0, 0) + [("HC", 2), ("XS", 1), ("HC", 3)] + A2(0, 1) + [("HQ", 2), ("HQ", 3), ("XC", 1)] + A2(0, 4) + [("G1", 1, 0)] + A2(0, 5) + [("G1", 1, 1)]
     + A2(1, 2) + [("M2", 0)] + A2(1, 3) + [("C", 0)] + A2(1, 0) + [("NM", 0), ("G1", 2, 0), ("V1", 0)] + A2(1, 1, 4, 5) + [("G1", 2, 1)] + A2(0, 6, 7) + [("CY", 0)]
     + [("M1",1), ("M2",1)] + A2(2,2) + [("C",1)] + A2(2,3) + [("NM",1)] + A2(2,0) + [("V1",1), ("G1",3,0)] + A2(2,1) + [("G1",3,1), ("CY",1)] + A2(2,4,5)
-    + A2(3,2,3,0,1) + [("M2",2), ("M1",3), ("C",2)] + A2(3,4) + [("NM",2)] + A2(3,5) + [("V1",2)] + [("HY",0,0)] + A2(1,6,7) + [("M2",3)] + A2(2,6) + [("C",3)] + A2(2,7) + [("NM",3), ("CY",2), ("V1",3)] + A2(3,6,7)
-    + [("HY",1,0), ("CY", 3), ("HY", 2, 0), ("HY", 3, 0), ("HY", 3, 1)]
+    + A2(3,2,3,0,1) + [("M2",2), ("M1",3), ("C",2)] + A2(3,4) + [("NM",2)] + A2(3,5) + [("V1",2)] + [("HY",0,0)] + A2(1,6,7) + [("M2",3)] + A2(2,6) + [("C",3)] + A2(2,7) + [("NM",3), ("HY",1,0), ("CY",2), ("V1",3)] + A2(3,6,7)
+    + [("CY", 3), ("HY", 2, 0), ("HY", 3, 0), ("HY", 3, 1)]
 )
 G_LIST = [("PW",0),("PW",1),("RS",0),("M1",0),("RS",1),("RS",2),("RC",0),("RC",1),("RS",3),("M1",2),("RC",2),("RC",3)]
 

from contextlib import ExitStack

import concourse.mybir as mybir
from concourse.masks import make_identity

F32 = mybir.dt.float32
BF16 = mybir.dt.bfloat16
I32 = mybir.dt.int32
U32 = mybir.dt.uint32
U8 = mybir.dt.uint8
FP8X4 = mybir.dt.float8_e4m3fn_x4
FP4X4 = mybir.dt.float4_e2m1fn_x4
ALU = mybir.AluOpType
ACT = mybir.ActivationFunctionType

P = 128
BATCH = 512
IN = 128
HID = 1024
GATES = 4 * HID
EPS = 1e-5
TILES = BATCH // P
BANK = 512
BANKS = GATES // BANK
BLOCKS = GATES // P
PER_BANK = BANK // P
K_PASS = 512
PASSES = HID // K_PASS
ONES = 2
R_SLOTS = 3
Q_SLOTS = 5
ORDER = [2, 3, 0, 1, 4, 5, 6, 7]
FIG = ORDER[0:6]
GROUPS = [[0], [1, 2, 3]]
WPARTS = 4
LAST_PARTS = 2
M1_POOL = [True,False,True,False]
HY_POOL = [False]*4
HC_ON = ["scalar", "vector", "vector", "vector"]
FLOPS = 2 * BATCH * GATES * (HID + IN)

SPC_ON = ["scalar"] * 4 + ["vector"] * 4
LOADS = [("vecs",), ("h", 0), ("x",), ("w", 0), ("w", 1), ("w", 2), ("w", 3), ("scales",), ("words", 0), ("words", 1), ("words", 2), ("words", 3), ("h", 1), ("gain_r", 0), ("gain_r", 1), ("h23",), ("c",), ("gain_c",), ("bias_c",)]


def R(t, a, b):
    return [("R", t, j) for j in range(a, b)]


def P1(t, a, b):
    return [("P1", t, j) for j in range(a, b)]


def Q(t, *js):
    return [("Q", t, j) for j in js]


def SP(a, b):
    return [("SP", i) for i in range(a, b)]


def A2(t, *js):
    return [("A2", t, j) for j in js]


def F(t, *gs):
    return [("F", t, g) for g in gs]


G4 = [("GB",), ("G", 0), ("G", 1), ("G", 2), ("G", 3)]
DUMMIES = [2]
T_LIST = (
    [("DUM",0), ("VEC",), ("HT",0), ("SP",2), ("SP",3), ("XT0",), ("SP",0), ("SP",1), ("GB",), ("G",0), ("G",1), ("SP",4), ("G",2), ("SP",5), ("G",3), ("WT",1), ("XM",0), ("SP",6), ("SP",7)] + R(0,0,4) + [("XM",1)] + R(0,4,8) + [("HT", 1), ("XT", 0), ("WT", 0), ("WT", 2), ("WT", 3)]
    + Q(0,2) + R(1,0,3) + Q(0,3) + R(1,3,8) + Q(0,0,1) + [("HT",2), ("HT",3)] + Q(0,4) + [("XT",1)] + Q(0,5)
    + R(2,0,3) + Q(1,2) + R(2,3,6) + Q(1,3) + R(2,6,8) + R(3,0,1) + Q(1,0,1,4,5) + Q(0,6,7)
    + R(3,1,5) + Q(2,2,3,0) + R(3,5,8) + Q(2,1,4,5)
    + Q(3, *FIG) + Q(1, 6, 7) + Q(2, 6, 7) + Q(3, 6, 7)
)
S_LIST = (
    [("SPC",2), ("HC",0), ("SPC",3), ("SPC",0), ("SPC",1)] + P1(0,0,8) + [("MEAN", 0), ("P2", 0)] + P1(1, 0, 5) + F(0, 1) + P1(1, 5, 8) + [("MEAN", 1), ("P2", 1)]
    + P1(2, 0, 3) + F(0, 0) + P1(2, 3, 5) + F(0, 2) + P1(2, 5, 8) + [("MEAN", 2), ("P2", 2), ("SQ", 0)]
    + F(1, 1) + P1(3, 0, 1) + F(1, 0) + P1(3, 1, 2) + F(1, 2) + P1(3, 2, 4) + F(0, 3) + P1(3,4,5) + [("TH",0,0)] + P1(3,5,8) + [("MEAN",3), ("SQ",1), ("P2",3)]
    + F(2,1,0,2) + F(3,1,0) + [("SQ",2)] + F(3,2) + F(1,3) + [("TH",1,0), ("SQ",3), ("TH",2,0)] + F(2,3) + F(3,3) + [("TH",3,0), ("TH",3,1)]
)
V_LIST = (
    [("VECC",), ("XC0",), ("HQ",0), ("SPC",4), ("SPC",5), ("NW",), ("AS", 0), ("SPC",6), ("AV", 0), ("SPC",7), ("WC", 1), ("XS", 0), ("AS", 1), ("AV", 1), ("HC", 1), ("XC", 0), ("HQ", 1), ("WC", 0)]
    + [("G1", 0, 0), ("WC", 2)] + A2(0, 2, 3) + [("WC", 3), ("G1", 0, 1)] + A2(0, 0) + [("HC", 2), ("XS", 1), ("HC", 3)] + A2(0, 1) + [("HQ", 2), ("HQ", 3), ("XC", 1)] + A2(0, 4) + [("G1", 1, 0)] + A2(0, 5) + [("G1", 1, 1)]
    + A2(1, 2) + [("M2", 0)] + A2(1, 3) + [("C", 0)] + A2(1, 0) + [("NM", 0), ("G1", 2, 0), ("V1", 0)] + A2(1, 1, 4, 5) + [("G1", 2, 1)] + A2(0, 6, 7) + [("CY", 0)]
    + [("M1",1), ("M2",1)] + A2(2,2) + [("C",1)] + A2(2,3) + [("NM",1)] + A2(2,0) + [("V1",1), ("G1",3,0)] + A2(2,1) + [("G1",3,1), ("CY",1)] + A2(2,4,5)
    + A2(3,2,3,0,1) + [("M2",2), ("M1",3), ("C",2)] + A2(3,4) + [("NM",2)] + A2(3,5) + [("V1",2)] + [("HY",0,0)] + A2(1,6,7) + [("M2",3)] + A2(2,6) + [("C",3)] + A2(2,7) + [("NM",3), ("HY",1,0), ("CY",2), ("V1",3)] + A2(3,6,7)
    + [("CY", 3), ("HY", 2, 0), ("HY", 3, 0), ("HY", 3, 1)]
)
G_LIST = [("PW",0),("PW",1),("RS",0),("M1",0),("RS",1),("RS",2),("RC",0),("RC",1),("RS",3),("M1",2),("RC",2),("RC",3)]


def tile_multilstm_pa_kernel(
    tc,
    x,
    h0,
    c0,
    w_ih1,
    w_hh1_words,
    w_hh1_scales,
    lni_w1,
    lni_b1,
    lnh_w1,
    lnh_b1,
    lnc_w1,
    lnc_b1,
    out_0,
    out_1,
):
    nc = tc.nc
    with ExitStack() as stack:
        stack.enter_context(tc.manual_schedule())
        keep = stack.enter_context(tc.tile_pool(name="keep", bufs=1))
        stage = stack.enter_context(tc.tile_pool(name="stage", bufs=2))
        r_pool = stack.enter_context(tc.tile_pool(name="r_pool", bufs=2))
        gate_pool = stack.enter_context(tc.tile_pool(name="gate_pool", bufs=TILES))
        stats = stack.enter_context(tc.tile_pool(name="stats", bufs=2 * TILES))
        psum = stack.enter_context(tc.psum_pool(name="psum", bufs=1))

        def r_bank(shape, dtype):
            r_slot = psum.tile(shape, dtype, tag="r", bufs=R_SLOTS)
            return r_slot

        def q_bank(shape, dtype):
            q_slot = psum.tile(shape, dtype, tag="q", bufs=Q_SLOTS)
            return q_slot

        zeros = keep.tile([P, P], F32)
        nc.vector.memset(zeros[:], 0.0)
        w_scales = keep.tile([P, PASSES, GATES], U8, align_bytes=64)
        nc.vector.memset(w_scales[:].rearrange("p g n -> p (g n)").bitcast(I32), 0)
        ident_f32 = keep.tile([P, P], F32)
        make_identity(nc, ident_f32[:])
        ident_bf = keep.tile([P, P], BF16)
        make_identity(nc, ident_bf[:])
        neg_half = keep.tile([P, TILES], F32)
        nc.gpsimd.memset(neg_half[:], -0.5)
        gate_vecs = keep.tile([P, P], BF16)
        nc.vector.memset(gate_vecs[3 * BLOCKS : P, :], 0.0)
        warm = keep.tile([P, 1], F32)
        nc.vector.memset(warm[:], 0.0)
        nc.scalar.activation(out=warm[:], in_=warm[:], func=ACT.Sigmoid)
        ones = keep.tile([P, ONES], BF16)
        nc.vector.memset(ones[:], 1.0)

        x_rows = keep.tile([P, TILES, IN], BF16)
        w_rows = keep.tile([P, BANKS, PER_BANK, IN], BF16)
        w_banks = w_ih1.rearrange("(b p t) v -> p b t v", p=P, t=PER_BANK)
        gain_a = keep.tile([P, GATES], BF16)
        h_rows = keep.tile([P, TILES, HID], BF16)
        h_tiles = h0.rearrange("(p t) k -> p t k", t=TILES)
        w_words = keep.tile([P, PASSES, 2 * GATES], U8, align_bytes=64)
        gain_r = keep.tile([P, GATES], BF16)
        c_rows = keep.tile([P, TILES, HID], BF16)
        gain_c = keep.tile([P, HID], BF16)
        bias_c = keep.tile([P, HID], BF16)
        hy_tiles = out_0.rearrange("(p t) k -> p t k", t=TILES)
        cy_tiles = out_1.rearrange("(p t) k -> p t k", t=TILES)

        def load(what, i=0):
            dma = nc.sync.dma_start
            if what == "vecs":
                for n, vec in enumerate((lni_w1, lni_b1, lnh_b1)):
                    dma(out=gate_vecs[BLOCKS * n : BLOCKS * (n + 1), :], in_=vec.rearrange("(j p) -> j p", p=P))
            elif what == "x":
                dma(out=x_rows[:], in_=x.rearrange("(p t) v -> p t v", t=TILES))
            elif what == "w":
                dma(out=w_rows[:, 2 * i : 2 * i + 2, :, :], in_=w_banks[:, 2 * i : 2 * i + 2, :, :])
            elif what == "h":
                dma(out=h_rows[:, i : i + 1, :], in_=h_tiles[:, i : i + 1, :])
            elif what == "h23":
                dma(out=h_rows[:, 2:4, :], in_=h_tiles[:, 2:4, :])
            elif what == "scales":
                for r in range(4):
                    dma(
                        out=w_scales[r:P:32, :, :].bitcast(I32),
                        in_=w_hh1_scales[:, r:16:4, :].rearrange("g q n -> q g n").bitcast(I32),
                    )
            elif what == "words":
                n = 2 * GATES // WPARTS
                some = slice(i * n, (i + 1) * n)
                for g in range(PASSES):
                    dma(out=w_words[:, g, some].bitcast(I32), in_=w_hh1_words[g, :, some].bitcast(I32))
            elif what == "gain_r":
                cols = slice(i * GATES // 2, (i + 1) * GATES // 2)
                dma(out=gain_r[:, cols], in_=lnh_w1[cols].partition_broadcast(P))
            elif what == "c":
                dma(out=c_rows[:], in_=c0.rearrange("(p t) k -> p t k", t=TILES))
            elif what == "gain_c":
                dma(out=gain_c[:], in_=lnc_w1.partition_broadcast(P))
            elif what == "bias_c":
                dma(out=bias_c[:], in_=lnc_b1.partition_broadcast(P))

        for name in LOADS:
            load(*name)

        S = {}
        ops = {}
        bank_tag = {}
        bank_users = {}

        def step(name, deps, what, bank=None, users=()):
            ops[name] = (what, deps)
            if bank is not None:
                bank_tag[name] = bank
                bank_users[name] = list(users)

        def do_DUM(count):
            dummy_ps = r_bank([P, P], F32)
            for n in range(count):
                nc.tensor.matmul(dummy_ps[:], lhsT=zeros[:], rhs=zeros[:], start=True, stop=True)

        for i, count in enumerate(DUMMIES):
            step(("DUM", i), [], lambda count=count: do_DUM(count), "r", [])

        vec_cols = keep.tile([P, P], BF16)
        bias_cols = keep.tile([P, BLOCKS], F32)
        xT_f32 = keep.tile([P, BATCH], F32)

        def do_VEC():
            vec_ps = r_bank([P, P], BF16)
            nc.tensor.transpose(vec_ps[:], gate_vecs[:], ident_bf[:])
            S["vec"] = vec_ps

        def do_VECC():
            nc.vector.tensor_copy(out=vec_cols[:], in_=S["vec"][:])
            nc.vector.tensor_tensor(
                out=bias_cols[:],
                in0=vec_cols[:, BLOCKS : 2 * BLOCKS],
                in1=vec_cols[:, 2 * BLOCKS : 3 * BLOCKS],
                op=ALU.add,
            )

        def do_XT0():
            xT_ps = r_bank([P, BATCH], BF16)
            for t in range(TILES):
                nc.tensor.transpose(xT_ps[:, t * P : (t + 1) * P], x_rows[:, t, :], ident_bf[:])
            S["xT"] = xT_ps

        def do_XC0():
            nc.vector.tensor_copy(out=xT_f32[:], in_=S["xT"][:])

        def do_SP(b):
            spread_ps = q_bank([P, BANK], BF16)
            for k in range(PER_BANK):
                block = b * PER_BANK + k
                nc.tensor.transpose(
                    spread_ps[:, k * P : (k + 1) * P], vec_cols[:, block : block + 1].to_broadcast([P, P]), ident_bf[:]
                )
            S["spread", b] = spread_ps

        def do_SPC(b):
            out = gain_a[:, b * BANK : (b + 1) * BANK]
            if SPC_ON[b] == "scalar":
                nc.scalar.copy(out=out, in_=S["spread", b][:])
            else:
                nc.vector.tensor_copy(out=out, in_=S["spread", b][:])

        for b in range(BANKS):
            step(("SP", b), [("VECC",)], lambda b=b: do_SP(b), "q", [("SPC", b)])
            step(("SPC", b), [("SP", b)], lambda b=b: do_SPC(b))
        step(("VEC",), [], do_VEC, "r", [("VECC",)])
        step(("VECC",), [("VEC",)], do_VECC)
        step(("XT0",), [], do_XT0, "r", [("XC0",)])
        step(("XC0",), [("XT0",)], do_XC0)

        h_codes = keep.tile([P, TILES, PASSES * P], U32, align_bytes=64)
        h_scales = keep.tile([P, TILES, PASSES * P], U8, align_bytes=64)
        pass_words = K_PASS // 2

        def do_HT(t):
            h_words = h_rows[:, t, :].bitcast(F32)
            hT_ps = r_bank([P, PASSES, 2, P], F32)
            for g in range(PASSES):
                for u in range(2):
                    nc.tensor.transpose(
                        hT_ps[:, g, u, :],
                        h_words[:, pass_words * g + u : pass_words * (g + 1) : 2],
                        ident_f32[:],
                    )
            S["hT", t] = hT_ps

        def do_HC(t):
            grouped = stage.tile([P, PASSES * P * 4], BF16, align_bytes=64)
            out = grouped[:].bitcast(F32).rearrange("p (g b u) -> p g b u", g=PASSES, u=2)
            hT = S["hT", t][:].rearrange("p g u b -> p g b u")
            if HC_ON[t] == "scalar":
                nc.scalar.copy(out=out, in_=hT)
            else:
                nc.vector.tensor_copy(out=out, in_=hT)
            S["grouped", t] = grouped

        def do_HQ(t):
            nc.vector.quantize_mx(
                out=h_codes[:, t, :].bitcast(FP8X4), scales=h_scales[:, t, :], in_=S["grouped", t][:]
            )

        for t in range(TILES):
            step(("HT", t), [], lambda t=t: do_HT(t), "r", [("HC", t)])
            step(("HC", t), [("HT", t)], lambda t=t: do_HC(t))
            step(("HQ", t), [("HC", t)], lambda t=t: do_HQ(t))

        neg_wmean = keep.tile([P, 1], F32)
        gram = keep.tile([P, IN + ONES], F32)

        def do_GB():
            gram_ps = q_bank([P, IN], F32)
            S["gram"] = gram_ps

        def do_G(q):
            if q == 0:
                wsum_ps = q_bank([P, ONES], F32)
                S["wsum"] = wsum_ps
            for b in range(2 * q, 2 * q + 2):
                for k in range(PER_BANK):
                    block = w_rows[:, b, k, :]
                    first = b == 0 and k == 0
                    last = b == BANKS - 1 and k == PER_BANK - 1
                    nc.tensor.matmul(S["gram"][:], lhsT=block, rhs=block, start=first, stop=last)
                    nc.tensor.matmul(S["wsum"][:], lhsT=block, rhs=ones[:], start=first, stop=last)

        def do_NW():
            nc.vector.tensor_scalar(
                out=neg_wmean[:], in0=S["wsum"][:, 0:1], scalar1=-1.0 / GATES, scalar2=None, op0=ALU.mult
            )
            nc.vector.tensor_copy(out=gram[:, 0:IN], in_=S["gram"][:])
            nc.vector.tensor_copy(out=gram[:, IN : IN + ONES], in_=S["wsum"][:])

        step(("GB",), [], do_GB, "q", [("NW",)])
        for q in range(4):
            step(("G", q), [("G", q - 1)] if q else [("GB",)], lambda q=q: do_G(q))
        bank_tag["G", 0] = "q"
        bank_users["G", 0] = [("NW",)]
        step(("NW",), [("G", 3)], do_NW)

        wcT = keep.tile([P, GATES], F32)

        def do_WT(q):
            wT_ps = q_bank([P, 2 * BANK], BF16)
            for k in range(2 * PER_BANK):
                nc.tensor.transpose(
                    wT_ps[:, k * P : (k + 1) * P], w_rows[:, 2 * q + k // PER_BANK, k % PER_BANK, :], ident_bf[:]
                )
            S["wT", q] = wT_ps

        def do_WC(q):
            for b in range(2):
                cols = slice((2 * q + b) * BANK, (2 * q + b + 1) * BANK)
                nc.vector.scalar_tensor_tensor(
                    out=wcT[:, cols].rearrange("v (p t) -> v p t", t=PER_BANK),
                    in0=S["wT", q][:, b * BANK : (b + 1) * BANK].rearrange("v (t p) -> v p t", t=PER_BANK),
                    scalar=neg_wmean[:],
                    in1=gain_a[:, cols].rearrange("v (p t) -> v p t", t=PER_BANK),
                    op0=ALU.add,
                    op1=ALU.mult,
                )

        for q in range(4):
            step(("WT", q), [], lambda q=q: do_WT(q), "q", [("WC", q)])
            step(("WC", q), [("WT", q), ("NW",), ("SPC", 2 * q), ("SPC", 2 * q + 1)], lambda q=q: do_WC(q))

        a_negmean = keep.tile([P, TILES], F32)
        a_sumsq = keep.tile([P, TILES], F32)
        a_meansq = keep.tile([P, TILES], F32)
        a_var = keep.tile([P, TILES], F32)
        a_rstd = keep.tile([P, TILES], F32)
        x_scaled = keep.tile([P, TILES, IN], F32)
        xsT = keep.tile([P, BATCH], F32)

        def do_XM(i):
            xm_ps = r_bank([P, len(GROUPS[i]), IN + ONES], F32)
            for n, t in enumerate(GROUPS[i]):
                nc.tensor.matmul(
                    xm_ps[:, n, :], lhsT=xT_f32[:, t * P : (t + 1) * P], rhs=gram[:], start=True, stop=True
                )
            S["xm", i] = xm_ps

        def some(i):
            return slice(GROUPS[i][0], GROUPS[i][-1] + 1)

        def do_AS(i):
            for n, t in enumerate(GROUPS[i]):
                products = stage.tile([P, IN], F32)
                nc.vector.scalar_tensor_tensor(
                    out=products[:],
                    in0=S["xm", i][:, n, 0:IN],
                    scalar=1.0,
                    in1=x_rows[:, t, :],
                    op0=ALU.mult,
                    op1=ALU.mult,
                    accum_out=a_sumsq[:, t : t + 1],
                )
            nc.vector.tensor_scalar(
                out=a_negmean[:, some(i)], in0=S["xm", i][:, :, IN], scalar1=-1.0 / GATES, scalar2=None, op0=ALU.mult
            )

        def do_AV(i):
            nc.vector.tensor_tensor(
                out=a_meansq[:, some(i)], in0=a_negmean[:, some(i)], in1=a_negmean[:, some(i)], op=ALU.mult
            )
            nc.vector.scalar_tensor_tensor(
                out=a_var[:, some(i)],
                in0=a_sumsq[:, some(i)],
                scalar=1.0 / GATES,
                in1=a_meansq[:, some(i)],
                op0=ALU.mult,
                op1=ALU.subtract,
            )
            nc.vector.tensor_scalar(
                out=a_var[:, some(i)], in0=a_var[:, some(i)], scalar1=EPS, scalar2=None, op0=ALU.add
            )

        def do_PW(i):
            nc.gpsimd.tensor_tensor(
                out=a_rstd[:, some(i)], in0=a_var[:, some(i)], in1=neg_half[:, some(i)], op=ALU.pow
            )

        def do_XS(i):
            for t in GROUPS[i]:
                nc.vector.tensor_scalar(
                    out=x_scaled[:, t, :], in0=x_rows[:, t, :], scalar1=a_rstd[:, t : t + 1], scalar2=None, op0=ALU.mult
                )

        def do_XT(i):
            xsT_ps = r_bank([P, len(GROUPS[i]), P], F32)
            for n, t in enumerate(GROUPS[i]):
                nc.tensor.transpose(xsT_ps[:, n, :], x_scaled[:, t, :], ident_f32[:])
            S["xsT", i] = xsT_ps

        def do_XC(i):
            out = xsT[:, GROUPS[i][0] * P : (GROUPS[i][-1] + 1) * P]
            nc.vector.tensor_copy(out=out, in_=S["xsT", i][:].rearrange("p t b -> p (t b)"))

        for i in range(2):
            step(("XM", i), [("NW",), ("XC0",)], lambda i=i: do_XM(i), "r", [("AS", i)])
            step(("AS", i), [("XM", i)], lambda i=i: do_AS(i))
            step(("AV", i), [("AS", i)], lambda i=i: do_AV(i))
            step(("PW", i), [("AV", i)], lambda i=i: do_PW(i))
            step(("XS", i), [("PW", i)], lambda i=i: do_XS(i))
            step(("XT", i), [("XS", i)], lambda i=i: do_XT(i), "r", [("XC", i)])
            step(("XC", i), [("XT", i)], lambda i=i: do_XC(i))

        def do_R(t, j):
            r_ps = r_bank([P, BANK], F32)
            for g in range(PASSES):
                nc.tensor.matmul_mx(
                    out=r_ps[:],
                    lhsT=h_codes[:, t, g * P : (g + 1) * P].bitcast(FP8X4),
                    lhsT_scale=h_scales[:, t, g * P : (g + 1) * P],
                    rhs=w_words[:, g, 2 * j * BANK : 2 * (j + 1) * BANK].bitcast(FP4X4),
                    rhs_scale=w_scales[:, g, j * BANK : (j + 1) * BANK],
                    start=(g == 0),
                    stop=(g == PASSES - 1),
                )
            S["r", t, j] = r_ps

        def do_P1(t, j):
            if j == 0:
                r_copy = r_pool.tile([P, GATES], F32)
                r_sums = stats.tile([P, BANKS], F32)
                S["copy", t] = r_copy
                S["sums", t] = r_sums
            nc.scalar.activation(
                out=S["copy", t][:, j * BANK : (j + 1) * BANK],
                in_=S["r", t, j][:],
                func=ACT.Identity,
                accum_out=S["sums", t][:, j : j + 1],
            )

        def do_MEAN(t):
            r_scaled = stats.tile([P, BANKS], F32)
            r_negmean = stats.tile([P, 1], F32)
            nc.scalar.activation(
                out=r_scaled[:], in_=S["sums", t][:], func=ACT.Identity, scale=-1.0 / GATES, accum_out=r_negmean[:]
            )
            S["negmean", t] = r_negmean

        def do_P2(t):
            r_squares = r_pool.tile([P, GATES], BF16, bufs=1)
            r_sumsq = stats.tile([P, 1], F32)
            nc.scalar.activation(
                out=r_squares[:], in_=S["copy", t][:], func=ACT.Square, bias=S["negmean", t][:], accum_out=r_sumsq[:]
            )
            S["sumsq", t] = r_sumsq

        def rstd_of(sum_of_squares, count):
            var = stats.tile([P, 1], F32)
            nc.gpsimd.tensor_scalar(
                out=var[:], in0=sum_of_squares, scalar1=1.0 / count, scalar2=EPS, op0=ALU.mult, op1=ALU.add
            )
            rstd = stats.tile([P, 1], F32)
            nc.gpsimd.tensor_tensor(out=rstd[:], in0=var[:], in1=neg_half[:, 0:1], op=ALU.pow)
            return rstd

        def do_RS(t):
            S["rstd", t] = rstd_of(S["sumsq", t][:], GATES)

        def do_G1(t, half):
            if half == 0:
                gates = gate_pool.tile([P, GATES], F32)
                S["gates", t] = gates
            cols = slice(half * GATES // 2, (half + 1) * GATES // 2)
            nc.vector.scalar_tensor_tensor(
                out=S["gates", t][:, cols],
                in0=S["copy", t][:, cols],
                scalar=S["negmean", t][:],
                in1=gain_r[:, cols],
                op0=ALU.add,
                op1=ALU.mult,
            )

        def do_Q(t, j):
            a_ps = q_bank([P, BANK], F32)
            nc.tensor.matmul(
                a_ps[:],
                lhsT=xsT[:, t * P : (t + 1) * P],
                rhs=wcT[:, j * BANK : (j + 1) * BANK],
                start=True,
                stop=False,
            )
            for k in range(PER_BANK):
                block = j * PER_BANK + k
                nc.tensor.matmul(
                    a_ps[:, k * P : (k + 1) * P],
                    lhsT=bias_cols[:, block : block + 1].to_broadcast([P, P]),
                    rhs=ident_f32[:],
                    is_transpose=True,
                    start=False,
                    stop=(k == PER_BANK - 1),
                )
            S["a", t, j] = a_ps

        def do_A2(t, j):
            cols = slice(j * BANK, (j + 1) * BANK)
            nc.vector.scalar_tensor_tensor(
                out=S["gates", t][:, cols],
                in0=S["gates", t][:, cols],
                scalar=S["rstd", t][:],
                in1=S["a", t, j][:],
                op0=ALU.mult,
                op1=ALU.add,
            )

        def gate(t, g):
            return S["gates", t][:, g * HID : (g + 1) * HID]

        def do_F(t, g):
            nc.scalar.activation(out=gate(t, g), in_=gate(t, g), func=ACT.Tanh if g == 2 else ACT.Sigmoid)

        def do_M1(t):
            engine = nc.gpsimd if M1_POOL[t] else nc.vector
            engine.tensor_tensor(out=gate(t, 1), in0=gate(t, 1), in1=c_rows[:, t, :], op=ALU.mult)

        def do_M2(t):
            nc.vector.tensor_tensor(out=gate(t, 0), in0=gate(t, 0), in1=gate(t, 2), op=ALU.mult)

        def do_C(t):
            c_sum = stats.tile([P, 1], F32)
            nc.vector.scalar_tensor_tensor(
                out=gate(t, 0),
                in0=gate(t, 1),
                scalar=1.0,
                in1=gate(t, 0),
                op0=ALU.mult,
                op1=ALU.add,
                accum_out=c_sum[:],
            )
            S["c_sum", t] = c_sum

        def do_NM(t):
            c_negmean = stats.tile([P, 1], F32)
            nc.vector.tensor_scalar(
                out=c_negmean[:], in0=S["c_sum", t][:], scalar1=-1.0 / HID, scalar2=None, op0=ALU.mult
            )
            S["c_negmean", t] = c_negmean

        def do_SQ(t):
            squares = stage.tile([P, HID], BF16)
            c_sumsq = stats.tile([P, 1], F32)
            nc.scalar.activation(
                out=squares[:], in_=gate(t, 0), func=ACT.Square, bias=S["c_negmean", t][:], accum_out=c_sumsq[:]
            )
            S["c_sumsq", t] = c_sumsq

        def do_RC(t):
            S["c_rstd", t] = rstd_of(S["c_sumsq", t][:], HID)

        def do_V1(t):
            nc.vector.scalar_tensor_tensor(
                out=gate(t, 2), in0=gate(t, 0), scalar=S["c_negmean", t][:], in1=gain_c[:], op0=ALU.add, op1=ALU.mult
            )

        def do_CY(t):
            nc.vector.scalar_tensor_tensor(
                out=gate(t, 2), in0=gate(t, 2), scalar=S["c_rstd", t][:], in1=bias_c[:], op0=ALU.mult, op1=ALU.add
            )
            nc.sync.dma_start(out=cy_tiles[:, t, :], in_=gate(t, 2))

        def part_cols(g, part, parts):
            return slice(g * HID + part * HID // parts, g * HID + (part + 1) * HID // parts)

        def do_TH(t, part, parts):
            gates = S["gates", t]
            nc.scalar.activation(
                out=gates[:, part_cols(1, part, parts)], in_=gates[:, part_cols(2, part, parts)], func=ACT.Tanh
            )

        def do_HY(t, part, parts):
            gates = S["gates", t]
            engine = nc.gpsimd if HY_POOL[t] else nc.vector
            tanh_cy = gates[:, part_cols(1, part, parts)]
            engine.tensor_tensor(out=tanh_cy, in0=tanh_cy, in1=gates[:, part_cols(3, part, parts)], op=ALU.mult)
            nc.sync.dma_start(out=hy_tiles[:, t, part_cols(0, part, parts)], in_=tanh_cy)

        for t in range(TILES):
            for j in range(BANKS):
                step(("R", t, j), [("HQ", t)], lambda t=t, j=j: do_R(t, j), "r", [("P1", t, j)])
                step(("P1", t, j), [("R", t, j)] + ([("P1", t, 0)] if j else []), lambda t=t, j=j: do_P1(t, j))
                step(
                    ("Q", t, j),
                    [("XC", 0 if t in GROUPS[0] else 1), ("WC", j // 2), ("VECC",)],
                    lambda t=t, j=j: do_Q(t, j),
                    "q",
                    [("A2", t, j)],
                )
                step(("A2", t, j), [("Q", t, j), ("G1", t, j // 4), ("RS", t)], lambda t=t, j=j: do_A2(t, j))
            step(("MEAN", t), [("P1", t, j) for j in range(BANKS)], lambda t=t: do_MEAN(t))
            step(("P2", t), [("MEAN", t)], lambda t=t: do_P2(t))
            step(("RS", t), [("P2", t)], lambda t=t: do_RS(t))
            for half in range(2):
                step(("G1", t, half), [("MEAN", t)] + ([("G1", t, 0)] if half else []), lambda t=t, half=half: do_G1(t, half))
            for g in range(4):
                step(("F", t, g), [("A2", t, 2 * g), ("A2", t, 2 * g + 1)], lambda t=t, g=g: do_F(t, g))
            step(("M1", t), [("F", t, 1)], lambda t=t: do_M1(t))
            step(("M2", t), [("F", t, 0), ("F", t, 2)], lambda t=t: do_M2(t))
            step(("C", t), [("M1", t), ("M2", t)], lambda t=t: do_C(t))
            step(("NM", t), [("C", t)], lambda t=t: do_NM(t))
            step(("SQ", t), [("NM", t)], lambda t=t: do_SQ(t))
            step(("RC", t), [("SQ", t)], lambda t=t: do_RC(t))
            step(("V1", t), [("NM", t)], lambda t=t: do_V1(t))
            step(("CY", t), [("V1", t), ("RC", t)], lambda t=t: do_CY(t))
            parts = LAST_PARTS if t == TILES - 1 else 1
            for part in range(parts):
                step(("TH", t, part), [("CY", t)], lambda t=t, part=part, parts=parts: do_TH(t, part, parts))
                step(("HY", t, part), [("TH", t, part), ("F", t, 3)], lambda t=t, part=part, parts=parts: do_HY(t, part, parts))

        queues = [T_LIST, S_LIST, V_LIST, G_LIST]
        slots = {"r": R_SLOTS, "q": Q_SLOTS}
        banks_taken = {"r": [], "q": []}
        done = set()
        place = [0, 0, 0, 0]
        moved = True
        while moved:
            moved = False
            for e in range(4):
                while place[e] < len(queues[e]):
                    name = queues[e][place[e]]
                    what, deps = ops[name]
                    if not all(d in done for d in deps):
                        break
                    tag = bank_tag.get(name)
                    if tag is not None:
                        taken = banks_taken[tag]
                        if len(taken) >= slots[tag]:
                            old = taken[len(taken) - slots[tag]]
                            if not all(u in done for u in bank_users[old]):
                                break
                        taken.append(name)
                    what()
                    done.add(name)
                    place[e] += 1
                    moved = True
        assert all(place[e] == len(queues[e]) for e in range(4))
